import numpy as np
import ml_dtypes


def mxq(x, axis, fmt="e4m3"):
    dtype, down = {"e4m3": (ml_dtypes.float8_e4m3fn, 7), "e5m2": (ml_dtypes.float8_e5m2, 14)}[fmt]
    v = np.moveaxis(np.asarray(x, np.float32).astype(ml_dtypes.bfloat16).astype(np.float64), axis, -1)
    blocks = v.reshape(v.shape[:-1] + (-1, 32))
    amax = np.abs(blocks).max(-1, keepdims=True)
    byte = np.maximum(np.where(amax > 0, np.frexp(amax)[1] - 1 + 127, 0) - down, 1)
    scale = np.exp2(byte - 127.0)
    codes = (blocks / scale).astype(np.float32).astype(dtype).astype(np.float64)
    return np.moveaxis((codes * scale).reshape(v.shape), -1, axis)


WIDE = False


def mx_kscale(k):
    if not WIDE:
        return np.ones(k)
    levels = np.array([10, -10, 5, -5, 0])
    if k % 512:
        return np.exp2(np.random.permutation(np.resize(levels, k // 32))).repeat(32)
    a = np.empty((k // 512, 16))
    for p in range(k // 512):
        a[p, :8] = np.random.permutation(np.resize(levels, 8))
        for g in range(8):
            far = levels[np.abs(levels - a[p, g]) >= 10]
            a[p, g + 8] = far[np.random.randint(len(far))]
    return np.exp2(a.ravel()).repeat(32)


BF16 = ml_dtypes.bfloat16


def bf(x):
    return np.asarray(x, np.float32).astype(BF16)


def f64(x):
    return np.asarray(x).astype(np.float64)


B, S, D, R = 2, 1024, 1024, 8
EPS = 1e-6


def draw0():
    s, t = mx_kscale(D), mx_kscale(D)
    return {"x": bf(np.random.standard_normal((B, S, D)) * s),
            "pos_emb": bf(np.random.standard_normal((1, S, D)) * s),
            "enc_w0": bf(np.random.standard_normal((D, D)) / np.sqrt(D) / s[None, :] * t[:, None]),
            "enc_w1": bf(np.random.standard_normal((D, D)) / np.sqrt(D) / t[None, :])}


def core(x, pos_emb, enc_w0, enc_w1):
    x = f64(x)
    y = x + f64(pos_emb)[:, : x.shape[1]]
    h = np.maximum(mxq(y, 2, "e4m3") @ mxq(f64(enc_w0), 1, "e4m3").T, 0.0)
    h = np.maximum(mxq(h, 2, "e4m3") @ mxq(f64(enc_w1), 1, "e4m3").T, 0.0)
    return h / (np.sqrt((h * h).sum(-1, keepdims=True)) + EPS)


def e4m3fn_bytes(y):
    return np.clip(np.asarray(y, np.float64), -448.0, 448.0).astype(np.float32).astype(ml_dtypes.float8_e4m3fn).view(np.uint8)


def e4m3fn_values(b):
    return np.asarray(b, np.uint8).view(ml_dtypes.float8_e4m3fn).astype(np.float64)


def setup_inputs():
    d = draw0()
    x0 = np.asarray(d['enc_w1']).astype(np.float64)
    s = (np.max(np.abs(x0), axis=(0,), keepdims=True) / 448.0).astype(np.float32)
    out = {}
    for k, v in d.items():
        if k == 'enc_w1':
            out['enc_w1_bytes'] = e4m3fn_bytes(x0 / s.astype(np.float64))
            out['enc_w1_scale'] = s
        else:
            out[k] = v
    return out


def reference(x, pos_emb, enc_w0, enc_w1_bytes, enc_w1_scale):
    return core(x, pos_emb, enc_w0, e4m3fn_values(enc_w1_bytes) * enc_w1_scale.astype(np.float64))

@@ -1,0 +1,397 @@
+from contextlib import ExitStack
+
+import concourse.mybir as mybir
+from concourse.masks import make_identity
+
+B, S, D = 2, 1024, 1024
+EPS = 1e-6
+FLOPS = 2 * (2 * B * S * D * D)
+
+F32 = mybir.dt.float32
+BF16 = mybir.dt.bfloat16
+U32 = mybir.dt.uint32
+U8 = mybir.dt.uint8
+FP8 = mybir.dt.float8_e4m3fn
+FP8X4 = mybir.dt.float8_e4m3fn_x4
+ADD = mybir.AluOpType.add
+MULT = mybir.AluOpType.mult
+MAX = mybir.AluOpType.max
+ACT = mybir.ActivationFunctionType
+
+P = 128
+PASSES = 2
+TILES = B * S // P
+HEAD = 9
+
+
+def tile_mybadtransfomerblock_pa_kernel(tc, x, pos_emb, enc_w0, enc_w1_bytes, enc_w1_scale, out):
+    nc = tc.nc
+    with ExitStack() as ctx:
+        keep = ctx.enter_context(tc.tile_pool(name="keep", bufs=1))
+        work = ctx.enter_context(tc.tile_pool(name="work", bufs=3))
+        psum = ctx.enter_context(tc.psum_pool(name="psum", bufs=8))
+
+        ident = keep.tile([P, P], F32, tag="ident")
+        make_identity(nc, ident[:])
+        warm = keep.tile([P, 1], F32, tag="warm")
+        nc.vector.memset(warm[:], 1.0)
+        warm2 = keep.tile([P, 1], F32, tag="warm2")
+        nc.scalar.activation(out=warm2[:], in_=warm[:], func=ACT.Sqrt)
+
+        x_in, pos_in, w0_in, yp, yt, y_codes, y_scales = {}, {}, {}, {}, {}, {}, {}
+        ht, h_codes, h_scales, bank, res, sums, inv = {}, {}, {}, {}, {}, {}, {}
+        w1_prod = {}
+
+        w1_in = keep.tile([P, 8, D], U8, tag="w1_in")
+        w1_scale = keep.tile([P, D], F32, tag="w1_scale")
+        w0_codes = keep.tile([P, 8, PASSES, P], U32, tag="w0_codes", align_bytes=64)
+        w0_scales = keep.tile([P, 8, PASSES, P], U8, tag="w0_scales", align_bytes=64)
+        w1_grouped = keep.tile([P, PASSES, D, 4], BF16, tag="w1_grouped", align_bytes=64)
+        w1_codes = keep.tile([P, PASSES, D], U32, tag="w1_codes", align_bytes=64)
+        w1_scales = keep.tile([P, PASSES, D], U8, tag="w1_scales", align_bytes=64)
+
+        def load_x(i):
+            x_in[i] = work.tile([P, D], BF16, tag="x_in", bufs=TILES, name="x_in")
+            s0 = (i // 2) * P
+            nc.sync.dma_start(out=x_in[i][:], in_=x[i % 2, s0 : s0 + P, :])
+
+        def load_pos(j):
+            pos_in[j] = work.tile([P, D], BF16, tag="pos_in", bufs=8, name="pos_in")
+            nc.sync.dma_start(out=pos_in[j][:], in_=pos_emb[0, j * P : (j + 1) * P, :])
+
+        w0_rows = enc_w0.rearrange("(h m t) k -> h t m k", h=2, m=P, t=4)
+
+        def load_w0(c):
+            w0_in[c] = work.tile([P, D], BF16, tag="w0_in", bufs=8, name="w0_in")
+            nc.sync.dma_start(out=w0_in[c][:], in_=w0_rows[c // 4, c % 4])
+
+        w1_rows = enc_w1_bytes.rearrange("(a m) k -> m a k", m=P)
+
+        def load_w1(a, n):
+            nc.sync.dma_start(out=w1_in[:, a : a + n, :], in_=w1_rows[:, a : a + n, :])
+
+        def new_bank(key):
+            bank[key] = psum.tile([P, 512], F32, tag="bank", name="bank")
+            return bank[key]
+
+        def transpose_words(key, words, stepped):
+            b = new_bank(key)
+            v = b[:].rearrange("p (g u n) -> p g u n", g=2, u=2)
+            for g in range(2):
+                for u in range(2):
+                    if stepped:
+                        src = words[:, 256 * g + u : 256 * (g + 1) : 2]
+                    else:
+                        src = words[:, 256 * u + 128 * g : 256 * u + 128 * (g + 1)]
+                    nc.tensor.transpose(v[:, g, u, :], src, ident[:])
+
+        def copy_words(engine, key, dst):
+            src = bank.pop(key)[:].rearrange("p (g u n) -> p g n u", g=2, u=2)
+            if engine == "s":
+                nc.scalar.copy(out=dst, in_=src)
+            else:
+                nc.vector.tensor_copy(out=dst, in_=src)
+
+        def add_pos(i):
+            yp[i] = work.tile([P, D], BF16, tag="yp", name="yp")
+            pairs = "p (w u e) -> p w u e"
+            nc.vector.tensor_tensor(
+                out=yp[i][:].rearrange("p (u w e) -> p w u e", u=2, e=2),
+                in0=x_in.pop(i)[:].rearrange(pairs, u=2, e=2),
+                in1=pos_in[i // 2][:].rearrange(pairs, u=2, e=2),
+                op=ADD,
+            )
+
+        def transpose_y(i):
+            transpose_words(("y", i), yp.pop(i)[:].bitcast(F32), False)
+
+        def copy_y(i, engine):
+            yt[i] = work.tile([P, D], BF16, tag="yt", name="yt", align_bytes=64)
+            copy_words(engine, ("y", i), yt[i][:].bitcast(F32).rearrange("p (g n u) -> p g n u", g=2, u=2))
+
+        def quant_y(i):
+            y_codes[i] = work.tile([P, 256], U32, tag="y_codes", name="y_codes", align_bytes=64, bufs=4)
+            y_scales[i] = work.tile([P, 256], U8, tag="y_scales", name="y_scales", align_bytes=64, bufs=4)
+            nc.vector.quantize_mx(out=y_codes[i][:].bitcast(FP8X4), scales=y_scales[i][:], in_=yt.pop(i)[:])
+
+        w0_grouped = {}
+
+        def transpose_w0(c):
+            transpose_words(("w0", c), w0_in.pop(c)[:].bitcast(F32), True)
+
+        def copy_w0(c, engine):
+            w0_grouped[c] = work.tile([P, D], BF16, tag="w0_grouped", name="w0_grouped", align_bytes=64)
+            copy_words(engine, ("w0", c), w0_grouped[c][:].bitcast(F32).rearrange("p (g n u) -> p g n u", g=2, u=2))
+
+        def quant_w0(c):
+            nc.vector.quantize_mx(
+                out=w0_codes[:, c].rearrange("p g m -> p (g m)").bitcast(FP8X4),
+                scales=w0_scales[:, c].rearrange("p g m -> p (g m)"),
+                in_=w0_grouped.pop(c)[:],
+            )
+
+        def scale_w1(a):
+            w1_prod[a] = work.tile([P, D], BF16, tag="w1_prod", name="w1_prod")
+            nc.vector.tensor_tensor(out=w1_prod[a][:], in0=w1_in[:, a, :].bitcast(FP8), in1=w1_scale[:], op=MULT)
+
+        def transpose_w1(a):
+            transpose_words(("w1", a), w1_prod.pop(a)[:].bitcast(F32), True)
+
+        def copy_w1(a, engine):
+            dst = w1_grouped[:, :, a * P : (a + 1) * P, :].rearrange("p g n t -> p g (n t)").bitcast(F32)
+            copy_words(engine, ("w1", a), dst.rearrange("p g (n u) -> p g n u", u=2))
+
+        def quant_w1(pair):
+            cols = slice(pair * 256, (pair + 1) * 256)
+            for g in range(2):
+                nc.vector.quantize_mx(
+                    out=w1_codes[:, g, cols].bitcast(FP8X4),
+                    scales=w1_scales[:, g, cols],
+                    in_=w1_grouped[:, g, cols, :].rearrange("p n t -> p (n t)"),
+                )
+
+        def stage1(i, h):
+            yc, ys = y_codes[i], y_scales[i]
+            b = new_bank(("h", i, h))
+            for t in range(4):
+                for g in range(2):
+                    nc.tensor.matmul_mx(
+                        out=b[:, t * P : (t + 1) * P],
+                        lhsT=w0_codes[:, 4 * h + t, g, :].bitcast(FP8X4),
+                        lhsT_scale=w0_scales[:, 4 * h + t, g, :],
+                        rhs=yc[:, g * P : (g + 1) * P].bitcast(FP8X4),
+                        rhs_scale=ys[:, g * P : (g + 1) * P],
+                        start=(g == 0),
+                        stop=(g == 1),
+                    )
+
+        def relu_h(i, h, engine):
+            if h == 0:
+                ht[i] = work.tile([P, 2, P, 4], BF16, tag="ht", name="ht", align_bytes=64)
+            src = bank.pop(("h", i, h))[:].rearrange("p (t n) -> p n t", t=4)
+            dst = ht[i][:, h]
+            if engine == "s":
+                nc.scalar.activation(out=dst, in_=src, func=ACT.Relu)
+            else:
+                nc.vector.tensor_scalar(out=dst, in0=src, scalar1=0.0, scalar2=None, op0=MAX)
+
+        def quant_h(i):
+            h_codes[i] = work.tile([P, 256], U32, tag="h_codes", name="h_codes", align_bytes=64, bufs=12)
+            h_scales[i] = work.tile([P, 256], U8, tag="h_scales", name="h_scales", align_bytes=64, bufs=12)
+            nc.vector.quantize_mx(
+                out=h_codes[i][:].bitcast(FP8X4),
+                scales=h_scales[i][:],
+                in_=ht.pop(i)[:].rearrange("p h n t -> p (h n t)"),
+            )
+
+        def stage2(i, n):
+            hc, hs = h_codes[i], h_scales[i]
+            b = new_bank(("o", i, n))
+            for h in range(2):
+                nc.tensor.matmul_mx(
+                    out=b[:],
+                    lhsT=hc[:, h * P : (h + 1) * P].bitcast(FP8X4),
+                    lhsT_scale=hs[:, h * P : (h + 1) * P],
+                    rhs=w1_codes[:, h, n * 512 : (n + 1) * 512].bitcast(FP8X4),
+                    rhs_scale=w1_scales[:, h, n * 512 : (n + 1) * 512],
+                    start=(h == 0),
+                    stop=(h == 1),
+                )
+
+        def relu_out(i, n, engine):
+            if n == 0:
+                res[i] = work.tile([P, D], F32, tag="res", name="res", bufs=8)
+            src = bank.pop(("o", i, n))[:]
+            dst = res[i][:, n * 512 : (n + 1) * 512]
+            if engine == "s":
+                nc.scalar.activation(out=dst, in_=src, func=ACT.Relu)
+            else:
+                nc.vector.tensor_scalar(out=dst, in0=src, scalar1=0.0, scalar2=None, op0=MAX)
+
+        def squares(i, n, engine):
+            if i not in sums:
+                sums[i] = work.tile([P, 2], F32, tag="sums", name="sums", bufs=6)
+            cols = slice(0, D) if n is None else slice(n * 512, (n + 1) * 512)
+            acc = sums[i][:, n or 0 : (n or 0) + 1]
+            part = res[i][:, cols]
+            if engine == "s":
+                junk_s = work.tile([P, D], F32, tag="junk_s", name="junk_s", bufs=2)
+                nc.scalar.activation(out=junk_s[:, cols], in_=part, func=ACT.Square, accum_out=acc)
+            else:
+                junk_v = work.tile([P, D], F32, tag="junk_v", name="junk_v", bufs=2)
+                nc.vector.scalar_tensor_tensor(
+                    out=junk_v[:, cols], in0=part, scalar=1.0, in1=part, op0=MULT, op1=MULT, accum_out=acc
+                )
+
+        def root(i, halves):
+            inv[i] = work.tile([P, 1], F32, tag="inv", name="inv", bufs=6)
+            if halves:
+                nc.scalar.activation(out=inv[i][:], in_=sums[i][:, 0:1], func=ACT.Sqrt, bias=sums[i][:, 1:2])
+            else:
+                nc.scalar.activation(out=inv[i][:], in_=sums[i][:, 0:1], func=ACT.Sqrt)
+
+        def add_eps(i):
+            nc.vector.tensor_scalar(out=inv[i][:], in0=inv[i][:], scalar1=EPS, scalar2=None, op0=ADD)
+
+        def reciprocal(i):
+            nc.vector.reciprocal(out=inv[i][:], in_=inv[i][:])
+
+        def scale_store(i, n, engine):
+            cols = slice(0, D) if n is None else slice(n * 512, (n + 1) * 512)
+            r = res[i][:, cols]
+            if engine == "v":
+                nc.vector.tensor_scalar(out=r, in0=r, scalar1=inv[i][:], scalar2=None, op0=MULT)
+            elif engine == "g":
+                nc.gpsimd.tensor_scalar(out=r, in0=r, scalar1=inv[i][:], scalar2=0.0, op0=MULT, op1=ADD)
+            else:
+                nc.scalar.activation(out=r, in_=r, func=ACT.Copy, scale=inv[i][:])
+            s0 = (i // 2) * P
+            nc.sync.dma_start(out=out[i % 2, s0 : s0 + P, cols], in_=r)
+
+        load_w0(0)
+        load_x(0)
+        load_pos(0)
+        for c in range(1, 4):
+            load_w0(c)
+        load_x(1)
+        for c in range(4, 8):
+            load_w0(c)
+        load_x(2)
+        load_pos(1)
+        nc.sync.dma_start(out=w1_scale[:], in_=enc_w1_scale.rearrange("o k -> (o k)").partition_broadcast(P))
+        load_w1(0, 2)
+        load_x(3)
+        load_w1(2, 2)
+        load_x(4)
+        load_pos(2)
+        load_w1(4, 2)
+        load_x(5)
+        load_w1(6, 2)
+        for i in range(6, TILES):
+            load_x(i)
+            if i % 2 == 0:
+                load_pos(i // 2)
+
+        transpose_w0(0)
+        copy_w0(0, "s")
+        add_pos(0)
+        quant_w0(0)
+        transpose_y(0)
+        transpose_w0(1)
+        copy_y(0, "s")
+        copy_w0(1, "s")
+        transpose_w0(2)
+        copy_w0(2, "s")
+        quant_w0(1)
+        quant_y(0)
+        transpose_w0(3)
+        copy_w0(3, "s")
+        quant_w0(2)
+        add_pos(1)
+        transpose_y(1)
+        quant_w0(3)
+        copy_y(1, "s")
+        transpose_w0(4)
+        copy_w0(4, "s")
+        stage1(0, 0)
+        transpose_w0(5)
+        copy_w0(5, "s")
+        quant_y(1)
+        quant_w0(4)
+        transpose_w0(6)
+        copy_w0(6, "s")
+        quant_w0(5)
+        transpose_w0(7)
+        copy_w0(7, "v")
+        quant_w0(6)
+        add_pos(2)
+        quant_w0(7)
+        relu_h(0, 0, "s")
+        stage1(1, 0)
+        stage1(0, 1)
+        transpose_y(2)
+        relu_h(1, 0, "s")
+        relu_h(0, 1, "s")
+        stage1(1, 1)
+        copy_y(2, "s")
+        scale_w1(0)
+        quant_h(0)
+        add_pos(3)
+        quant_y(2)
+        relu_h(1, 1, "s")
+
+        for s in range(1, HEAD):
+            transpose_w1(s - 1)
+            transpose_y(s + 2)
+            copy_w1(s - 1, "s")
+            if s < 8:
+                scale_w1(s)
+            stage1(s + 1, 0)
+            stage1(s + 1, 1)
+            copy_y(s + 2, "s")
+            quant_h(s)
+            relu_h(s + 1, 0, "s")
+            add_pos(s + 3)
+            relu_h(s + 1, 1, "s")
+            if s % 2 == 0:
+                quant_w1(s // 2 - 1)
+            quant_y(s + 2)
+            if s >= 6:
+                stage2(s - 6, 0)
+                relu_out(s - 6, 0, "s")
+
+        transpose_y(HEAD + 2)
+        quant_h(HEAD)
+
+        started = 3
+        for q in range(10):
+            a, b = 2 * q, 2 * q + 1
+            i = HEAD + 1 + q
+            if a < TILES:
+                if a >= started:
+                    stage2(a, 0)
+                stage2(a, 1)
+            if i < TILES:
+                stage1(i, 0)
+                stage1(i, 1)
+            if i + 1 < TILES:
+                copy_y(i + 1, "v")
+            if a < TILES and a >= started:
+                relu_out(a, 0, "s")
+            if a < TILES:
+                relu_out(a, 1, "v")
+            if i + 2 < TILES:
+                add_pos(i + 2)
+                transpose_y(i + 2)
+            if i + 1 < TILES:
+                quant_y(i + 1)
+            if i < TILES:
+                relu_h(i, 0, "s")
+                relu_h(i, 1, "v")
+            if b < TILES:
+                if b >= started:
+                    stage2(b, 0)
+                stage2(b, 1)
+            for j in (a - 2, a - 1):
+                if 0 <= j < TILES - 2:
+                    squares(j, None, "s")
+                    root(j, False)
+                elif TILES - 2 <= j < TILES:
+                    squares(j, 0, "s")
+                    squares(j, 1, "v")
+                    root(j, True)
+            if i < TILES:
+                quant_h(i)
+            if b < TILES:
+                if b >= started:
+                    relu_out(b, 0, "s")
+                relu_out(b, 1, "s" if q % 3 == 0 and q < 6 else "v")
+            for j in (a - 2, a - 1):
+                if 0 <= j < TILES:
+                    add_eps(j)
+                    reciprocal(j)
+                    if j < TILES - 2:
+                        scale_store(j, None, "v")
+                    else:
+                        scale_store(j, 0, "v")
+                        scale_store(j, 1, "s")

@@ -21,7 +21,8 @@ ACT = mybir.ActivationFunctionType
 P = 128
 PASSES = 2
 TILES = B * S // P
-HEAD = 9
+CHUNKS = D // P
+BANKS = 8
 
 
 def tile_mybadtransfomerblock_pa_kernel(tc, x, pos_emb, enc_w0, enc_w1_bytes, enc_w1_scale, out):
@@ -29,26 +30,27 @@ def tile_mybadtransfomerblock_pa_kernel(tc, x, pos_emb, enc_w0, enc_w1_bytes, en
     with ExitStack() as ctx:
         keep = ctx.enter_context(tc.tile_pool(name="keep", bufs=1))
         work = ctx.enter_context(tc.tile_pool(name="work", bufs=3))
-        psum = ctx.enter_context(tc.psum_pool(name="psum", bufs=8))
+        psum = ctx.enter_context(tc.psum_pool(name="psum", bufs=1))
+        ctx.enter_context(tc.manual_schedule())
 
         ident = keep.tile([P, P], F32, tag="ident")
         make_identity(nc, ident[:])
-        warm = keep.tile([P, 1], F32, tag="warm")
-        nc.vector.memset(warm[:], 1.0)
-        warm2 = keep.tile([P, 1], F32, tag="warm2")
-        nc.scalar.activation(out=warm2[:], in_=warm[:], func=ACT.Sqrt)
 
-        x_in, pos_in, w0_in, yp, yt, y_codes, y_scales = {}, {}, {}, {}, {}, {}, {}
+        x_in, pos_in, w0_in, w1_in, yp, yt, y_codes, y_scales = {}, {}, {}, {}, {}, {}, {}, {}
         ht, h_codes, h_scales, bank, res, sums, inv = {}, {}, {}, {}, {}, {}, {}
-        w1_prod = {}
+        w1_prod, w0_grouped, w1_grouped = {}, {}, {}
+        free_banks = list(range(BANKS))
+        bank_number = {}
 
-        w1_in = keep.tile([P, 8, D], U8, tag="w1_in")
+        scale_cols = keep.tile([P, CHUNKS], F32, tag="scale_cols")
         w1_scale = keep.tile([P, D], F32, tag="w1_scale")
-        w0_codes = keep.tile([P, 8, PASSES, P], U32, tag="w0_codes", align_bytes=64)
-        w0_scales = keep.tile([P, 8, PASSES, P], U8, tag="w0_scales", align_bytes=64)
-        w1_grouped = keep.tile([P, PASSES, D, 4], BF16, tag="w1_grouped", align_bytes=64)
+        w0_codes = keep.tile([P, CHUNKS, PASSES, P], U32, tag="w0_codes", align_bytes=64)
+        w0_scales = keep.tile([P, CHUNKS, PASSES, P], U8, tag="w0_scales", align_bytes=64)
         w1_codes = keep.tile([P, PASSES, D], U32, tag="w1_codes", align_bytes=64)
         w1_scales = keep.tile([P, PASSES, D], U8, tag="w1_scales", align_bytes=64)
+
+        def load_scale():
+            nc.sync.dma_start(out=scale_cols[:], in_=enc_w1_scale.rearrange("o (p j) -> p (o j)", p=P))
 
         def load_x(i):
             x_in[i] = work.tile([P, D], BF16, tag="x_in", bufs=TILES, name="x_in")
@@ -62,17 +64,35 @@ def tile_mybadtransfomerblock_pa_kernel(tc, x, pos_emb, enc_w0, enc_w1_bytes, en
         w0_rows = enc_w0.rearrange("(h m t) k -> h t m k", h=2, m=P, t=4)
 
         def load_w0(c):
-            w0_in[c] = work.tile([P, D], BF16, tag="w0_in", bufs=8, name="w0_in")
+            w0_in[c] = work.tile([P, D], BF16, tag="w0_in", bufs=CHUNKS, name="w0_in")
             nc.sync.dma_start(out=w0_in[c][:], in_=w0_rows[c // 4, c % 4])
 
-        w1_rows = enc_w1_bytes.rearrange("(a m) k -> m a k", m=P)
-
-        def load_w1(a, n):
-            nc.sync.dma_start(out=w1_in[:, a : a + n, :], in_=w1_rows[:, a : a + n, :])
+        def load_w1(a):
+            w1_in[a] = work.tile([P, D], U8, tag="w1_in", bufs=CHUNKS, name="w1_in")
+            nc.sync.dma_start(out=w1_in[a][:], in_=enc_w1_bytes[a * P : (a + 1) * P, :])
 
         def new_bank(key):
-            bank[key] = psum.tile([P, 512], F32, tag="bank", name="bank")
+            bank_number[key] = free_banks.pop(0)
+            bank[key] = psum.tile([P, 512], F32, tag="bank%d" % bank_number[key], name="bank")
             return bank[key]
+
+        def take_bank(key):
+            free_banks.append(bank_number.pop(key))
+            return bank.pop(key)
+
+        def spread_scale(half):
+            b = new_bank(("scale", half))
+            for j in range(4):
+                col = scale_cols[:, 4 * half + j : 4 * half + j + 1]
+                nc.tensor.transpose(b[:, j * P : (j + 1) * P], col.to_broadcast([P, P]), ident[:])
+
+        def copy_scale(half, engine):
+            src = take_bank(("scale", half))[:].rearrange("p (j q) -> p q j", j=4)
+            dst = w1_scale[:].rearrange("p (q j) -> p q j", j=CHUNKS)[:, :, 4 * half : 4 * half + 4]
+            if engine == "s":
+                nc.scalar.copy(out=dst, in_=src)
+            else:
+                nc.vector.tensor_copy(out=dst, in_=src)
 
         def transpose_words(key, words, stepped):
             b = new_bank(key)
@@ -86,14 +106,14 @@ def tile_mybadtransfomerblock_pa_kernel(tc, x, pos_emb, enc_w0, enc_w1_bytes, en
                     nc.tensor.transpose(v[:, g, u, :], src, ident[:])
 
         def copy_words(engine, key, dst):
-            src = bank.pop(key)[:].rearrange("p (g u n) -> p g n u", g=2, u=2)
+            src = take_bank(key)[:].rearrange("p (g u n) -> p g n u", g=2, u=2)
             if engine == "s":
                 nc.scalar.copy(out=dst, in_=src)
             else:
                 nc.vector.tensor_copy(out=dst, in_=src)
 
         def add_pos(i):
-            yp[i] = work.tile([P, D], BF16, tag="yp", name="yp")
+            yp[i] = work.tile([P, D], BF16, tag="yp", name="yp", bufs=4)
             pairs = "p (w u e) -> p w u e"
             nc.vector.tensor_tensor(
                 out=yp[i][:].rearrange("p (u w e) -> p w u e", u=2, e=2),
@@ -106,15 +126,13 @@ def tile_mybadtransfomerblock_pa_kernel(tc, x, pos_emb, enc_w0, enc_w1_bytes, en
             transpose_words(("y", i), yp.pop(i)[:].bitcast(F32), False)
 
         def copy_y(i, engine):
-            yt[i] = work.tile([P, D], BF16, tag="yt", name="yt", align_bytes=64)
+            yt[i] = work.tile([P, D], BF16, tag="yt", name="yt", align_bytes=64, bufs=4)
             copy_words(engine, ("y", i), yt[i][:].bitcast(F32).rearrange("p (g n u) -> p g n u", g=2, u=2))
 
         def quant_y(i):
-            y_codes[i] = work.tile([P, 256], U32, tag="y_codes", name="y_codes", align_bytes=64, bufs=4)
-            y_scales[i] = work.tile([P, 256], U8, tag="y_scales", name="y_scales", align_bytes=64, bufs=4)
+            y_codes[i] = work.tile([P, 256], U32, tag="y_codes", name="y_codes", align_bytes=64, bufs=6)
+            y_scales[i] = work.tile([P, 256], U8, tag="y_scales", name="y_scales", align_bytes=64, bufs=6)
             nc.vector.quantize_mx(out=y_codes[i][:].bitcast(FP8X4), scales=y_scales[i][:], in_=yt.pop(i)[:])
-
-        w0_grouped = {}
 
         def transpose_w0(c):
             transpose_words(("w0", c), w0_in.pop(c)[:].bitcast(F32), True)
@@ -132,48 +150,54 @@ def tile_mybadtransfomerblock_pa_kernel(tc, x, pos_emb, enc_w0, enc_w1_bytes, en
 
         def scale_w1(a):
             w1_prod[a] = work.tile([P, D], BF16, tag="w1_prod", name="w1_prod")
-            nc.vector.tensor_tensor(out=w1_prod[a][:], in0=w1_in[:, a, :].bitcast(FP8), in1=w1_scale[:], op=MULT)
+            nc.vector.tensor_tensor(out=w1_prod[a][:], in0=w1_in.pop(a)[:].bitcast(FP8), in1=w1_scale[:], op=MULT)
 
         def transpose_w1(a):
             transpose_words(("w1", a), w1_prod.pop(a)[:].bitcast(F32), True)
 
         def copy_w1(a, engine):
-            dst = w1_grouped[:, :, a * P : (a + 1) * P, :].rearrange("p g n t -> p g (n t)").bitcast(F32)
+            if a % 2 == 0:
+                w1_grouped[a // 2] = work.tile([P, PASSES, 2 * P, 4], BF16, tag="w1_grouped", name="w1_grouped", align_bytes=64, bufs=2)
+            rows = slice((a % 2) * P, (a % 2 + 1) * P)
+            dst = w1_grouped[a // 2][:, :, rows, :].rearrange("p g n t -> p g (n t)").bitcast(F32)
             copy_words(engine, ("w1", a), dst.rearrange("p g (n u) -> p g n u", u=2))
 
-        def quant_w1(pair):
+        def quant_w1(pair, g):
             cols = slice(pair * 256, (pair + 1) * 256)
-            for g in range(2):
-                nc.vector.quantize_mx(
-                    out=w1_codes[:, g, cols].bitcast(FP8X4),
-                    scales=w1_scales[:, g, cols],
-                    in_=w1_grouped[:, g, cols, :].rearrange("p n t -> p (n t)"),
+            nc.vector.quantize_mx(
+                out=w1_codes[:, g, cols].bitcast(FP8X4),
+                scales=w1_scales[:, g, cols],
+                in_=w1_grouped[pair][:, g].rearrange("p n t -> p (n t)"),
+            )
+
+        def stage1_chunk(i, c):
+            h, t = divmod(c, 4)
+            b = new_bank(("h", i, h)) if t == 0 else bank[("h", i, h)]
+            for g in range(PASSES):
+                nc.tensor.matmul_mx(
+                    out=b[:, t * P : (t + 1) * P],
+                    lhsT=w0_codes[:, c, g, :].bitcast(FP8X4),
+                    lhsT_scale=w0_scales[:, c, g, :],
+                    rhs=y_codes[i][:, g * P : (g + 1) * P].bitcast(FP8X4),
+                    rhs_scale=y_scales[i][:, g * P : (g + 1) * P],
+                    start=(g == 0),
+                    stop=(g == PASSES - 1),
                 )
 
         def stage1(i, h):
-            yc, ys = y_codes[i], y_scales[i]
-            b = new_bank(("h", i, h))
             for t in range(4):
-                for g in range(2):
-                    nc.tensor.matmul_mx(
-                        out=b[:, t * P : (t + 1) * P],
-                        lhsT=w0_codes[:, 4 * h + t, g, :].bitcast(FP8X4),
-                        lhsT_scale=w0_scales[:, 4 * h + t, g, :],
-                        rhs=yc[:, g * P : (g + 1) * P].bitcast(FP8X4),
-                        rhs_scale=ys[:, g * P : (g + 1) * P],
-                        start=(g == 0),
-                        stop=(g == 1),
-                    )
+                stage1_chunk(i, 4 * h + t)
 
-        def relu_h(i, h, engine):
-            if h == 0:
-                ht[i] = work.tile([P, 2, P, 4], BF16, tag="ht", name="ht", align_bytes=64)
-            src = bank.pop(("h", i, h))[:].rearrange("p (t n) -> p n t", t=4)
-            dst = ht[i][:, h]
+        def relu(engine, dst, src):
             if engine == "s":
                 nc.scalar.activation(out=dst, in_=src, func=ACT.Relu)
             else:
                 nc.vector.tensor_scalar(out=dst, in0=src, scalar1=0.0, scalar2=None, op0=MAX)
+
+        def relu_h(i, h, engine):
+            if h == 0:
+                ht[i] = work.tile([P, 2, P, 4], BF16, tag="ht", name="ht", align_bytes=64, bufs=5)
+            relu(engine, ht[i][:, h], take_bank(("h", i, h))[:].rearrange("p (t n) -> p n t", t=4))
 
         def quant_h(i):
             h_codes[i] = work.tile([P, 256], U32, tag="h_codes", name="h_codes", align_bytes=64, bufs=12)
@@ -200,198 +224,232 @@ def tile_mybadtransfomerblock_pa_kernel(tc, x, pos_emb, enc_w0, enc_w1_bytes, en
 
         def relu_out(i, n, engine):
             if n == 0:
-                res[i] = work.tile([P, D], F32, tag="res", name="res", bufs=8)
-            src = bank.pop(("o", i, n))[:]
-            dst = res[i][:, n * 512 : (n + 1) * 512]
-            if engine == "s":
-                nc.scalar.activation(out=dst, in_=src, func=ACT.Relu)
-            else:
-                nc.vector.tensor_scalar(out=dst, in0=src, scalar1=0.0, scalar2=None, op0=MAX)
+                res[i] = work.tile([P, D], F32, tag="res", name="res", bufs=10)
+            relu(engine, res[i][:, n * 512 : (n + 1) * 512], take_bank(("o", i, n))[:])
 
-        def squares(i, n, engine):
-            if i not in sums:
-                sums[i] = work.tile([P, 2], F32, tag="sums", name="sums", bufs=6)
-            cols = slice(0, D) if n is None else slice(n * 512, (n + 1) * 512)
-            acc = sums[i][:, n or 0 : (n or 0) + 1]
+        def squares(i, cols, engine, slot):
+            if i // 2 not in sums:
+                sums[i // 2] = work.tile([P, 4], F32, tag="sums", name="sums", bufs=4)
+            acc = sums[i // 2][:, slot : slot + 1]
             part = res[i][:, cols]
             if engine == "s":
-                junk_s = work.tile([P, D], F32, tag="junk_s", name="junk_s", bufs=2)
+                junk_s = work.tile([P, D], BF16, tag="junk_s", name="junk_s", bufs=2)
                 nc.scalar.activation(out=junk_s[:, cols], in_=part, func=ACT.Square, accum_out=acc)
             else:
-                junk_v = work.tile([P, D], F32, tag="junk_v", name="junk_v", bufs=2)
+                junk_v = work.tile([P, D], BF16, tag="junk_v", name="junk_v", bufs=2)
                 nc.vector.scalar_tensor_tensor(
                     out=junk_v[:, cols], in0=part, scalar=1.0, in1=part, op0=MULT, op1=MULT, accum_out=acc
                 )
 
-        def root(i, halves):
-            inv[i] = work.tile([P, 1], F32, tag="inv", name="inv", bufs=6)
-            if halves:
-                nc.scalar.activation(out=inv[i][:], in_=sums[i][:, 0:1], func=ACT.Sqrt, bias=sums[i][:, 1:2])
-            else:
-                nc.scalar.activation(out=inv[i][:], in_=sums[i][:, 0:1], func=ACT.Sqrt)
+        def root(f):
+            inv[f] = work.tile([P, 2], F32, tag="inv", name="inv", bufs=4)
+            nc.scalar.activation(out=inv[f][:], in_=sums[f][:, 0:2], func=ACT.Sqrt)
 
-        def add_eps(i):
-            nc.vector.tensor_scalar(out=inv[i][:], in0=inv[i][:], scalar1=EPS, scalar2=None, op0=ADD)
+        def root_of_halves(i):
+            f, e = divmod(i, 2)
+            if e == 0:
+                inv[f] = work.tile([P, 2], F32, tag="inv", name="inv", bufs=4)
+            nc.scalar.activation(
+                out=inv[f][:, e : e + 1], in_=sums[f][:, e : e + 1], func=ACT.Sqrt, bias=sums[f][:, 2 + e : 3 + e]
+            )
 
-        def reciprocal(i):
-            nc.vector.reciprocal(out=inv[i][:], in_=inv[i][:])
+        def add_eps(f):
+            nc.vector.tensor_scalar(out=inv[f][:], in0=inv[f][:], scalar1=EPS, scalar2=None, op0=ADD)
 
-        def scale_store(i, n, engine):
+        def reciprocal(f):
+            nc.vector.reciprocal(out=inv[f][:], in_=inv[f][:])
+
+        def scale_out(i, n, engine):
             cols = slice(0, D) if n is None else slice(n * 512, (n + 1) * 512)
             r = res[i][:, cols]
             if engine == "v":
-                nc.vector.tensor_scalar(out=r, in0=r, scalar1=inv[i][:], scalar2=None, op0=MULT)
+                nc.vector.tensor_scalar(out=r, in0=r, scalar1=inv[i // 2][:, i % 2 : i % 2 + 1], scalar2=None, op0=MULT)
             elif engine == "g":
-                nc.gpsimd.tensor_scalar(out=r, in0=r, scalar1=inv[i][:], scalar2=0.0, op0=MULT, op1=ADD)
+                nc.gpsimd.tensor_scalar(out=r, in0=r, scalar1=inv[i // 2][:, i % 2 : i % 2 + 1], scalar2=0.0, op0=MULT, op1=ADD)
             else:
-                nc.scalar.activation(out=r, in_=r, func=ACT.Copy, scale=inv[i][:])
+                nc.scalar.activation(out=r, in_=r, func=ACT.Copy, scale=inv[i // 2][:, i % 2 : i % 2 + 1])
             s0 = (i // 2) * P
             nc.sync.dma_start(out=out[i % 2, s0 : s0 + P, cols], in_=r)
 
-        load_w0(0)
+        load_scale()
         load_x(0)
         load_pos(0)
-        for c in range(1, 4):
-            load_w0(c)
+        load_w1(0)
+        load_w0(0)
+        load_w0(1)
         load_x(1)
-        for c in range(4, 8):
+        load_w1(1)
+        for c in range(2, 6):
             load_w0(c)
         load_x(2)
         load_pos(1)
-        nc.sync.dma_start(out=w1_scale[:], in_=enc_w1_scale.rearrange("o k -> (o k)").partition_broadcast(P))
-        load_w1(0, 2)
+        load_w0(6)
+        load_w0(7)
         load_x(3)
-        load_w1(2, 2)
-        load_x(4)
-        load_pos(2)
-        load_w1(4, 2)
-        load_x(5)
-        load_w1(6, 2)
-        for i in range(6, TILES):
+        for i in range(4, TILES):
+            if i - 2 < CHUNKS:
+                load_w1(i - 2)
             load_x(i)
             if i % 2 == 0:
                 load_pos(i // 2)
 
-        transpose_w0(0)
-        copy_w0(0, "s")
+        spread_scale(0)
+        spread_scale(1)
+        copy_scale(0, "v")
+        copy_scale(1, "s")
         add_pos(0)
-        quant_w0(0)
+        scale_w1(0)
         transpose_y(0)
-        transpose_w0(1)
         copy_y(0, "s")
-        copy_w0(1, "s")
-        transpose_w0(2)
-        copy_w0(2, "s")
+        for c in range(2):
+            transpose_w0(c)
+            copy_w0(c, "s")
+        transpose_w1(0)
+        copy_w1(0, "s")
+        add_pos(1)
+        quant_w0(0)
+        scale_w1(1)
+        for c in range(2, 4):
+            transpose_w0(c)
+            copy_w0(c, "s")
         quant_w0(1)
         quant_y(0)
-        transpose_w0(3)
-        copy_w0(3, "s")
-        quant_w0(2)
-        add_pos(1)
         transpose_y(1)
-        quant_w0(3)
-        copy_y(1, "s")
         transpose_w0(4)
-        copy_w0(4, "s")
-        stage1(0, 0)
+        transpose_w1(1)
         transpose_w0(5)
+        copy_y(1, "v")
+        quant_w0(2)
+        quant_w0(3)
+        copy_w0(4, "s")
+        copy_w1(1, "s")
         copy_w0(5, "s")
         quant_y(1)
+        stage1(0, 0)
+        add_pos(2)
         quant_w0(4)
         transpose_w0(6)
-        copy_w0(6, "s")
-        quant_w0(5)
         transpose_w0(7)
-        copy_w0(7, "v")
-        quant_w0(6)
-        add_pos(2)
-        quant_w0(7)
-        relu_h(0, 0, "s")
-        stage1(1, 0)
-        stage1(0, 1)
         transpose_y(2)
-        relu_h(1, 0, "s")
-        relu_h(0, 1, "s")
-        stage1(1, 1)
+        relu_h(0, 0, "s")
+        quant_w0(5)
+        copy_w0(6, "s")
+        copy_w0(7, "s")
         copy_y(2, "s")
-        scale_w1(0)
-        quant_h(0)
+        stage1(1, 0)
         add_pos(3)
+        quant_w0(6)
+        quant_w0(7)
+        relu_h(1, 0, "s")
+        transpose_y(3)
+        copy_y(3, "s")
+        stage1(0, 1)
+        stage1(1, 1)
         quant_y(2)
+        add_pos(4)
+        quant_w1(0, 0)
+        quant_w1(0, 1)
+        relu_h(0, 1, "s")
         relu_h(1, 1, "s")
 
-        for s in range(1, HEAD):
-            transpose_w1(s - 1)
-            transpose_y(s + 2)
-            copy_w1(s - 1, "s")
-            if s < 8:
-                scale_w1(s)
-            stage1(s + 1, 0)
-            stage1(s + 1, 1)
-            copy_y(s + 2, "s")
-            quant_h(s)
-            relu_h(s + 1, 0, "s")
+        W1_TURN = {3: 2, 4: 3, 5: 4, 6: 5, 7: 6, 8: 7}
+        EARLY = {6: 0, 7: 1, 8: 2, 9: 3}
+        FIRST = 10
+        ALL = slice(0, D)
+        for s in range(2, FIRST):
+            turns = [(transpose_y, copy_y, (s + 2,))]
+            if s in W1_TURN:
+                turns.append((transpose_w1, copy_w1, (W1_TURN[s],)))
+            products = [(stage1, relu_h, (s, h)) for h in range(2)]
+            if s in EARLY:
+                products.append((stage2, relu_out, (EARLY[s], 0)))
             add_pos(s + 3)
-            relu_h(s + 1, 1, "s")
-            if s % 2 == 0:
-                quant_w1(s // 2 - 1)
-            quant_y(s + 2)
-            if s >= 6:
-                stage2(s - 6, 0)
-                relu_out(s - 6, 0, "s")
-
-        transpose_y(HEAD + 2)
-        quant_h(HEAD)
-
-        started = 3
-        for q in range(10):
-            a, b = 2 * q, 2 * q + 1
-            i = HEAD + 1 + q
-            if a < TILES:
-                if a >= started:
-                    stage2(a, 0)
-                stage2(a, 1)
-            if i < TILES:
-                stage1(i, 0)
-                stage1(i, 1)
-            if i + 1 < TILES:
-                copy_y(i + 1, "v")
-            if a < TILES and a >= started:
-                relu_out(a, 0, "s")
-            if a < TILES:
-                relu_out(a, 1, "v")
-            if i + 2 < TILES:
-                add_pos(i + 2)
-                transpose_y(i + 2)
-            if i + 1 < TILES:
-                quant_y(i + 1)
-            if i < TILES:
-                relu_h(i, 0, "s")
-                relu_h(i, 1, "v")
-            if b < TILES:
-                if b >= started:
-                    stage2(b, 0)
-                stage2(b, 1)
-            for j in (a - 2, a - 1):
-                if 0 <= j < TILES - 2:
-                    squares(j, None, "s")
-                    root(j, False)
-                elif TILES - 2 <= j < TILES:
-                    squares(j, 0, "s")
-                    squares(j, 1, "v")
-                    root(j, True)
-            if i < TILES:
+            quant_y(s + 1)
+            if s + 1 in W1_TURN:
+                scale_w1(W1_TURN[s + 1])
+            for i in (0, 1) if s == 2 else (s - 1,):
                 quant_h(i)
-            if b < TILES:
-                if b >= started:
-                    relu_out(b, 0, "s")
-                relu_out(b, 1, "s" if q % 3 == 0 and q < 6 else "v")
-            for j in (a - 2, a - 1):
-                if 0 <= j < TILES:
-                    add_eps(j)
-                    reciprocal(j)
-                    if j < TILES - 2:
-                        scale_store(j, None, "v")
-                    else:
-                        scale_store(j, 0, "v")
-                        scale_store(j, 1, "s")
+            if s - 1 in W1_TURN and W1_TURN[s - 1] % 2 == 1:
+                quant_w1(W1_TURN[s - 1] // 2, 0)
+                quant_w1(W1_TURN[s - 1] // 2, 1)
+            jobs = turns + products if s % 2 == 0 else products + turns
+            for n, (fill, empty, args) in enumerate(jobs):
+                fill(*args)
+                empty(*args, "v" if s + 1 not in W1_TURN and n == 1 else "s")
+
+        PAIRS = TILES // 2
+        for f in range(PAIRS - 1):
+            s = FIRST + f
+            a, b = 2 * f, 2 * f + 1
+            early = a in EARLY.values()
+            if s == TILES - 1:
+                quant_h(s - 1)
+                stage1(s, 0)
+                relu_h(s, 0, "s")
+                stage1(s, 1)
+                relu_h(s, 1, "v")
+            if not early:
+                stage2(a, 0)
+                relu_out(a, 0, "v")
+            stage2(a, 1)
+            relu_out(a, 1, "s" if s < TILES else "v")
+            if f > 0:
+                root(f - 1)
+            if not early:
+                stage2(b, 0)
+                relu_out(b, 0, "v")
+            stage2(b, 1)
+            relu_out(b, 1, "v" if early else "s")
+            if f > 0:
+                add_eps(f - 1)
+            if s < TILES:
+                quant_h(s - 1 if s < TILES - 1 else s)
+            if s + 3 < TILES:
+                add_pos(s + 3)
+            if f > 0:
+                reciprocal(f - 1)
+            if s < TILES - 1:
+                stage1(s, 0)
+                relu_h(s, 0, "s")
+            squares(a, ALL, "s", 0)
+            if s + 1 < TILES:
+                quant_y(s + 1)
+            if f > 0:
+                scale_out(a - 2, None, "v")
+                scale_out(a - 1, None, "v")
+            if s < TILES - 1:
+                stage1(s, 1)
+                relu_h(s, 1, "v")
+            if s + 2 < TILES:
+                transpose_y(s + 2)
+                copy_y(s + 2, "v" if early or False else "s")
+            squares(b, ALL, "s", 1)
+        f = PAIRS - 1
+        a, b = 2 * f, 2 * f + 1
+        LOW, HIGH = slice(0, 512), slice(512, D)
+        stage2(a, 0)
+        relu_out(a, 0, "v")
+        root(f - 1)
+        stage2(a, 1)
+        relu_out(a, 1, "s")
+        add_eps(f - 1)
+        stage2(b, 0)
+        relu_out(b, 0, "v")
+        reciprocal(f - 1)
+        stage2(b, 1)
+        relu_out(b, 1, "s")
+        squares(a, HIGH, "v", 2)
+        squares(a, LOW, "s", 0)
+        scale_out(a - 2, None, "v")
+        squares(b, LOW, "s", 1)
+        squares(b, HIGH, "v", 3)
+        root_of_halves(a)
+        scale_out(a - 1, 0, "s")
+        scale_out(a - 1, 1, "v")
+        root_of_halves(b)
+        add_eps(f)
+        reciprocal(f)
+        scale_out(a, 0, "v")
+        scale_out(b, 0, "s")
+        scale_out(a, 1, "v")
+        scale_out(b, 1, "v")

@@ -35,10 +35,14 @@ def tile_mybadtransfomerblock_pa_kernel(tc, x, pos_emb, enc_w0, enc_w1_bytes, en
 
         ident = keep.tile([P, P], F32, tag="ident")
         make_identity(nc, ident[:])
+        warm = keep.tile([P, 1], F32, tag="warm")
+        nc.vector.memset(warm[:], 1.0)
+        warm2 = keep.tile([P, 1], F32, tag="warm2")
+        nc.scalar.activation(out=warm2[:], in_=warm[:], func=ACT.Sqrt)
 
         x_in, pos_in, w0_in, w1_in, yp, yt, y_codes, y_scales = {}, {}, {}, {}, {}, {}, {}, {}
         ht, h_codes, h_scales, bank, res, sums, inv = {}, {}, {}, {}, {}, {}, {}
-        w1_prod, w0_grouped, w1_grouped = {}, {}, {}
+        w1_prod, w0_grouped, w1_grouped, w0_sorted = {}, {}, {}, {}
         free_banks = list(range(BANKS))
         bank_number = {}
 
@@ -134,8 +138,18 @@ def tile_mybadtransfomerblock_pa_kernel(tc, x, pos_emb, enc_w0, enc_w1_bytes, en
             y_scales[i] = work.tile([P, 256], U8, tag="y_scales", name="y_scales", align_bytes=64, bufs=6)
             nc.vector.quantize_mx(out=y_codes[i][:].bitcast(FP8X4), scales=y_scales[i][:], in_=yt.pop(i)[:])
 
+        def sort_w0(c):
+            w0_sorted[c] = work.tile([P, D], BF16, tag="w0_sorted", name="w0_sorted")
+            nc.vector.tensor_copy(
+                out=w0_sorted[c][:].bitcast(F32).rearrange("p (u w) -> p u w", u=2),
+                in_=w0_in.pop(c)[:].bitcast(F32).rearrange("p (w u) -> p u w", u=2),
+            )
+
         def transpose_w0(c):
-            transpose_words(("w0", c), w0_in.pop(c)[:].bitcast(F32), True)
+            if c in w0_sorted:
+                transpose_words(("w0", c), w0_sorted.pop(c)[:].bitcast(F32), False)
+            else:
+                transpose_words(("w0", c), w0_in.pop(c)[:].bitcast(F32), True)
 
         def copy_w0(c, engine):
             w0_grouped[c] = work.tile([P, D], BF16, tag="w0_grouped", name="w0_grouped", align_bytes=64)
@@ -149,7 +163,7 @@ def tile_mybadtransfomerblock_pa_kernel(tc, x, pos_emb, enc_w0, enc_w1_bytes, en
             )
 
         def scale_w1(a):
-            w1_prod[a] = work.tile([P, D], BF16, tag="w1_prod", name="w1_prod")
+            w1_prod[a] = work.tile([P, D], BF16, tag="w1_prod", name="w1_prod", bufs=4)
             nc.vector.tensor_tensor(out=w1_prod[a][:], in0=w1_in.pop(a)[:].bitcast(FP8), in1=w1_scale[:], op=MULT)
 
         def transpose_w1(a):
@@ -272,91 +286,129 @@ def tile_mybadtransfomerblock_pa_kernel(tc, x, pos_emb, enc_w0, enc_w1_bytes, en
             nc.sync.dma_start(out=out[i % 2, s0 : s0 + P, cols], in_=r)
 
         load_scale()
+        load_w0(0)
         load_x(0)
         load_pos(0)
-        load_w1(0)
-        load_w0(0)
         load_w0(1)
+        load_w1(0)
         load_x(1)
+        load_w0(2)
+        load_w0(3)
         load_w1(1)
-        for c in range(2, 6):
-            load_w0(c)
         load_x(2)
         load_pos(1)
+        load_x(3)
+        load_w0(4)
+        load_w0(5)
+        load_w1(2)
         load_w0(6)
         load_w0(7)
-        load_x(3)
         for i in range(4, TILES):
-            if i - 2 < CHUNKS:
-                load_w1(i - 2)
+            if i - 4 + 3 < CHUNKS:
+                load_w1(i - 4 + 3)
             load_x(i)
             if i % 2 == 0:
                 load_pos(i // 2)
-
         spread_scale(0)
         spread_scale(1)
         copy_scale(0, "v")
         copy_scale(1, "s")
+        transpose_w0(0)
+        copy_w0(0, "s")
         add_pos(0)
-        scale_w1(0)
+        sort_w0(1)
         transpose_y(0)
+        transpose_w0(1)
         copy_y(0, "s")
-        for c in range(2):
-            transpose_w0(c)
-            copy_w0(c, "s")
-        transpose_w1(0)
-        copy_w1(0, "s")
+        copy_w0(1, "s")
+        scale_w1(0)
+        sort_w0(2)
         add_pos(1)
+        sort_w0(3)
         quant_w0(0)
-        scale_w1(1)
-        for c in range(2, 4):
-            transpose_w0(c)
-            copy_w0(c, "s")
-        quant_w0(1)
-        quant_y(0)
+        transpose_w0(2)
+        copy_w0(2, "s")
         transpose_y(1)
-        transpose_w0(4)
-        transpose_w1(1)
-        transpose_w0(5)
-        copy_y(1, "v")
-        quant_w0(2)
-        quant_w0(3)
-        copy_w0(4, "s")
-        copy_w1(1, "s")
-        copy_w0(5, "s")
-        quant_y(1)
-        stage1(0, 0)
+        copy_y(1, "s")
+        transpose_w0(3)
+        copy_w0(3, "s")
+        quant_y(0)
+        quant_w0(1)
         add_pos(2)
+        quant_w0(2)
+        quant_y(1)
+        transpose_y(2)
+        copy_y(2, "s")
+        quant_w0(3)
+        add_pos(3)
+        scale_w1(1)
+        stage1_chunk(0, 0)
+        stage1_chunk(1, 0)
+        stage1_chunk(0, 1)
+        stage1_chunk(1, 1)
+        stage1_chunk(0, 2)
+        stage1_chunk(1, 2)
+        stage1_chunk(0, 3)
+        stage1_chunk(1, 3)
+        quant_y(2)
+        scale_w1(2)
+        transpose_w0(4)
+        transpose_y(3)
+        relu_h(0, 0, "s")
+        relu_h(1, 0, "s")
+        copy_w0(4, "s")
+        copy_y(3, "s")
+        stage1(2, 0)
+        transpose_w0(5)
+        transpose_w1(0)
         quant_w0(4)
+        quant_y(3)
+        relu_h(2, 0, "v")
+        copy_w0(5, "s")
+        copy_w1(0, "s")
+        add_pos(4)
+        stage1(3, 0)
         transpose_w0(6)
         transpose_w0(7)
-        transpose_y(2)
-        relu_h(0, 0, "s")
         quant_w0(5)
+        relu_h(3, 0, "s")
         copy_w0(6, "s")
-        copy_w0(7, "s")
-        copy_y(2, "s")
-        stage1(1, 0)
-        add_pos(3)
+        copy_w0(7, "v")
+        stage1_chunk(0, 4)
+        stage1_chunk(1, 4)
+        stage1_chunk(0, 5)
+        stage1_chunk(1, 5)
+        transpose_y(4)
+        transpose_w1(1)
         quant_w0(6)
         quant_w0(7)
-        relu_h(1, 0, "s")
-        transpose_y(3)
-        copy_y(3, "s")
-        stage1(0, 1)
-        stage1(1, 1)
-        quant_y(2)
-        add_pos(4)
-        quant_w1(0, 0)
-        quant_w1(0, 1)
+        copy_y(4, "s")
+        copy_w1(1, "s")
+        add_pos(5)
+        stage1_chunk(0, 6)
+        stage1_chunk(1, 6)
+        stage1_chunk(0, 7)
+        stage1_chunk(1, 7)
+        stage1(2, 1)
+        transpose_y(5)
+        transpose_w1(2)
         relu_h(0, 1, "s")
         relu_h(1, 1, "s")
-
-        W1_TURN = {3: 2, 4: 3, 5: 4, 6: 5, 7: 6, 8: 7}
+        scale_w1(3)
+        quant_y(4)
+        stage1(3, 1)
+        relu_h(2, 1, "s")
+        copy_y(5, "s")
+        copy_w1(2, "s")
+        relu_h(3, 1, "s")
+        quant_w1(0, 0)
+        quant_w1(0, 1)
+        add_pos(6)
+        W1_TURN = {4: 3, 5: 4, 6: 5, 7: 6, 8: 7}
         EARLY = {6: 0, 7: 1, 8: 2, 9: 3}
         FIRST = 10
         ALL = slice(0, D)
-        for s in range(2, FIRST):
+        for s in range(4, FIRST):
             turns = [(transpose_y, copy_y, (s + 2,))]
             if s in W1_TURN:
                 turns.append((transpose_w1, copy_w1, (W1_TURN[s],)))
@@ -367,30 +419,35 @@ def tile_mybadtransfomerblock_pa_kernel(tc, x, pos_emb, enc_w0, enc_w1_bytes, en
             quant_y(s + 1)
             if s + 1 in W1_TURN:
                 scale_w1(W1_TURN[s + 1])
-            for i in (0, 1) if s == 2 else (s - 1,):
+            for i in range(0, s) if s == 4 else (s - 1,):
                 quant_h(i)
             if s - 1 in W1_TURN and W1_TURN[s - 1] % 2 == 1:
                 quant_w1(W1_TURN[s - 1] // 2, 0)
                 quant_w1(W1_TURN[s - 1] // 2, 1)
-            jobs = turns + products if s % 2 == 0 else products + turns
+            jobs = turns + products
             for n, (fill, empty, args) in enumerate(jobs):
                 fill(*args)
                 empty(*args, "v" if s + 1 not in W1_TURN and n == 1 else "s")
 
         PAIRS = TILES // 2
+
+        def turns_of(s):
+            return [i for i in (s + 2, s + 3) if i < TILES and (s - FIRST) % 2 == 0]
+
+        def adds(s):
+            return [i for i in (s + 3, s + 4) if (s - FIRST) % 2 == 1 and i in x_in]
+
+        add_pos(FIRST + 3)
+
         for f in range(PAIRS - 1):
             s = FIRST + f
             a, b = 2 * f, 2 * f + 1
             early = a in EARLY.values()
-            if s == TILES - 1:
-                quant_h(s - 1)
-                stage1(s, 0)
-                relu_h(s, 0, "s")
-                stage1(s, 1)
-                relu_h(s, 1, "v")
             if not early:
                 stage2(a, 0)
                 relu_out(a, 0, "v")
+            if s == TILES:
+                quant_h(s - 1)
             stage2(a, 1)
             relu_out(a, 1, "s" if s < TILES else "v")
             if f > 0:
@@ -403,12 +460,12 @@ def tile_mybadtransfomerblock_pa_kernel(tc, x, pos_emb, enc_w0, enc_w1_bytes, en
             if f > 0:
                 add_eps(f - 1)
             if s < TILES:
-                quant_h(s - 1 if s < TILES - 1 else s)
-            if s + 3 < TILES:
-                add_pos(s + 3)
+                quant_h(s - 1)
+            for i in adds(s):
+                add_pos(i)
             if f > 0:
                 reciprocal(f - 1)
-            if s < TILES - 1:
+            if s < TILES:
                 stage1(s, 0)
                 relu_h(s, 0, "s")
             squares(a, ALL, "s", 0)
@@ -417,12 +474,12 @@ def tile_mybadtransfomerblock_pa_kernel(tc, x, pos_emb, enc_w0, enc_w1_bytes, en
             if f > 0:
                 scale_out(a - 2, None, "v")
                 scale_out(a - 1, None, "v")
-            if s < TILES - 1:
+            if s < TILES:
                 stage1(s, 1)
                 relu_h(s, 1, "v")
-            if s + 2 < TILES:
-                transpose_y(s + 2)
-                copy_y(s + 2, "v" if early or False else "s")
+            for i in turns_of(s):
+                transpose_y(i)
+                copy_y(i, "v" if early or i % 2 == 1 else "s")
             squares(b, ALL, "s", 1)
         f = PAIRS - 1
         a, b = 2 * f, 2 * f + 1

@@ -100,7 +100,7 @@ def tile_mybadtransfomerblock_pa_kernel(tc, x, pos_emb, enc_w0, enc_w1_bytes, en
 
         def transpose_words(key, words, stepped):
             b = new_bank(key)
-            v = b[:].rearrange("p (g u n) -> p g u n", g=2, u=2)
+            v = b[:].rearrange("p (u g n) -> p g u n", g=2, u=2)
             for g in range(2):
                 for u in range(2):
                     if stepped:
@@ -110,7 +110,7 @@ def tile_mybadtransfomerblock_pa_kernel(tc, x, pos_emb, enc_w0, enc_w1_bytes, en
                     nc.tensor.transpose(v[:, g, u, :], src, ident[:])
 
         def copy_words(engine, key, dst):
-            src = take_bank(key)[:].rearrange("p (g u n) -> p g n u", g=2, u=2)
+            src = take_bank(key)[:].rearrange("p (u g c i) -> p g c u i", g=2, u=2, i=2)
             if engine == "s":
                 nc.scalar.copy(out=dst, in_=src)
             else:
@@ -120,9 +120,9 @@ def tile_mybadtransfomerblock_pa_kernel(tc, x, pos_emb, enc_w0, enc_w1_bytes, en
             yp[i] = work.tile([P, D], BF16, tag="yp", name="yp", bufs=4)
             pairs = "p (w u e) -> p w u e"
             nc.vector.tensor_tensor(
-                out=yp[i][:].rearrange("p (u w e) -> p w u e", u=2, e=2),
-                in0=x_in.pop(i)[:].rearrange(pairs, u=2, e=2),
-                in1=pos_in[i // 2][:].rearrange(pairs, u=2, e=2),
+                out=yp[i][:].rearrange("p (u w e) -> p w u e", u=2, e=16),
+                in0=x_in.pop(i)[:].rearrange(pairs, u=2, e=16),
+                in1=pos_in[i // 2][:].rearrange(pairs, u=2, e=16),
                 op=ADD,
             )
 
@@ -131,7 +131,7 @@ def tile_mybadtransfomerblock_pa_kernel(tc, x, pos_emb, enc_w0, enc_w1_bytes, en
 
         def copy_y(i, engine):
             yt[i] = work.tile([P, D], BF16, tag="yt", name="yt", align_bytes=64, bufs=4)
-            copy_words(engine, ("y", i), yt[i][:].bitcast(F32).rearrange("p (g n u) -> p g n u", g=2, u=2))
+            copy_words(engine, ("y", i), yt[i][:].bitcast(F32).rearrange("p (g c i u) -> p g c u i", g=2, u=2, i=2))
 
         def quant_y(i):
             y_codes[i] = work.tile([P, 256], U32, tag="y_codes", name="y_codes", align_bytes=64, bufs=6)
@@ -139,21 +139,18 @@ def tile_mybadtransfomerblock_pa_kernel(tc, x, pos_emb, enc_w0, enc_w1_bytes, en
             nc.vector.quantize_mx(out=y_codes[i][:].bitcast(FP8X4), scales=y_scales[i][:], in_=yt.pop(i)[:])
 
         def sort_w0(c):
-            w0_sorted[c] = work.tile([P, D], BF16, tag="w0_sorted", name="w0_sorted")
+            w0_sorted[c] = work.tile([P, D], BF16, tag="w0_sorted", name="w0_sorted", bufs=4)
             nc.vector.tensor_copy(
-                out=w0_sorted[c][:].bitcast(F32).rearrange("p (u w) -> p u w", u=2),
-                in_=w0_in.pop(c)[:].bitcast(F32).rearrange("p (w u) -> p u w", u=2),
+                out=w0_sorted[c][:].rearrange("p (u w e) -> p w u e", u=2, e=16),
+                in_=w0_in.pop(c)[:].rearrange("p (w u e) -> p w u e", u=2, e=16),
             )
 
         def transpose_w0(c):
-            if c in w0_sorted:
-                transpose_words(("w0", c), w0_sorted.pop(c)[:].bitcast(F32), False)
-            else:
-                transpose_words(("w0", c), w0_in.pop(c)[:].bitcast(F32), True)
+            transpose_words(("w0", c), w0_sorted.pop(c)[:].bitcast(F32), False)
 
         def copy_w0(c, engine):
             w0_grouped[c] = work.tile([P, D], BF16, tag="w0_grouped", name="w0_grouped", align_bytes=64)
-            copy_words(engine, ("w0", c), w0_grouped[c][:].bitcast(F32).rearrange("p (g n u) -> p g n u", g=2, u=2))
+            copy_words(engine, ("w0", c), w0_grouped[c][:].bitcast(F32).rearrange("p (g c i u) -> p g c u i", g=2, u=2, i=2))
 
         def quant_w0(c):
             nc.vector.quantize_mx(
@@ -174,7 +171,7 @@ def tile_mybadtransfomerblock_pa_kernel(tc, x, pos_emb, enc_w0, enc_w1_bytes, en
                 w1_grouped[a // 2] = work.tile([P, PASSES, 2 * P, 4], BF16, tag="w1_grouped", name="w1_grouped", align_bytes=64, bufs=2)
             rows = slice((a % 2) * P, (a % 2 + 1) * P)
             dst = w1_grouped[a // 2][:, :, rows, :].rearrange("p g n t -> p g (n t)").bitcast(F32)
-            copy_words(engine, ("w1", a), dst.rearrange("p g (n u) -> p g n u", u=2))
+            copy_words(engine, ("w1", a), dst.rearrange("p g (c i u) -> p g c u i", u=2, i=2))
 
         def quant_w1(pair, g):
             cols = slice(pair * 256, (pair + 1) * 256)
@@ -211,7 +208,8 @@ def tile_mybadtransfomerblock_pa_kernel(tc, x, pos_emb, enc_w0, enc_w1_bytes, en
         def relu_h(i, h, engine):
             if h == 0:
                 ht[i] = work.tile([P, 2, P, 4], BF16, tag="ht", name="ht", align_bytes=64, bufs=5)
-            relu(engine, ht[i][:, h], take_bank(("h", i, h))[:].rearrange("p (t n) -> p n t", t=4))
+            src = take_bank(("h", i, h))[:].rearrange("p (t c i) -> p c t i", t=4, i=2)
+            relu(engine, ht[i][:, h].rearrange("p (c i) t -> p c t i", i=2), src)
 
         def quant_h(i):
             h_codes[i] = work.tile([P, 256], U32, tag="h_codes", name="h_codes", align_bytes=64, bufs=12)
@@ -312,6 +310,7 @@ def tile_mybadtransfomerblock_pa_kernel(tc, x, pos_emb, enc_w0, enc_w1_bytes, en
         spread_scale(0)
         spread_scale(1)
         copy_scale(0, "v")
+        sort_w0(0)
         copy_scale(1, "s")
         transpose_w0(0)
         copy_w0(0, "s")
@@ -350,7 +349,9 @@ def tile_mybadtransfomerblock_pa_kernel(tc, x, pos_emb, enc_w0, enc_w1_bytes, en
         stage1_chunk(1, 2)
         stage1_chunk(0, 3)
         stage1_chunk(1, 3)
+        sort_w0(4)
         quant_y(2)
+        sort_w0(5)
         scale_w1(2)
         transpose_w0(4)
         transpose_y(3)
@@ -358,6 +359,8 @@ def tile_mybadtransfomerblock_pa_kernel(tc, x, pos_emb, enc_w0, enc_w1_bytes, en
         relu_h(1, 0, "s")
         copy_w0(4, "s")
         copy_y(3, "s")
+        sort_w0(6)
+        sort_w0(7)
         stage1(2, 0)
         transpose_w0(5)
         transpose_w1(0)

@@ -21,8 +21,10 @@ ACT = mybir.ActivationFunctionType
 P = 128
 PASSES = 2
 TILES = B * S // P
+PAIRS = TILES // B
 CHUNKS = D // P
 BANKS = 8
+RUN = 2
 
 
 def tile_mybadtransfomerblock_pa_kernel(tc, x, pos_emb, enc_w0, enc_w1_bytes, enc_w1_scale, out):
@@ -42,7 +44,7 @@ def tile_mybadtransfomerblock_pa_kernel(tc, x, pos_emb, enc_w0, enc_w1_bytes, en
 
         x_in, pos_in, w0_in, w1_in, yp, yt, y_codes, y_scales = {}, {}, {}, {}, {}, {}, {}, {}
         ht, h_codes, h_scales, bank, res, sums, inv = {}, {}, {}, {}, {}, {}, {}
-        w1_prod, w0_grouped, w1_grouped, w0_sorted = {}, {}, {}, {}
+        w1_prod, w0_grouped, w1_grouped = {}, {}, {}
         free_banks = list(range(BANKS))
         bank_number = {}
 
@@ -56,10 +58,12 @@ def tile_mybadtransfomerblock_pa_kernel(tc, x, pos_emb, enc_w0, enc_w1_bytes, en
         def load_scale():
             nc.sync.dma_start(out=scale_cols[:], in_=enc_w1_scale.rearrange("o (p j) -> p (o j)", p=P))
 
-        def load_x(i):
-            x_in[i] = work.tile([P, D], BF16, tag="x_in", bufs=TILES, name="x_in")
-            s0 = (i // 2) * P
-            nc.sync.dma_start(out=x_in[i][:], in_=x[i % 2, s0 : s0 + P, :])
+        def load_x(p, b=None):
+            if p not in x_in:
+                x_in[p] = work.tile([P, B, D], BF16, tag="x_in", bufs=PAIRS, name="x_in")
+            rows = x[:, p * P : (p + 1) * P, :].rearrange("b s k -> s b k")
+            part = slice(0, B) if b is None else slice(b, b + 1)
+            nc.sync.dma_start(out=x_in[p][:, part], in_=rows[:, part])
 
         def load_pos(j):
             pos_in[j] = work.tile([P, D], BF16, tag="pos_in", bufs=8, name="pos_in")
@@ -98,16 +102,11 @@ def tile_mybadtransfomerblock_pa_kernel(tc, x, pos_emb, enc_w0, enc_w1_bytes, en
             else:
                 nc.vector.tensor_copy(out=dst, in_=src)
 
-        def transpose_words(key, words, stepped):
-            b = new_bank(key)
-            v = b[:].rearrange("p (u g n) -> p g u n", g=2, u=2)
+        def transpose_words(key, source):
+            v = new_bank(key)[:].rearrange("p (u g n) -> p g u n", g=2, u=2)
             for g in range(2):
                 for u in range(2):
-                    if stepped:
-                        src = words[:, 256 * g + u : 256 * (g + 1) : 2]
-                    else:
-                        src = words[:, 256 * u + 128 * g : 256 * u + 128 * (g + 1)]
-                    nc.tensor.transpose(v[:, g, u, :], src, ident[:])
+                    nc.tensor.transpose(v[:, g, u, :], source(g, u), ident[:])
 
         def copy_words(engine, key, dst):
             src = take_bank(key)[:].rearrange("p (u g c i) -> p g c u i", g=2, u=2, i=2)
@@ -116,55 +115,66 @@ def tile_mybadtransfomerblock_pa_kernel(tc, x, pos_emb, enc_w0, enc_w1_bytes, en
             else:
                 nc.vector.tensor_copy(out=dst, in_=src)
 
-        def add_pos(i):
-            yp[i] = work.tile([P, D], BF16, tag="yp", name="yp", bufs=4)
-            pairs = "p (w u e) -> p w u e"
+        def add_pos(p, b=None):
+            if p not in yp:
+                yp[p] = work.tile([P, 2, B, D // 2], BF16, tag="yp", name="yp")
+            part = slice(0, B) if b is None else slice(b, b + 1)
+            count = B if b is None else 1
+            runs = "p b (w u e) -> p b w u e"
             nc.vector.tensor_tensor(
-                out=yp[i][:].rearrange("p (u w e) -> p w u e", u=2, e=16),
-                in0=x_in.pop(i)[:].rearrange(pairs, u=2, e=16),
-                in1=pos_in[i // 2][:].rearrange(pairs, u=2, e=16),
+                out=yp[p][:, :, part].rearrange("p u b (w e) -> p b w u e", e=RUN),
+                in0=x_in[p][:, part].rearrange(runs, u=2, e=RUN),
+                in1=pos_in[p][:].unsqueeze(1).to_broadcast([P, count, D]).rearrange(runs, u=2, e=RUN),
                 op=ADD,
             )
 
         def transpose_y(i):
-            transpose_words(("y", i), yp.pop(i)[:].bitcast(F32), False)
+            words = yp[i // B][:, :, i % B].bitcast(F32)
+            transpose_words(("y", i), lambda g, u: words[:, u, g * P : (g + 1) * P])
 
         def copy_y(i, engine):
-            yt[i] = work.tile([P, D], BF16, tag="yt", name="yt", align_bytes=64, bufs=4)
-            copy_words(engine, ("y", i), yt[i][:].bitcast(F32).rearrange("p (g c i u) -> p g c u i", g=2, u=2, i=2))
+            if i // B not in yt:
+                yt[i // B] = work.tile([P, B, D], BF16, tag="yt", name="yt", align_bytes=64)
+            dst = yt[i // B][:, i % B].bitcast(F32)
+            copy_words(engine, ("y", i), dst.rearrange("p (g c i u) -> p g c u i", g=2, u=2, i=2))
 
-        def quant_y(i):
-            y_codes[i] = work.tile([P, 256], U32, tag="y_codes", name="y_codes", align_bytes=64, bufs=6)
-            y_scales[i] = work.tile([P, 256], U8, tag="y_scales", name="y_scales", align_bytes=64, bufs=6)
-            nc.vector.quantize_mx(out=y_codes[i][:].bitcast(FP8X4), scales=y_scales[i][:], in_=yt.pop(i)[:])
-
-        def sort_w0(c):
-            w0_sorted[c] = work.tile([P, D], BF16, tag="w0_sorted", name="w0_sorted", bufs=4)
-            nc.vector.tensor_copy(
-                out=w0_sorted[c][:].rearrange("p (u w e) -> p w u e", u=2, e=16),
-                in_=w0_in.pop(c)[:].rearrange("p (w u e) -> p w u e", u=2, e=16),
+        def quant_y(p, b=None):
+            if p not in y_codes:
+                y_codes[p] = work.tile([P, B, 256], U32, tag="y_codes", name="y_codes", align_bytes=64, bufs=4)
+                y_scales[p] = work.tile([P, B, 256], U8, tag="y_scales", name="y_scales", align_bytes=64, bufs=4)
+            part = slice(0, B) if b is None else slice(b, b + 1)
+            flat = "p b n -> p (b n)"
+            nc.vector.quantize_mx(
+                out=y_codes[p][:, part].rearrange(flat).bitcast(FP8X4),
+                scales=y_scales[p][:, part].rearrange(flat),
+                in_=yt[p][:, part].rearrange(flat),
             )
 
         def transpose_w0(c):
-            transpose_words(("w0", c), w0_sorted.pop(c)[:].bitcast(F32), False)
+            words = w0_in.pop(c)[:].bitcast(F32)
+            transpose_words(("w0", c), lambda g, u: words[:, 256 * g + u : 256 * (g + 1) : 2])
 
         def copy_w0(c, engine):
-            w0_grouped[c] = work.tile([P, D], BF16, tag="w0_grouped", name="w0_grouped", align_bytes=64)
-            copy_words(engine, ("w0", c), w0_grouped[c][:].bitcast(F32).rearrange("p (g c i u) -> p g c u i", g=2, u=2, i=2))
+            if c // 2 not in w0_grouped:
+                w0_grouped[c // 2] = work.tile([P, 2, D], BF16, tag="w0_grouped", name="w0_grouped", align_bytes=64, bufs=2)
+            dst = w0_grouped[c // 2][:, c % 2].bitcast(F32)
+            copy_words(engine, ("w0", c), dst.rearrange("p (g c i u) -> p g c u i", g=2, u=2, i=2))
 
-        def quant_w0(c):
+        def quant_w0(q, c=None):
+            part = slice(0, 2) if c is None else slice(c, c + 1)
             nc.vector.quantize_mx(
-                out=w0_codes[:, c].rearrange("p g m -> p (g m)").bitcast(FP8X4),
-                scales=w0_scales[:, c].rearrange("p g m -> p (g m)"),
-                in_=w0_grouped.pop(c)[:],
+                out=w0_codes[:, 2 * q : 2 * q + 2][:, part].rearrange("p c g m -> p (c g m)").bitcast(FP8X4),
+                scales=w0_scales[:, 2 * q : 2 * q + 2][:, part].rearrange("p c g m -> p (c g m)"),
+                in_=w0_grouped[q][:, part].rearrange("p c n -> p (c n)"),
             )
 
         def scale_w1(a):
-            w1_prod[a] = work.tile([P, D], BF16, tag="w1_prod", name="w1_prod", bufs=4)
+            w1_prod[a] = work.tile([P, D], BF16, tag="w1_prod", name="w1_prod", bufs=3)
             nc.vector.tensor_tensor(out=w1_prod[a][:], in0=w1_in.pop(a)[:].bitcast(FP8), in1=w1_scale[:], op=MULT)
 
         def transpose_w1(a):
-            transpose_words(("w1", a), w1_prod.pop(a)[:].bitcast(F32), True)
+            words = w1_prod.pop(a)[:].bitcast(F32)
+            transpose_words(("w1", a), lambda g, u: words[:, 256 * g + u : 256 * (g + 1) : 2])
 
         def copy_w1(a, engine):
             if a % 2 == 0:
@@ -189,8 +199,8 @@ def tile_mybadtransfomerblock_pa_kernel(tc, x, pos_emb, enc_w0, enc_w1_bytes, en
                     out=b[:, t * P : (t + 1) * P],
                     lhsT=w0_codes[:, c, g, :].bitcast(FP8X4),
                     lhsT_scale=w0_scales[:, c, g, :],
-                    rhs=y_codes[i][:, g * P : (g + 1) * P].bitcast(FP8X4),
-                    rhs_scale=y_scales[i][:, g * P : (g + 1) * P],
+                    rhs=y_codes[i // B][:, i % B, g * P : (g + 1) * P].bitcast(FP8X4),
+                    rhs_scale=y_scales[i // B][:, i % B, g * P : (g + 1) * P],
                     start=(g == 0),
                     stop=(g == PASSES - 1),
                 )
@@ -206,22 +216,24 @@ def tile_mybadtransfomerblock_pa_kernel(tc, x, pos_emb, enc_w0, enc_w1_bytes, en
                 nc.vector.tensor_scalar(out=dst, in0=src, scalar1=0.0, scalar2=None, op0=MAX)
 
         def relu_h(i, h, engine):
-            if h == 0:
-                ht[i] = work.tile([P, 2, P, 4], BF16, tag="ht", name="ht", align_bytes=64, bufs=5)
+            if i // B not in ht:
+                ht[i // B] = work.tile([P, B, 2, P, 4], BF16, tag="ht", name="ht", align_bytes=64)
             src = take_bank(("h", i, h))[:].rearrange("p (t c i) -> p c t i", t=4, i=2)
-            relu(engine, ht[i][:, h].rearrange("p (c i) t -> p c t i", i=2), src)
+            relu(engine, ht[i // B][:, i % B, h].rearrange("p (c i) t -> p c t i", i=2), src)
 
-        def quant_h(i):
-            h_codes[i] = work.tile([P, 256], U32, tag="h_codes", name="h_codes", align_bytes=64, bufs=12)
-            h_scales[i] = work.tile([P, 256], U8, tag="h_scales", name="h_scales", align_bytes=64, bufs=12)
+        def quant_h(p, b=None):
+            if p not in h_codes:
+                h_codes[p] = work.tile([P, B, 256], U32, tag="h_codes", name="h_codes", align_bytes=64, bufs=PAIRS)
+                h_scales[p] = work.tile([P, B, 256], U8, tag="h_scales", name="h_scales", align_bytes=64, bufs=PAIRS)
+            part = slice(0, B) if b is None else slice(b, b + 1)
             nc.vector.quantize_mx(
-                out=h_codes[i][:].bitcast(FP8X4),
-                scales=h_scales[i][:],
-                in_=ht.pop(i)[:].rearrange("p h n t -> p (h n t)"),
+                out=h_codes[p][:, part].rearrange("p b n -> p (b n)").bitcast(FP8X4),
+                scales=h_scales[p][:, part].rearrange("p b n -> p (b n)"),
+                in_=ht[p][:, part].rearrange("p b h n t -> p (b h n t)"),
             )
 
         def stage2(i, n):
-            hc, hs = h_codes[i], h_scales[i]
+            hc, hs = h_codes[i // B][:, i % B], h_scales[i // B][:, i % B]
             b = new_bank(("o", i, n))
             for h in range(2):
                 nc.tensor.matmul_mx(
@@ -239,10 +251,13 @@ def tile_mybadtransfomerblock_pa_kernel(tc, x, pos_emb, enc_w0, enc_w1_bytes, en
                 res[i] = work.tile([P, D], F32, tag="res", name="res", bufs=10)
             relu(engine, res[i][:, n * 512 : (n + 1) * 512], take_bank(("o", i, n))[:])
 
-        def squares(i, cols, engine, slot):
-            if i // 2 not in sums:
-                sums[i // 2] = work.tile([P, 4], F32, tag="sums", name="sums", bufs=4)
-            acc = sums[i // 2][:, slot : slot + 1]
+        def squares(i, engine, half=None):
+            group, place = GROUP[i]
+            if group not in sums:
+                sums[group] = work.tile([P, 4], F32, tag="sums", name="sums", bufs=4)
+            cols = slice(0, D) if half is None else slice(half * 512, (half + 1) * 512)
+            slot = place + 2 * (half or 0)
+            acc = sums[group][:, slot : slot + 1]
             part = res[i][:, cols]
             if engine == "s":
                 junk_s = work.tile([P, D], BF16, tag="junk_s", name="junk_s", bufs=2)
@@ -254,19 +269,22 @@ def tile_mybadtransfomerblock_pa_kernel(tc, x, pos_emb, enc_w0, enc_w1_bytes, en
                 )
 
         def root(f):
-            inv[f] = work.tile([P, 2], F32, tag="inv", name="inv", bufs=4)
-            nc.scalar.activation(out=inv[f][:], in_=sums[f][:, 0:2], func=ACT.Sqrt)
+            inv[f] = work.tile([P, len(GROUPS[f])], F32, tag="inv", name="inv", bufs=4)
+            nc.scalar.activation(out=inv[f][:], in_=sums[f][:, 0 : len(GROUPS[f])], func=ACT.Sqrt)
 
         def root_of_halves(i):
-            f, e = divmod(i, 2)
-            if e == 0:
-                inv[f] = work.tile([P, 2], F32, tag="inv", name="inv", bufs=4)
+            f, e = GROUP[i]
+            if f not in inv:
+                inv[f] = work.tile([P, len(GROUPS[f])], F32, tag="inv", name="inv", bufs=4)
             nc.scalar.activation(
                 out=inv[f][:, e : e + 1], in_=sums[f][:, e : e + 1], func=ACT.Sqrt, bias=sums[f][:, 2 + e : 3 + e]
             )
 
-        def add_eps(f):
-            nc.vector.tensor_scalar(out=inv[f][:], in0=inv[f][:], scalar1=EPS, scalar2=None, op0=ADD)
+        def add_eps(f, engine):
+            if engine == "s":
+                nc.scalar.activation(out=inv[f][:], in_=inv[f][:], func=ACT.Copy, bias=EPS)
+            else:
+                nc.vector.tensor_scalar(out=inv[f][:], in0=inv[f][:], scalar1=EPS, scalar2=None, op0=ADD)
 
         def reciprocal(f):
             nc.vector.reciprocal(out=inv[f][:], in_=inv[f][:])
@@ -274,242 +292,348 @@ def tile_mybadtransfomerblock_pa_kernel(tc, x, pos_emb, enc_w0, enc_w1_bytes, en
         def scale_out(i, n, engine):
             cols = slice(0, D) if n is None else slice(n * 512, (n + 1) * 512)
             r = res[i][:, cols]
+            factor = inv[GROUP[i][0]][:, GROUP[i][1] : GROUP[i][1] + 1]
             if engine == "v":
-                nc.vector.tensor_scalar(out=r, in0=r, scalar1=inv[i // 2][:, i % 2 : i % 2 + 1], scalar2=None, op0=MULT)
+                nc.vector.tensor_scalar(out=r, in0=r, scalar1=factor, scalar2=None, op0=MULT)
             elif engine == "g":
-                nc.gpsimd.tensor_scalar(out=r, in0=r, scalar1=inv[i // 2][:, i % 2 : i % 2 + 1], scalar2=0.0, op0=MULT, op1=ADD)
+                nc.gpsimd.tensor_scalar(out=r, in0=r, scalar1=factor, scalar2=0.0, op0=MULT, op1=ADD)
             else:
-                nc.scalar.activation(out=r, in_=r, func=ACT.Copy, scale=inv[i // 2][:, i % 2 : i % 2 + 1])
+                nc.scalar.activation(out=r, in_=r, func=ACT.Copy, scale=factor)
             s0 = (i // 2) * P
             nc.sync.dma_start(out=out[i % 2, s0 : s0 + P, cols], in_=r)
 
+        GROUPS = [(0, 1, 2), (3, 4, 5), (6, 7, 8), (9, 10), (11, 12), (13,), (14,), (15,)]
+        GROUP = {i: (f, e) for f, tiles in enumerate(GROUPS) for e, i in enumerate(tiles)}
         load_scale()
-        load_w0(0)
-        load_x(0)
+        load_x(0, 0)
         load_pos(0)
-        load_w0(1)
         load_w1(0)
-        load_x(1)
+        load_w0(0)
+        load_w0(1)
+        load_x(0, 1)
+        load_w1(1)
         load_w0(2)
         load_w0(3)
-        load_w1(1)
-        load_x(2)
-        load_pos(1)
-        load_x(3)
         load_w0(4)
         load_w0(5)
         load_w1(2)
+        load_x(1)
+        load_pos(1)
         load_w0(6)
         load_w0(7)
-        for i in range(4, TILES):
-            if i - 4 + 3 < CHUNKS:
-                load_w1(i - 4 + 3)
-            load_x(i)
-            if i % 2 == 0:
-                load_pos(i // 2)
+        load_w1(3)
+        load_w1(4)
+        load_x(2)
+        load_pos(2)
+        load_w1(5)
+        load_w1(6)
+        load_w1(7)
+        load_x(3)
+        load_pos(3)
+        load_x(4)
+        load_pos(4)
+        load_x(5)
+        load_pos(5)
+        load_x(6)
+        load_pos(6)
+        load_x(7)
+        load_pos(7)
         spread_scale(0)
         spread_scale(1)
         copy_scale(0, "v")
-        sort_w0(0)
         copy_scale(1, "s")
+        add_pos(0, 0)
+        scale_w1(0)
+        transpose_y(0)
+        copy_y(0, "s")
         transpose_w0(0)
         copy_w0(0, "s")
-        add_pos(0)
-        sort_w0(1)
-        transpose_y(0)
         transpose_w0(1)
-        copy_y(0, "s")
         copy_w0(1, "s")
-        scale_w1(0)
-        sort_w0(2)
-        add_pos(1)
-        sort_w0(3)
-        quant_w0(0)
+        add_pos(0, 1)
+        transpose_w1(0)
+        copy_w1(0, "s")
+        scale_w1(1)
         transpose_w0(2)
         copy_w0(2, "s")
         transpose_y(1)
         copy_y(1, "s")
         transpose_w0(3)
         copy_w0(3, "s")
+        quant_w0(0)
         quant_y(0)
+        transpose_w0(4)
+        copy_w0(4, "s")
         quant_w0(1)
-        add_pos(2)
+        transpose_w1(1)
+        copy_w1(1, "s")
+        scale_w1(2)
+        transpose_w0(5)
+        copy_w0(5, "s")
+        stage1(0, 0)
+        stage1(1, 0)
+        add_pos(1)
+        relu_h(0, 0, "s")
+        transpose_w0(6)
+        copy_w0(6, "s")
+        relu_h(1, 0, "s")
+        transpose_w0(7)
+        copy_w0(7, "s")
         quant_w0(2)
-        quant_y(1)
+        scale_w1(3)
         transpose_y(2)
         copy_y(2, "s")
-        quant_w0(3)
-        add_pos(3)
-        scale_w1(1)
-        stage1_chunk(0, 0)
-        stage1_chunk(1, 0)
-        stage1_chunk(0, 1)
-        stage1_chunk(1, 1)
-        stage1_chunk(0, 2)
-        stage1_chunk(1, 2)
-        stage1_chunk(0, 3)
-        stage1_chunk(1, 3)
-        sort_w0(4)
-        quant_y(2)
-        sort_w0(5)
-        scale_w1(2)
-        transpose_w0(4)
         transpose_y(3)
-        relu_h(0, 0, "s")
-        relu_h(1, 0, "s")
-        copy_w0(4, "s")
         copy_y(3, "s")
-        sort_w0(6)
-        sort_w0(7)
-        stage1(2, 0)
-        transpose_w0(5)
-        transpose_w1(0)
-        quant_w0(4)
-        quant_y(3)
-        relu_h(2, 0, "v")
-        copy_w0(5, "s")
-        copy_w1(0, "s")
-        add_pos(4)
-        stage1(3, 0)
-        transpose_w0(6)
-        transpose_w0(7)
-        quant_w0(5)
-        relu_h(3, 0, "s")
-        copy_w0(6, "s")
-        copy_w0(7, "v")
-        stage1_chunk(0, 4)
-        stage1_chunk(1, 4)
-        stage1_chunk(0, 5)
-        stage1_chunk(1, 5)
-        transpose_y(4)
-        transpose_w1(1)
-        quant_w0(6)
-        quant_w0(7)
-        copy_y(4, "s")
-        copy_w1(1, "s")
-        add_pos(5)
-        stage1_chunk(0, 6)
-        stage1_chunk(1, 6)
-        stage1_chunk(0, 7)
-        stage1_chunk(1, 7)
-        stage1(2, 1)
-        transpose_y(5)
-        transpose_w1(2)
-        relu_h(0, 1, "s")
-        relu_h(1, 1, "s")
-        scale_w1(3)
-        quant_y(4)
-        stage1(3, 1)
-        relu_h(2, 1, "s")
-        copy_y(5, "s")
-        copy_w1(2, "s")
-        relu_h(3, 1, "s")
+        quant_w0(3)
         quant_w1(0, 0)
         quant_w1(0, 1)
+        transpose_w1(2)
+        copy_w1(2, "s")
+        stage1(0, 1)
+        relu_h(0, 1, "s")
+        add_pos(2)
+        stage1(1, 1)
+        relu_h(1, 1, "s")
+        quant_y(1)
+        transpose_w1(3)
+        copy_w1(3, "s")
+        stage1(2, 0)
+        relu_h(2, 0, "s")
+        scale_w1(4)
+        stage1(2, 1)
+        relu_h(2, 1, "s")
+        transpose_y(4)
+        copy_y(4, "s")
+        transpose_y(5)
+        copy_y(5, "s")
+        quant_h(0)
+        scale_w1(5)
+        stage1(3, 0)
+        relu_h(3, 0, "s")
+        stage1(3, 1)
+        relu_h(3, 1, "s")
+        quant_w1(1, 0)
+        quant_w1(1, 1)
+        add_pos(3)
+        quant_y(2)
+        transpose_w1(4)
+        copy_w1(4, "s")
+        transpose_w1(5)
+        copy_w1(5, "s")
+        stage1(4, 0)
+        relu_h(4, 0, "s")
+        scale_w1(6)
+        stage1(4, 1)
+        relu_h(4, 1, "s")
+        quant_h(1)
+        transpose_y(6)
+        copy_y(6, "s")
+        transpose_y(7)
+        copy_y(7, "s")
+        scale_w1(7)
+        stage2(0, 0)
+        relu_out(0, 0, "s")
+        stage1(5, 0)
+        relu_h(5, 0, "s")
+        stage1(5, 1)
+        relu_h(5, 1, "s")
+        quant_w1(2, 0)
+        quant_w1(2, 1)
+        quant_y(3)
+        add_pos(4)
+        stage2(1, 0)
+        relu_out(1, 0, "s")
+        transpose_w1(6)
+        copy_w1(6, "s")
+        transpose_w1(7)
+        copy_w1(7, "s")
+        stage1(6, 0)
+        relu_h(6, 0, "s")
+        stage1(6, 1)
+        relu_h(6, 1, "s")
+        quant_h(2)
+        transpose_y(8)
+        copy_y(8, "s")
+        transpose_y(9)
+        copy_y(9, "s")
+        add_pos(5)
+        quant_w1(3, 0)
+        quant_w1(3, 1)
+        stage2(2, 0)
+        relu_out(2, 0, "s")
+        stage1(7, 0)
+        relu_h(7, 0, "s")
+        stage1(7, 1)
+        relu_h(7, 1, "v")
+        stage2(3, 0)
+        relu_out(3, 0, "v")
+        quant_y(4)
+        transpose_y(10)
+        copy_y(10, "s")
+        transpose_y(11)
+        copy_y(11, "s")
+        quant_h(3)
+        stage2(0, 1)
+        relu_out(0, 1, "s")
         add_pos(6)
-        W1_TURN = {4: 3, 5: 4, 6: 5, 7: 6, 8: 7}
-        EARLY = {6: 0, 7: 1, 8: 2, 9: 3}
-        FIRST = 10
-        ALL = slice(0, D)
-        for s in range(4, FIRST):
-            turns = [(transpose_y, copy_y, (s + 2,))]
-            if s in W1_TURN:
-                turns.append((transpose_w1, copy_w1, (W1_TURN[s],)))
-            products = [(stage1, relu_h, (s, h)) for h in range(2)]
-            if s in EARLY:
-                products.append((stage2, relu_out, (EARLY[s], 0)))
-            add_pos(s + 3)
-            quant_y(s + 1)
-            if s + 1 in W1_TURN:
-                scale_w1(W1_TURN[s + 1])
-            for i in range(0, s) if s == 4 else (s - 1,):
-                quant_h(i)
-            if s - 1 in W1_TURN and W1_TURN[s - 1] % 2 == 1:
-                quant_w1(W1_TURN[s - 1] // 2, 0)
-                quant_w1(W1_TURN[s - 1] // 2, 1)
-            jobs = turns + products
-            for n, (fill, empty, args) in enumerate(jobs):
-                fill(*args)
-                empty(*args, "v" if s + 1 not in W1_TURN and n == 1 else "s")
-
-        PAIRS = TILES // 2
-
-        def turns_of(s):
-            return [i for i in (s + 2, s + 3) if i < TILES and (s - FIRST) % 2 == 0]
-
-        def adds(s):
-            return [i for i in (s + 3, s + 4) if (s - FIRST) % 2 == 1 and i in x_in]
-
-        add_pos(FIRST + 3)
-
-        for f in range(PAIRS - 1):
-            s = FIRST + f
-            a, b = 2 * f, 2 * f + 1
-            early = a in EARLY.values()
-            if not early:
-                stage2(a, 0)
-                relu_out(a, 0, "v")
-            if s == TILES:
-                quant_h(s - 1)
-            stage2(a, 1)
-            relu_out(a, 1, "s" if s < TILES else "v")
-            if f > 0:
-                root(f - 1)
-            if not early:
-                stage2(b, 0)
-                relu_out(b, 0, "v")
-            stage2(b, 1)
-            relu_out(b, 1, "v" if early else "s")
-            if f > 0:
-                add_eps(f - 1)
-            if s < TILES:
-                quant_h(s - 1)
-            for i in adds(s):
-                add_pos(i)
-            if f > 0:
-                reciprocal(f - 1)
-            if s < TILES:
-                stage1(s, 0)
-                relu_h(s, 0, "s")
-            squares(a, ALL, "s", 0)
-            if s + 1 < TILES:
-                quant_y(s + 1)
-            if f > 0:
-                scale_out(a - 2, None, "v")
-                scale_out(a - 1, None, "v")
-            if s < TILES:
-                stage1(s, 1)
-                relu_h(s, 1, "v")
-            for i in turns_of(s):
-                transpose_y(i)
-                copy_y(i, "v" if early or i % 2 == 1 else "s")
-            squares(b, ALL, "s", 1)
-        f = PAIRS - 1
-        a, b = 2 * f, 2 * f + 1
-        LOW, HIGH = slice(0, 512), slice(512, D)
-        stage2(a, 0)
-        relu_out(a, 0, "v")
-        root(f - 1)
-        stage2(a, 1)
-        relu_out(a, 1, "s")
-        add_eps(f - 1)
-        stage2(b, 0)
-        relu_out(b, 0, "v")
-        reciprocal(f - 1)
-        stage2(b, 1)
-        relu_out(b, 1, "s")
-        squares(a, HIGH, "v", 2)
-        squares(a, LOW, "s", 0)
-        scale_out(a - 2, None, "v")
-        squares(b, LOW, "s", 1)
-        squares(b, HIGH, "v", 3)
-        root_of_halves(a)
-        scale_out(a - 1, 0, "s")
-        scale_out(a - 1, 1, "v")
-        root_of_halves(b)
-        add_eps(f)
-        reciprocal(f)
-        scale_out(a, 0, "v")
-        scale_out(b, 0, "s")
-        scale_out(a, 1, "v")
-        scale_out(b, 1, "v")
+        stage2(1, 1)
+        relu_out(1, 1, "s")
+        stage2(2, 1)
+        relu_out(2, 1, "v")
+        squares(0, "s")
+        stage2(3, 1)
+        relu_out(3, 1, "v")
+        stage2(4, 0)
+        relu_out(4, 0, "v")
+        squares(1, "s")
+        stage2(4, 1)
+        relu_out(4, 1, "v")
+        stage1(8, 0)
+        relu_h(8, 0, "v")
+        squares(2, "s")
+        stage1(8, 1)
+        relu_h(8, 1, "v")
+        stage1(9, 0)
+        relu_h(9, 0, "v")
+        stage1(9, 1)
+        relu_h(9, 1, "s")
+        quant_y(5)
+        transpose_y(12)
+        copy_y(12, "s")
+        root(0)
+        transpose_y(13)
+        copy_y(13, "s")
+        quant_h(4)
+        add_eps(0, "s")
+        stage2(5, 0)
+        relu_out(5, 0, "s")
+        add_pos(7)
+        stage2(5, 1)
+        relu_out(5, 1, "s")
+        reciprocal(0)
+        scale_out(0, None, "g")
+        scale_out(1, None, "g")
+        scale_out(2, None, "g")
+        stage2(6, 0)
+        relu_out(6, 0, "s")
+        stage2(6, 1)
+        relu_out(6, 1, "v")
+        squares(3, "s")
+        stage2(7, 0)
+        relu_out(7, 0, "v")
+        stage2(7, 1)
+        relu_out(7, 1, "v")
+        squares(4, "s")
+        stage1(10, 0)
+        relu_h(10, 0, "v")
+        stage1(10, 1)
+        relu_h(10, 1, "v")
+        squares(5, "s")
+        stage1(11, 0)
+        relu_h(11, 0, "v")
+        stage1(11, 1)
+        relu_h(11, 1, "v")
+        quant_y(6)
+        transpose_y(14)
+        copy_y(14, "s")
+        root(1)
+        transpose_y(15)
+        copy_y(15, "s")
+        quant_h(5)
+        add_eps(1, "s")
+        stage2(8, 0)
+        relu_out(8, 0, "s")
+        quant_y(7)
+        reciprocal(1)
+        scale_out(3, None, "g")
+        scale_out(4, None, "g")
+        scale_out(5, None, "g")
+        stage2(8, 1)
+        relu_out(8, 1, "v")
+        stage2(9, 0)
+        relu_out(9, 0, "s")
+        stage2(9, 1)
+        relu_out(9, 1, "v")
+        squares(6, "s")
+        stage1(12, 0)
+        relu_h(12, 0, "v")
+        stage1(12, 1)
+        relu_h(12, 1, "v")
+        squares(7, "s")
+        stage1(13, 0)
+        relu_h(13, 0, "v")
+        stage1(13, 1)
+        relu_h(13, 1, "v")
+        squares(8, "s")
+        stage1(14, 0)
+        relu_h(14, 0, "v")
+        stage1(14, 1)
+        relu_h(14, 1, "v")
+        stage1(15, 0)
+        relu_h(15, 0, "s")
+        root(2)
+        quant_h(6)
+        stage1(15, 1)
+        relu_h(15, 1, "s")
+        add_eps(2, "s")
+        stage2(10, 0)
+        relu_out(10, 0, "s")
+        quant_h(7)
+        reciprocal(2)
+        scale_out(6, None, "g")
+        scale_out(7, None, "g")
+        scale_out(8, None, "g")
+        stage2(10, 1)
+        relu_out(10, 1, "v")
+        squares(9, "s")
+        stage2(11, 0)
+        relu_out(11, 0, "v")
+        stage2(11, 1)
+        relu_out(11, 1, "v")
+        squares(10, "s")
+        stage2(12, 0)
+        relu_out(12, 0, "v")
+        stage2(12, 1)
+        relu_out(12, 1, "v")
+        squares(11, "s")
+        root(3)
+        stage2(13, 0)
+        relu_out(13, 0, "v")
+        squares(12, "s")
+        add_eps(3, "s")
+        stage2(13, 1)
+        relu_out(13, 1, "v")
+        reciprocal(3)
+        scale_out(9, None, "g")
+        scale_out(10, None, "g")
+        stage2(14, 0)
+        relu_out(14, 0, "v")
+        root(4)
+        squares(13, "s")
+        add_eps(4, "s")
+        stage2(14, 1)
+        relu_out(14, 1, "v")
+        reciprocal(4)
+        stage2(15, 0)
+        relu_out(15, 0, "v")
+        stage2(15, 1)
+        relu_out(15, 1, "v")
+        root(5)
+        squares(14, "s")
+        add_eps(5, "s")
+        scale_out(11, None, "v")
+        scale_out(12, None, "v")
+        reciprocal(5)
+        squares(15, "s", 0)
+        root(6)
+        squares(15, "v", 1)
+        add_eps(6, "s")
+        scale_out(13, None, "v")
+        root_of_halves(15)
+        reciprocal(6)
+        add_eps(7, "v")
+        scale_out(14, None, "v")
+        reciprocal(7)
+        scale_out(15, 0, "s")
+        scale_out(15, 1, "v")

@@ -117,7 +117,7 @@ def tile_mybadtransfomerblock_pa_kernel(tc, x, pos_emb, enc_w0, enc_w1_bytes, en
 
         def add_pos(p, b=None):
             if p not in yp:
-                yp[p] = work.tile([P, 2, B, D // 2], BF16, tag="yp", name="yp")
+                yp[p] = work.tile([P, 2, B, D // 2], BF16, tag="yp", name="yp", bufs=3)
             part = slice(0, B) if b is None else slice(b, b + 1)
             count = B if b is None else 1
             runs = "p b (w u e) -> p b w u e"
@@ -134,7 +134,7 @@ def tile_mybadtransfomerblock_pa_kernel(tc, x, pos_emb, enc_w0, enc_w1_bytes, en
 
         def copy_y(i, engine):
             if i // B not in yt:
-                yt[i // B] = work.tile([P, B, D], BF16, tag="yt", name="yt", align_bytes=64)
+                yt[i // B] = work.tile([P, B, D], BF16, tag="yt", name="yt", align_bytes=64, bufs=3)
             dst = yt[i // B][:, i % B].bitcast(F32)
             copy_words(engine, ("y", i), dst.rearrange("p (g c i u) -> p g c u i", g=2, u=2, i=2))
 
@@ -156,7 +156,7 @@ def tile_mybadtransfomerblock_pa_kernel(tc, x, pos_emb, enc_w0, enc_w1_bytes, en
 
         def copy_w0(c, engine):
             if c // 2 not in w0_grouped:
-                w0_grouped[c // 2] = work.tile([P, 2, D], BF16, tag="w0_grouped", name="w0_grouped", align_bytes=64, bufs=2)
+                w0_grouped[c // 2] = work.tile([P, 2, D], BF16, tag="w0_grouped", name="w0_grouped", align_bytes=64, bufs=3)
             dst = w0_grouped[c // 2][:, c % 2].bitcast(F32)
             copy_words(engine, ("w0", c), dst.rearrange("p (g c i u) -> p g c u i", g=2, u=2, i=2))
 
@@ -178,7 +178,7 @@ def tile_mybadtransfomerblock_pa_kernel(tc, x, pos_emb, enc_w0, enc_w1_bytes, en
 
         def copy_w1(a, engine):
             if a % 2 == 0:
-                w1_grouped[a // 2] = work.tile([P, PASSES, 2 * P, 4], BF16, tag="w1_grouped", name="w1_grouped", align_bytes=64, bufs=2)
+                w1_grouped[a // 2] = work.tile([P, PASSES, 2 * P, 4], BF16, tag="w1_grouped", name="w1_grouped", align_bytes=64, bufs=3)
             rows = slice((a % 2) * P, (a % 2 + 1) * P)
             dst = w1_grouped[a // 2][:, :, rows, :].rearrange("p g n t -> p g (n t)").bitcast(F32)
             copy_words(engine, ("w1", a), dst.rearrange("p g (c i u) -> p g c u i", u=2, i=2))
@@ -217,7 +217,7 @@ def tile_mybadtransfomerblock_pa_kernel(tc, x, pos_emb, enc_w0, enc_w1_bytes, en
 
         def relu_h(i, h, engine):
             if i // B not in ht:
-                ht[i // B] = work.tile([P, B, 2, P, 4], BF16, tag="ht", name="ht", align_bytes=64)
+                ht[i // B] = work.tile([P, B, 2, P, 4], BF16, tag="ht", name="ht", align_bytes=64, bufs=4)
             src = take_bank(("h", i, h))[:].rearrange("p (t c i) -> p c t i", t=4, i=2)
             relu(engine, ht[i // B][:, i % B, h].rearrange("p (c i) t -> p c t i", i=2), src)
 
@@ -247,8 +247,8 @@ def tile_mybadtransfomerblock_pa_kernel(tc, x, pos_emb, enc_w0, enc_w1_bytes, en
                 )
 
         def relu_out(i, n, engine):
-            if n == 0:
-                res[i] = work.tile([P, D], F32, tag="res", name="res", bufs=10)
+            if i not in res:
+                res[i] = work.tile([P, D], F32, tag="res", name="res", bufs=8)
             relu(engine, res[i][:, n * 512 : (n + 1) * 512], take_bank(("o", i, n))[:])
 
         def squares(i, engine, half=None):
@@ -263,7 +263,7 @@ def tile_mybadtransfomerblock_pa_kernel(tc, x, pos_emb, enc_w0, enc_w1_bytes, en
                 junk_s = work.tile([P, D], BF16, tag="junk_s", name="junk_s", bufs=2)
                 nc.scalar.activation(out=junk_s[:, cols], in_=part, func=ACT.Square, accum_out=acc)
             else:
-                junk_v = work.tile([P, D], BF16, tag="junk_v", name="junk_v", bufs=2)
+                junk_v = work.tile([P, D], BF16, tag="junk_v", name="junk_v", bufs=1)
                 nc.vector.scalar_tensor_tensor(
                     out=junk_v[:, cols], in0=part, scalar=1.0, in1=part, op0=MULT, op1=MULT, accum_out=acc
                 )
@@ -302,34 +302,34 @@ def tile_mybadtransfomerblock_pa_kernel(tc, x, pos_emb, enc_w0, enc_w1_bytes, en
             s0 = (i // 2) * P
             nc.sync.dma_start(out=out[i % 2, s0 : s0 + P, cols], in_=r)
 
-        GROUPS = [(0, 1, 2), (3, 4, 5), (6, 7, 8), (9, 10), (11, 12), (13,), (14,), (15,)]
+        GROUPS = [(0, 1), (2, 3), (4, 5), (6, 7), (8, 9), (10, 11), (12, 13), (14,), (15,)]
         GROUP = {i: (f, e) for f, tiles in enumerate(GROUPS) for e, i in enumerate(tiles)}
         load_scale()
         load_x(0, 0)
         load_pos(0)
-        load_w1(0)
         load_w0(0)
-        load_w0(1)
         load_x(0, 1)
+        load_w1(0)
+        load_w0(1)
         load_w1(1)
         load_w0(2)
         load_w0(3)
+        load_w1(2)
         load_w0(4)
         load_w0(5)
-        load_w1(2)
-        load_x(1)
-        load_pos(1)
+        load_w1(3)
         load_w0(6)
         load_w0(7)
-        load_w1(3)
+        load_x(1)
+        load_pos(1)
         load_w1(4)
         load_x(2)
         load_pos(2)
         load_w1(5)
         load_w1(6)
-        load_w1(7)
         load_x(3)
         load_pos(3)
+        load_w1(7)
         load_x(4)
         load_pos(4)
         load_x(5)
@@ -340,300 +340,304 @@ def tile_mybadtransfomerblock_pa_kernel(tc, x, pos_emb, enc_w0, enc_w1_bytes, en
         load_pos(7)
         spread_scale(0)
         spread_scale(1)
-        copy_scale(0, "v")
+        copy_scale(0, "s")
         copy_scale(1, "s")
         add_pos(0, 0)
-        scale_w1(0)
+        add_pos(0, 1)
         transpose_y(0)
         copy_y(0, "s")
         transpose_w0(0)
         copy_w0(0, "s")
-        transpose_w0(1)
-        copy_w0(1, "s")
-        add_pos(0, 1)
-        transpose_w1(0)
-        copy_w1(0, "s")
-        scale_w1(1)
-        transpose_w0(2)
-        copy_w0(2, "s")
         transpose_y(1)
         copy_y(1, "s")
+        scale_w1(0)
+        transpose_w0(1)
+        copy_w0(1, "s")
+        scale_w1(1)
+        transpose_w1(0)
+        copy_w1(0, "s")
+        transpose_w0(2)
+        copy_w0(2, "s")
         transpose_w0(3)
         copy_w0(3, "s")
+        scale_w1(2)
         quant_w0(0)
-        quant_y(0)
         transpose_w0(4)
         copy_w0(4, "s")
-        quant_w0(1)
+        quant_y(0)
         transpose_w1(1)
         copy_w1(1, "s")
-        scale_w1(2)
+        quant_w0(1)
         transpose_w0(5)
         copy_w0(5, "s")
-        stage1(0, 0)
-        stage1(1, 0)
-        add_pos(1)
-        relu_h(0, 0, "s")
+        scale_w1(3)
         transpose_w0(6)
         copy_w0(6, "s")
-        relu_h(1, 0, "s")
         transpose_w0(7)
         copy_w0(7, "s")
+        transpose_w1(2)
+        copy_w1(2, "s")
+        stage1(0, 0)
+        relu_h(0, 0, "s")
         quant_w0(2)
-        scale_w1(3)
+        add_pos(1)
+        stage1(1, 0)
+        relu_h(1, 0, "s")
+        quant_w0(3)
         transpose_y(2)
         copy_y(2, "s")
         transpose_y(3)
         copy_y(3, "s")
-        quant_w0(3)
-        quant_w1(0, 0)
-        quant_w1(0, 1)
-        transpose_w1(2)
-        copy_w1(2, "s")
+        add_pos(2)
+        transpose_w1(3)
+        copy_w1(3, "s")
         stage1(0, 1)
         relu_h(0, 1, "s")
-        add_pos(2)
+        scale_w1(4)
         stage1(1, 1)
         relu_h(1, 1, "s")
         quant_y(1)
-        transpose_w1(3)
-        copy_w1(3, "s")
-        stage1(2, 0)
-        relu_h(2, 0, "s")
-        scale_w1(4)
-        stage1(2, 1)
-        relu_h(2, 1, "s")
         transpose_y(4)
         copy_y(4, "s")
         transpose_y(5)
         copy_y(5, "s")
-        quant_h(0)
         scale_w1(5)
-        stage1(3, 0)
-        relu_h(3, 0, "s")
-        stage1(3, 1)
-        relu_h(3, 1, "s")
-        quant_w1(1, 0)
-        quant_w1(1, 1)
-        add_pos(3)
-        quant_y(2)
         transpose_w1(4)
         copy_w1(4, "s")
+        add_pos(3)
+        stage1(2, 0)
+        relu_h(2, 0, "s")
+        stage1(2, 1)
+        relu_h(2, 1, "s")
+        scale_w1(6)
+        stage1(3, 0)
+        relu_h(3, 0, "s")
+        quant_y(2)
+        stage1(3, 1)
+        relu_h(3, 1, "s")
         transpose_w1(5)
         copy_w1(5, "s")
-        stage1(4, 0)
-        relu_h(4, 0, "s")
-        scale_w1(6)
-        stage1(4, 1)
-        relu_h(4, 1, "s")
-        quant_h(1)
         transpose_y(6)
         copy_y(6, "s")
         transpose_y(7)
         copy_y(7, "s")
         scale_w1(7)
-        stage2(0, 0)
-        relu_out(0, 0, "s")
-        stage1(5, 0)
-        relu_h(5, 0, "s")
-        stage1(5, 1)
-        relu_h(5, 1, "s")
-        quant_w1(2, 0)
-        quant_w1(2, 1)
-        quant_y(3)
+        stage1(4, 0)
+        relu_h(4, 0, "s")
+        stage1(4, 1)
+        relu_h(4, 1, "s")
         add_pos(4)
-        stage2(1, 0)
-        relu_out(1, 0, "s")
+        quant_w1(0, 0)
+        quant_w1(0, 1)
         transpose_w1(6)
         copy_w1(6, "s")
+        stage1(5, 0)
+        relu_h(5, 0, "s")
+        quant_y(3)
+        stage1(5, 1)
+        relu_h(5, 1, "s")
+        quant_w1(1, 0)
+        quant_w1(1, 1)
         transpose_w1(7)
         copy_w1(7, "s")
-        stage1(6, 0)
-        relu_h(6, 0, "s")
-        stage1(6, 1)
-        relu_h(6, 1, "s")
-        quant_h(2)
         transpose_y(8)
         copy_y(8, "s")
         transpose_y(9)
         copy_y(9, "s")
         add_pos(5)
-        quant_w1(3, 0)
-        quant_w1(3, 1)
-        stage2(2, 0)
-        relu_out(2, 0, "s")
+        quant_w1(2, 0)
+        quant_w1(2, 1)
+        stage1(6, 0)
+        relu_h(6, 0, "s")
+        stage1(6, 1)
+        relu_h(6, 1, "s")
+        quant_h(0)
         stage1(7, 0)
         relu_h(7, 0, "s")
-        stage1(7, 1)
-        relu_h(7, 1, "v")
-        stage2(3, 0)
-        relu_out(3, 0, "v")
         quant_y(4)
+        stage1(7, 1)
+        relu_h(7, 1, "s")
+        quant_w1(3, 0)
+        quant_w1(3, 1)
         transpose_y(10)
         copy_y(10, "s")
         transpose_y(11)
         copy_y(11, "s")
-        quant_h(3)
+        add_pos(6)
+        stage2(0, 0)
+        relu_out(0, 0, "s")
         stage2(0, 1)
         relu_out(0, 1, "s")
-        add_pos(6)
+        quant_h(1)
+        stage2(1, 0)
+        relu_out(1, 0, "s")
+        add_pos(7)
         stage2(1, 1)
         relu_out(1, 1, "s")
-        stage2(2, 1)
-        relu_out(2, 1, "v")
-        squares(0, "s")
-        stage2(3, 1)
-        relu_out(3, 1, "v")
-        stage2(4, 0)
-        relu_out(4, 0, "v")
-        squares(1, "s")
-        stage2(4, 1)
-        relu_out(4, 1, "v")
         stage1(8, 0)
         relu_h(8, 0, "v")
-        squares(2, "s")
+        squares(0, "s")
         stage1(8, 1)
         relu_h(8, 1, "v")
+        quant_y(5)
+        quant_h(2)
+        squares(1, "s")
         stage1(9, 0)
         relu_h(9, 0, "v")
         stage1(9, 1)
-        relu_h(9, 1, "s")
-        quant_y(5)
-        transpose_y(12)
-        copy_y(12, "s")
+        relu_h(9, 1, "v")
+        stage2(2, 0)
+        relu_out(2, 0, "s")
+        stage2(2, 1)
+        relu_out(2, 1, "v")
         root(0)
-        transpose_y(13)
-        copy_y(13, "s")
-        quant_h(4)
+        stage2(3, 0)
+        relu_out(3, 0, "s")
+        stage2(3, 1)
+        relu_out(3, 1, "v")
         add_eps(0, "s")
-        stage2(5, 0)
-        relu_out(5, 0, "s")
-        add_pos(7)
-        stage2(5, 1)
-        relu_out(5, 1, "s")
         reciprocal(0)
+        quant_h(3)
+        quant_h(4)
+        squares(2, "s")
         scale_out(0, None, "g")
         scale_out(1, None, "g")
-        scale_out(2, None, "g")
-        stage2(6, 0)
-        relu_out(6, 0, "s")
-        stage2(6, 1)
-        relu_out(6, 1, "v")
-        squares(3, "s")
-        stage2(7, 0)
-        relu_out(7, 0, "v")
-        stage2(7, 1)
-        relu_out(7, 1, "v")
-        squares(4, "s")
         stage1(10, 0)
         relu_h(10, 0, "v")
         stage1(10, 1)
         relu_h(10, 1, "v")
-        squares(5, "s")
+        transpose_y(12)
+        copy_y(12, "v")
+        transpose_y(13)
+        copy_y(13, "s")
+        squares(3, "s")
+        stage2(4, 0)
+        relu_out(4, 0, "s")
+        stage2(4, 1)
+        relu_out(4, 1, "v")
+        root(1)
+        stage2(5, 0)
+        relu_out(5, 0, "s")
+        stage2(5, 1)
+        relu_out(5, 1, "v")
+        add_eps(1, "s")
+        reciprocal(1)
+        quant_y(6)
+        squares(4, "s")
+        scale_out(2, None, "g")
+        scale_out(3, None, "g")
         stage1(11, 0)
         relu_h(11, 0, "v")
         stage1(11, 1)
         relu_h(11, 1, "v")
-        quant_y(6)
         transpose_y(14)
-        copy_y(14, "s")
-        root(1)
+        copy_y(14, "v")
         transpose_y(15)
         copy_y(15, "s")
+        squares(5, "s")
+        stage2(6, 0)
+        relu_out(6, 0, "s")
+        stage2(6, 1)
+        relu_out(6, 1, "v")
+        root(2)
+        stage2(7, 0)
+        relu_out(7, 0, "s")
+        stage2(7, 1)
+        relu_out(7, 1, "v")
+        add_eps(2, "s")
+        reciprocal(2)
         quant_h(5)
-        add_eps(1, "s")
-        stage2(8, 0)
-        relu_out(8, 0, "s")
         quant_y(7)
-        reciprocal(1)
-        scale_out(3, None, "g")
+        squares(6, "s")
         scale_out(4, None, "g")
         scale_out(5, None, "g")
-        stage2(8, 1)
-        relu_out(8, 1, "v")
-        stage2(9, 0)
-        relu_out(9, 0, "s")
-        stage2(9, 1)
-        relu_out(9, 1, "v")
-        squares(6, "s")
         stage1(12, 0)
         relu_h(12, 0, "v")
         stage1(12, 1)
         relu_h(12, 1, "v")
         squares(7, "s")
+        stage2(8, 0)
+        relu_out(8, 0, "s")
+        stage2(8, 1)
+        relu_out(8, 1, "v")
+        root(3)
+        stage2(9, 0)
+        relu_out(9, 0, "s")
+        stage2(9, 1)
+        relu_out(9, 1, "v")
+        add_eps(3, "s")
+        reciprocal(3)
+        squares(8, "s")
+        scale_out(6, None, "g")
+        scale_out(7, None, "g")
         stage1(13, 0)
         relu_h(13, 0, "v")
         stage1(13, 1)
         relu_h(13, 1, "v")
-        squares(8, "s")
+        squares(9, "s")
+        stage2(10, 0)
+        relu_out(10, 0, "s")
+        stage2(10, 1)
+        relu_out(10, 1, "v")
+        root(4)
+        stage2(11, 0)
+        relu_out(11, 0, "s")
+        stage2(11, 1)
+        relu_out(11, 1, "v")
+        add_eps(4, "s")
+        reciprocal(4)
+        quant_h(6)
+        squares(10, "s")
+        scale_out(8, None, "g")
+        scale_out(9, None, "g")
         stage1(14, 0)
         relu_h(14, 0, "v")
         stage1(14, 1)
         relu_h(14, 1, "v")
-        stage1(15, 0)
-        relu_h(15, 0, "s")
-        root(2)
-        quant_h(6)
-        stage1(15, 1)
-        relu_h(15, 1, "s")
-        add_eps(2, "s")
-        stage2(10, 0)
-        relu_out(10, 0, "s")
-        quant_h(7)
-        reciprocal(2)
-        scale_out(6, None, "g")
-        scale_out(7, None, "g")
-        scale_out(8, None, "g")
-        stage2(10, 1)
-        relu_out(10, 1, "v")
-        squares(9, "s")
-        stage2(11, 0)
-        relu_out(11, 0, "v")
-        stage2(11, 1)
-        relu_out(11, 1, "v")
-        squares(10, "s")
-        stage2(12, 0)
-        relu_out(12, 0, "v")
-        stage2(12, 1)
-        relu_out(12, 1, "v")
         squares(11, "s")
-        root(3)
-        stage2(13, 0)
-        relu_out(13, 0, "v")
-        squares(12, "s")
-        add_eps(3, "s")
+        stage1(15, 0)
+        relu_h(15, 0, "v")
+        stage1(15, 1)
+        relu_h(15, 1, "v")
+        stage2(12, 0)
+        relu_out(12, 0, "s")
+        root(5)
+        stage2(12, 1)
+        relu_out(12, 1, "s")
+        add_eps(5, "s")
         stage2(13, 1)
         relu_out(13, 1, "v")
-        reciprocal(3)
-        scale_out(9, None, "g")
-        scale_out(10, None, "g")
+        quant_h(7)
+        reciprocal(5)
+        stage2(13, 0)
+        relu_out(13, 0, "s")
+        squares(12, "s")
+        scale_out(10, None, "v")
+        scale_out(11, None, "g")
         stage2(14, 0)
         relu_out(14, 0, "v")
-        root(4)
         squares(13, "s")
-        add_eps(4, "s")
         stage2(14, 1)
         relu_out(14, 1, "v")
-        reciprocal(4)
         stage2(15, 0)
         relu_out(15, 0, "v")
+        root(6)
+        squares(14, "s", 0)
+        add_eps(6, "s")
         stage2(15, 1)
         relu_out(15, 1, "v")
-        root(5)
-        squares(14, "s")
-        add_eps(5, "s")
-        scale_out(11, None, "v")
+        squares(14, "s", 1)
+        reciprocal(6)
         scale_out(12, None, "v")
-        reciprocal(5)
         squares(15, "s", 0)
-        root(6)
+        root_of_halves(14)
         squares(15, "v", 1)
-        add_eps(6, "s")
+        add_eps(7, "s")
         scale_out(13, None, "v")
         root_of_halves(15)
-        reciprocal(6)
-        add_eps(7, "v")
-        scale_out(14, None, "v")
         reciprocal(7)
-        scale_out(15, 0, "s")
+        add_eps(8, "s")
+        scale_out(14, None, "v")
+        reciprocal(8)
         scale_out(15, 1, "v")
+        scale_out(15, 0, "v")

@@ -24,7 +24,13 @@ TILES = B * S // P
 PAIRS = TILES // B
 CHUNKS = D // P
 BANKS = 8
-RUN = 2
+BANK = 512
+WIDE = 22
+WORDS = D // 4
+
+W1_STEPS = {1: (4,), 2: (5, 6), 3: (7,)}
+GROUPS = [(B * f, B * f + 1) for f in range(PAIRS - 1)] + [(TILES - 2,), (TILES - 1,)]
+PLACE = {i: (group, n) for group, tiles in enumerate(GROUPS) for n, i in enumerate(tiles)}
 
 
 def tile_mybadtransfomerblock_pa_kernel(tc, x, pos_emb, enc_w0, enc_w1_bytes, enc_w1_scale, out):
@@ -37,39 +43,46 @@ def tile_mybadtransfomerblock_pa_kernel(tc, x, pos_emb, enc_w0, enc_w1_bytes, en
 
         ident = keep.tile([P, P], F32, tag="ident")
         make_identity(nc, ident[:])
-        warm = keep.tile([P, 1], F32, tag="warm")
-        nc.vector.memset(warm[:], 1.0)
-        warm2 = keep.tile([P, 1], F32, tag="warm2")
-        nc.scalar.activation(out=warm2[:], in_=warm[:], func=ACT.Sqrt)
-
-        x_in, pos_in, w0_in, w1_in, yp, yt, y_codes, y_scales = {}, {}, {}, {}, {}, {}, {}, {}
-        ht, h_codes, h_scales, bank, res, sums, inv = {}, {}, {}, {}, {}, {}, {}
-        w1_prod, w0_grouped, w1_grouped = {}, {}, {}
-        free_banks = list(range(BANKS))
-        bank_number = {}
+        one = keep.tile([P, 1], F32, tag="one")
+        nc.vector.memset(one[:], 1.0)
+        unread = keep.tile([P, 1], F32, tag="unread")
+        nc.scalar.activation(out=unread[:], in_=one[:], func=ACT.Sqrt)
 
         scale_cols = keep.tile([P, CHUNKS], F32, tag="scale_cols")
         w1_scale = keep.tile([P, D], F32, tag="w1_scale")
-        w0_codes = keep.tile([P, CHUNKS, PASSES, P], U32, tag="w0_codes", align_bytes=64)
-        w0_scales = keep.tile([P, CHUNKS, PASSES, P], U8, tag="w0_scales", align_bytes=64)
-        w1_codes = keep.tile([P, PASSES, D], U32, tag="w1_codes", align_bytes=64)
-        w1_scales = keep.tile([P, PASSES, D], U8, tag="w1_scales", align_bytes=64)
+        w0_codes = keep.tile([P, CHUNKS, PASSES, P], U32, tag="w0_codes", align_bytes=256)
+        w0_scales = keep.tile([P, CHUNKS, PASSES, P], U8, tag="w0_scales", align_bytes=256)
+        w1_codes = keep.tile([P, PASSES, D], U32, tag="w1_codes", align_bytes=256)
+        w1_scales = keep.tile([P, PASSES, D], U8, tag="w1_scales", align_bytes=256)
 
-        def load_scale():
-            nc.sync.dma_start(out=scale_cols[:], in_=enc_w1_scale.rearrange("o (p j) -> p (o j)", p=P))
+        x_in, pos_in, w0_in, w1_in = {}, {}, {}, {}
+        y_rows, y_turned, y_codes, y_scales = {}, {}, {}, {}
+        w0_turned, w1_rows, w1_turned = {}, {}, {}
+        h_turned, h_codes, h_scales = {}, {}, {}
+        h2, sums, factors = {}, {}, {}
+        banks_used = []
 
-        def load_x(p, b=None):
+        def next_bank():
+            banks_used.append(psum.tile([P, BANK], F32, tag="bank%d" % (len(banks_used) % BANKS), name="bank"))
+            return banks_used[-1]
+
+        def relu(engine, dst, src):
+            if engine == "scalar":
+                nc.scalar.activation(out=dst, in_=src, func=ACT.Relu)
+            else:
+                nc.vector.tensor_scalar(out=dst, in0=src, scalar1=0.0, scalar2=None, op0=MAX)
+
+        def load_x(p, batches=slice(0, B)):
             if p not in x_in:
                 x_in[p] = work.tile([P, B, D], BF16, tag="x_in", bufs=PAIRS, name="x_in")
             rows = x[:, p * P : (p + 1) * P, :].rearrange("b s k -> s b k")
-            part = slice(0, B) if b is None else slice(b, b + 1)
-            nc.sync.dma_start(out=x_in[p][:, part], in_=rows[:, part])
+            nc.sync.dma_start(out=x_in[p][:, batches], in_=rows[:, batches])
 
-        def load_pos(j):
-            pos_in[j] = work.tile([P, D], BF16, tag="pos_in", bufs=8, name="pos_in")
-            nc.sync.dma_start(out=pos_in[j][:], in_=pos_emb[0, j * P : (j + 1) * P, :])
+        def load_pos(p):
+            pos_in[p] = work.tile([P, D], BF16, tag="pos_in", bufs=PAIRS, name="pos_in")
+            nc.sync.dma_start(out=pos_in[p][:], in_=pos_emb[0, p * P : (p + 1) * P, :])
 
-        w0_rows = enc_w0.rearrange("(h m t) k -> h t m k", h=2, m=P, t=4)
+        w0_rows = enc_w0.rearrange("(h m t) k -> h t m k", h=PASSES, m=P, t=4)
 
         def load_w0(c):
             w0_in[c] = work.tile([P, D], BF16, tag="w0_in", bufs=CHUNKS, name="w0_in")
@@ -79,565 +92,358 @@ def tile_mybadtransfomerblock_pa_kernel(tc, x, pos_emb, enc_w0, enc_w1_bytes, en
             w1_in[a] = work.tile([P, D], U8, tag="w1_in", bufs=CHUNKS, name="w1_in")
             nc.sync.dma_start(out=w1_in[a][:], in_=enc_w1_bytes[a * P : (a + 1) * P, :])
 
-        def new_bank(key):
-            bank_number[key] = free_banks.pop(0)
-            bank[key] = psum.tile([P, 512], F32, tag="bank%d" % bank_number[key], name="bank")
-            return bank[key]
-
-        def take_bank(key):
-            free_banks.append(bank_number.pop(key))
-            return bank.pop(key)
-
         def spread_scale(half):
-            b = new_bank(("scale", half))
+            bank = next_bank()
             for j in range(4):
-                col = scale_cols[:, 4 * half + j : 4 * half + j + 1]
-                nc.tensor.transpose(b[:, j * P : (j + 1) * P], col.to_broadcast([P, P]), ident[:])
+                column = scale_cols[:, 4 * half + j : 4 * half + j + 1]
+                nc.tensor.transpose(bank[:, j * P : (j + 1) * P], column.to_broadcast([P, P]), ident[:])
+            return bank
 
-        def copy_scale(half, engine):
-            src = take_bank(("scale", half))[:].rearrange("p (j q) -> p q j", j=4)
-            dst = w1_scale[:].rearrange("p (q j) -> p q j", j=CHUNKS)[:, :, 4 * half : 4 * half + 4]
-            if engine == "s":
-                nc.scalar.copy(out=dst, in_=src)
-            else:
-                nc.vector.tensor_copy(out=dst, in_=src)
+        def copy_scale(half, bank):
+            dst = w1_scale[:].rearrange("q (p j) -> q p j", j=CHUNKS)[:, :, 4 * half : 4 * half + 4]
+            nc.scalar.copy(out=dst, in_=bank[:].rearrange("q (j p) -> q p j", j=4))
 
-        def transpose_words(key, source):
-            v = new_bank(key)[:].rearrange("p (u g n) -> p g u n", g=2, u=2)
-            for g in range(2):
+        def transpose_words(source):
+            bank = next_bank()
+            blocks = bank[:].rearrange("p (u g n) -> p g u n", g=PASSES, u=2)
+            for g in range(PASSES):
                 for u in range(2):
-                    nc.tensor.transpose(v[:, g, u, :], source(g, u), ident[:])
+                    nc.tensor.transpose(blocks[:, g, u, :], source(g, u), ident[:])
+            return bank
 
-        def copy_words(engine, key, dst):
-            src = take_bank(key)[:].rearrange("p (u g c i) -> p g c u i", g=2, u=2, i=2)
-            if engine == "s":
+        def copy_words(engine, bank, dst):
+            src = bank[:].rearrange("p (u g c i) -> p g c u i", g=PASSES, u=2, i=2)
+            dst = dst.rearrange("p g (c i u) -> p g c u i", u=2, i=2)
+            if engine == "scalar":
                 nc.scalar.copy(out=dst, in_=src)
             else:
                 nc.vector.tensor_copy(out=dst, in_=src)
 
-        def add_pos(p, b=None):
-            if p not in yp:
-                yp[p] = work.tile([P, 2, B, D // 2], BF16, tag="yp", name="yp", bufs=3)
-            part = slice(0, B) if b is None else slice(b, b + 1)
-            count = B if b is None else 1
-            runs = "p b (w u e) -> p b w u e"
-            nc.vector.tensor_tensor(
-                out=yp[p][:, :, part].rearrange("p u b (w e) -> p b w u e", e=RUN),
-                in0=x_in[p][:, part].rearrange(runs, u=2, e=RUN),
-                in1=pos_in[p][:].unsqueeze(1).to_broadcast([P, count, D]).rearrange(runs, u=2, e=RUN),
-                op=ADD,
-            )
+        def every_second_word(rows):
+            words = rows[:].bitcast(F32)
+            return lambda g, u: words[:, 2 * P * g + u : 2 * P * (g + 1) : 2]
 
-        def transpose_y(i):
-            words = yp[i // B][:, :, i % B].bitcast(F32)
-            transpose_words(("y", i), lambda g, u: words[:, u, g * P : (g + 1) * P])
+        def turn_y(i, engine):
+            p, b = divmod(i, B)
+            words = y_rows[p][:, :, b].bitcast(F32)
+            bank = transpose_words(lambda g, u: words[:, u, g * P : (g + 1) * P])
+            if b == 0:
+                y_turned[p] = work.tile([P, B, D], BF16, tag="wide", bufs=WIDE, name="y_turned", align_bytes=64)
+            copy_words(engine, bank, y_turned[p][:, b].bitcast(F32).rearrange("p (g n) -> p g n", g=PASSES))
 
-        def copy_y(i, engine):
-            if i // B not in yt:
-                yt[i // B] = work.tile([P, B, D], BF16, tag="yt", name="yt", align_bytes=64, bufs=3)
-            dst = yt[i // B][:, i % B].bitcast(F32)
-            copy_words(engine, ("y", i), dst.rearrange("p (g c i u) -> p g c u i", g=2, u=2, i=2))
+        def turn_w0(c):
+            q, e = divmod(c, 2)
+            bank = transpose_words(every_second_word(w0_in.pop(c)))
+            if e == 0:
+                w0_turned[q] = work.tile([P, 2, D], BF16, tag="wide", bufs=WIDE, name="w0_turned", align_bytes=64)
+            copy_words("scalar", bank, w0_turned[q][:, e].bitcast(F32).rearrange("p (g n) -> p g n", g=PASSES))
 
-        def quant_y(p, b=None):
-            if p not in y_codes:
-                y_codes[p] = work.tile([P, B, 256], U32, tag="y_codes", name="y_codes", align_bytes=64, bufs=4)
-                y_scales[p] = work.tile([P, B, 256], U8, tag="y_scales", name="y_scales", align_bytes=64, bufs=4)
-            part = slice(0, B) if b is None else slice(b, b + 1)
-            flat = "p b n -> p (b n)"
-            nc.vector.quantize_mx(
-                out=y_codes[p][:, part].rearrange(flat).bitcast(FP8X4),
-                scales=y_scales[p][:, part].rearrange(flat),
-                in_=yt[p][:, part].rearrange(flat),
-            )
+        def turn_w1(a):
+            q, e = divmod(a, 2)
+            bank = transpose_words(every_second_word(w1_rows.pop(a)))
+            if e == 0:
+                w1_turned[q] = work.tile([P, PASSES, 2, P * 4], BF16, tag="wide", bufs=WIDE, name="w1_turned", align_bytes=64)
+            copy_words("scalar", bank, w1_turned[q][:, :, e].bitcast(F32))
 
-        def transpose_w0(c):
-            words = w0_in.pop(c)[:].bitcast(F32)
-            transpose_words(("w0", c), lambda g, u: words[:, 256 * g + u : 256 * (g + 1) : 2])
+        def stage1(i, h, engine):
+            p, b = divmod(i, B)
+            bank = next_bank()
+            for t in range(4):
+                for g in range(PASSES):
+                    nc.tensor.matmul_mx(
+                        out=bank[:, t * P : (t + 1) * P],
+                        lhsT=w0_codes[:, 4 * h + t, g, :].bitcast(FP8X4),
+                        lhsT_scale=w0_scales[:, 4 * h + t, g, :],
+                        rhs=y_codes[p][:, b, g * P : (g + 1) * P].bitcast(FP8X4),
+                        rhs_scale=y_scales[p][:, b, g * P : (g + 1) * P],
+                        start=(g == 0),
+                        stop=(g == PASSES - 1),
+                    )
+            if p not in h_turned:
+                h_turned[p] = work.tile([P, B, PASSES, P, 4], BF16, tag="wide", bufs=WIDE, name="h_turned", align_bytes=64)
+            dst = h_turned[p][:, b, h].rearrange("p (c i) t -> p c t i", i=2)
+            relu(engine, dst, bank[:].rearrange("p (t c i) -> p c t i", t=4, i=2))
 
-        def copy_w0(c, engine):
-            if c // 2 not in w0_grouped:
-                w0_grouped[c // 2] = work.tile([P, 2, D], BF16, tag="w0_grouped", name="w0_grouped", align_bytes=64, bufs=3)
-            dst = w0_grouped[c // 2][:, c % 2].bitcast(F32)
-            copy_words(engine, ("w0", c), dst.rearrange("p (g c i u) -> p g c u i", g=2, u=2, i=2))
-
-        def quant_w0(q, c=None):
-            part = slice(0, 2) if c is None else slice(c, c + 1)
-            nc.vector.quantize_mx(
-                out=w0_codes[:, 2 * q : 2 * q + 2][:, part].rearrange("p c g m -> p (c g m)").bitcast(FP8X4),
-                scales=w0_scales[:, 2 * q : 2 * q + 2][:, part].rearrange("p c g m -> p (c g m)"),
-                in_=w0_grouped[q][:, part].rearrange("p c n -> p (c n)"),
-            )
-
-        def scale_w1(a):
-            w1_prod[a] = work.tile([P, D], BF16, tag="w1_prod", name="w1_prod", bufs=3)
-            nc.vector.tensor_tensor(out=w1_prod[a][:], in0=w1_in.pop(a)[:].bitcast(FP8), in1=w1_scale[:], op=MULT)
-
-        def transpose_w1(a):
-            words = w1_prod.pop(a)[:].bitcast(F32)
-            transpose_words(("w1", a), lambda g, u: words[:, 256 * g + u : 256 * (g + 1) : 2])
-
-        def copy_w1(a, engine):
-            if a % 2 == 0:
-                w1_grouped[a // 2] = work.tile([P, PASSES, 2 * P, 4], BF16, tag="w1_grouped", name="w1_grouped", align_bytes=64, bufs=3)
-            rows = slice((a % 2) * P, (a % 2 + 1) * P)
-            dst = w1_grouped[a // 2][:, :, rows, :].rearrange("p g n t -> p g (n t)").bitcast(F32)
-            copy_words(engine, ("w1", a), dst.rearrange("p g (c i u) -> p g c u i", u=2, i=2))
-
-        def quant_w1(pair, g):
-            cols = slice(pair * 256, (pair + 1) * 256)
-            nc.vector.quantize_mx(
-                out=w1_codes[:, g, cols].bitcast(FP8X4),
-                scales=w1_scales[:, g, cols],
-                in_=w1_grouped[pair][:, g].rearrange("p n t -> p (n t)"),
-            )
-
-        def stage1_chunk(i, c):
-            h, t = divmod(c, 4)
-            b = new_bank(("h", i, h)) if t == 0 else bank[("h", i, h)]
+        def stage2(i, n, engine):
+            p, b = divmod(i, B)
+            cols = slice(n * BANK, (n + 1) * BANK)
+            bank = next_bank()
             for g in range(PASSES):
                 nc.tensor.matmul_mx(
-                    out=b[:, t * P : (t + 1) * P],
-                    lhsT=w0_codes[:, c, g, :].bitcast(FP8X4),
-                    lhsT_scale=w0_scales[:, c, g, :],
-                    rhs=y_codes[i // B][:, i % B, g * P : (g + 1) * P].bitcast(FP8X4),
-                    rhs_scale=y_scales[i // B][:, i % B, g * P : (g + 1) * P],
+                    out=bank[:],
+                    lhsT=h_codes[p][:, b, g * P : (g + 1) * P].bitcast(FP8X4),
+                    lhsT_scale=h_scales[p][:, b, g * P : (g + 1) * P],
+                    rhs=w1_codes[:, g, cols].bitcast(FP8X4),
+                    rhs_scale=w1_scales[:, g, cols],
                     start=(g == 0),
                     stop=(g == PASSES - 1),
                 )
+            if i not in h2:
+                h2[i] = work.tile([P, D], F32, tag="wide", bufs=WIDE, name="h2", align_bytes=64)
+            relu(engine, h2[i][:, cols], bank[:])
 
-        def stage1(i, h):
-            for t in range(4):
-                stage1_chunk(i, 4 * h + t)
-
-        def relu(engine, dst, src):
-            if engine == "s":
-                nc.scalar.activation(out=dst, in_=src, func=ACT.Relu)
-            else:
-                nc.vector.tensor_scalar(out=dst, in0=src, scalar1=0.0, scalar2=None, op0=MAX)
-
-        def relu_h(i, h, engine):
-            if i // B not in ht:
-                ht[i // B] = work.tile([P, B, 2, P, 4], BF16, tag="ht", name="ht", align_bytes=64, bufs=4)
-            src = take_bank(("h", i, h))[:].rearrange("p (t c i) -> p c t i", t=4, i=2)
-            relu(engine, ht[i // B][:, i % B, h].rearrange("p (c i) t -> p c t i", i=2), src)
-
-        def quant_h(p, b=None):
-            if p not in h_codes:
-                h_codes[p] = work.tile([P, B, 256], U32, tag="h_codes", name="h_codes", align_bytes=64, bufs=PAIRS)
-                h_scales[p] = work.tile([P, B, 256], U8, tag="h_scales", name="h_scales", align_bytes=64, bufs=PAIRS)
-            part = slice(0, B) if b is None else slice(b, b + 1)
-            nc.vector.quantize_mx(
-                out=h_codes[p][:, part].rearrange("p b n -> p (b n)").bitcast(FP8X4),
-                scales=h_scales[p][:, part].rearrange("p b n -> p (b n)"),
-                in_=ht[p][:, part].rearrange("p b h n t -> p (b h n t)"),
+        def add_pos(p, batches=slice(0, B)):
+            if p not in y_rows:
+                y_rows[p] = work.tile([P, 2, B, D // 2], BF16, tag="wide", bufs=WIDE, name="y_rows", align_bytes=64)
+            words = "p b (w u e) -> p b w u e"
+            count = batches.stop - batches.start
+            nc.vector.tensor_tensor(
+                out=y_rows[p][:, :, batches].rearrange("p u b (w e) -> p b w u e", e=2),
+                in0=x_in[p][:, batches].rearrange(words, u=2, e=2),
+                in1=pos_in[p][:].unsqueeze(1).to_broadcast([P, count, D]).rearrange(words, u=2, e=2),
+                op=ADD,
             )
 
-        def stage2(i, n):
-            hc, hs = h_codes[i // B][:, i % B], h_scales[i // B][:, i % B]
-            b = new_bank(("o", i, n))
-            for h in range(2):
-                nc.tensor.matmul_mx(
-                    out=b[:],
-                    lhsT=hc[:, h * P : (h + 1) * P].bitcast(FP8X4),
-                    lhsT_scale=hs[:, h * P : (h + 1) * P],
-                    rhs=w1_codes[:, h, n * 512 : (n + 1) * 512].bitcast(FP8X4),
-                    rhs_scale=w1_scales[:, h, n * 512 : (n + 1) * 512],
-                    start=(h == 0),
-                    stop=(h == 1),
-                )
+        def scale_w1(a):
+            w1_rows[a] = work.tile([P, D], BF16, tag="w1_rows", name="w1_rows", bufs=CHUNKS)
+            nc.vector.tensor_tensor(out=w1_rows[a][:], in0=w1_in.pop(a)[:].bitcast(FP8), in1=w1_scale[:], op=MULT)
 
-        def relu_out(i, n, engine):
-            if i not in res:
-                res[i] = work.tile([P, D], F32, tag="res", name="res", bufs=8)
-            relu(engine, res[i][:, n * 512 : (n + 1) * 512], take_bank(("o", i, n))[:])
+        def quantise_pair(p, values, codes, scales, tag, bufs):
+            codes[p] = work.tile([P, B, WORDS], U32, tag=tag + "_codes", name="codes", align_bytes=256, bufs=bufs)
+            scales[p] = work.tile([P, B, WORDS], U8, tag=tag + "_scales", name="scales", align_bytes=256, bufs=bufs)
+            nc.vector.quantize_mx(
+                out=codes[p][:].rearrange("p b n -> p (b n)").bitcast(FP8X4),
+                scales=scales[p][:].rearrange("p b n -> p (b n)"),
+                in_=values,
+            )
+
+        def quantise_y(p):
+            quantise_pair(p, y_turned.pop(p)[:].rearrange("p b n -> p (b n)"), y_codes, y_scales, "y", 4)
+
+        def quantise_h(p):
+            quantise_pair(p, h_turned.pop(p)[:].rearrange("p b h n t -> p (b h n t)"), h_codes, h_scales, "h", PAIRS)
+
+        def quantise_w0(q):
+            nc.vector.quantize_mx(
+                out=w0_codes[:, 2 * q : 2 * q + 2].rearrange("p c g m -> p (c g m)").bitcast(FP8X4),
+                scales=w0_scales[:, 2 * q : 2 * q + 2].rearrange("p c g m -> p (c g m)"),
+                in_=w0_turned.pop(q)[:].rearrange("p c n -> p (c n)"),
+            )
+
+        def quantise_w1(q):
+            values = w1_turned.pop(q)
+            cols = slice(2 * P * q, 2 * P * (q + 1))
+            for g in range(PASSES):
+                nc.vector.quantize_mx(
+                    out=w1_codes[:, g, cols].bitcast(FP8X4),
+                    scales=w1_scales[:, g, cols],
+                    in_=values[:, g].rearrange("p e n -> p (e n)"),
+                )
 
         def squares(i, engine, half=None):
-            group, place = GROUP[i]
+            group, n = PLACE[i]
             if group not in sums:
-                sums[group] = work.tile([P, 4], F32, tag="sums", name="sums", bufs=4)
-            cols = slice(0, D) if half is None else slice(half * 512, (half + 1) * 512)
-            slot = place + 2 * (half or 0)
-            acc = sums[group][:, slot : slot + 1]
-            part = res[i][:, cols]
-            if engine == "s":
-                junk_s = work.tile([P, D], BF16, tag="junk_s", name="junk_s", bufs=2)
-                nc.scalar.activation(out=junk_s[:, cols], in_=part, func=ACT.Square, accum_out=acc)
+                sums[group] = work.tile([P, 4], F32, tag="sums", name="sums", bufs=len(GROUPS))
+            cols = slice(0, D) if half is None else slice(half * BANK, (half + 1) * BANK)
+            slot = n if half is None else n + 2 * half
+            total = sums[group][:, slot : slot + 1]
+            values = h2[i][:, cols]
+            if engine == "scalar":
+                squared = work.tile([P, D], BF16, tag="squared_s", name="squared", bufs=2)
+                nc.scalar.activation(out=squared[:, cols], in_=values, func=ACT.Square, accum_out=total)
             else:
-                junk_v = work.tile([P, D], BF16, tag="junk_v", name="junk_v", bufs=1)
+                squared = work.tile([P, D], BF16, tag="squared_v", name="squared", bufs=1)
                 nc.vector.scalar_tensor_tensor(
-                    out=junk_v[:, cols], in0=part, scalar=1.0, in1=part, op0=MULT, op1=MULT, accum_out=acc
+                    out=squared[:, cols], in0=values, scalar=1.0, in1=values, op0=MULT, op1=MULT, accum_out=total
                 )
 
-        def root(f):
-            inv[f] = work.tile([P, len(GROUPS[f])], F32, tag="inv", name="inv", bufs=4)
-            nc.scalar.activation(out=inv[f][:], in_=sums[f][:, 0 : len(GROUPS[f])], func=ACT.Sqrt)
-
-        def root_of_halves(i):
-            f, e = GROUP[i]
-            if f not in inv:
-                inv[f] = work.tile([P, len(GROUPS[f])], F32, tag="inv", name="inv", bufs=4)
-            nc.scalar.activation(
-                out=inv[f][:, e : e + 1], in_=sums[f][:, e : e + 1], func=ACT.Sqrt, bias=sums[f][:, 2 + e : 3 + e]
-            )
-
-        def add_eps(f, engine):
-            if engine == "s":
-                nc.scalar.activation(out=inv[f][:], in_=inv[f][:], func=ACT.Copy, bias=EPS)
+        def root(group):
+            count = len(GROUPS[group])
+            factors[group] = work.tile([P, count], F32, tag="factors", name="factors", bufs=len(GROUPS))
+            if count == B:
+                nc.scalar.activation(out=factors[group][:], in_=sums[group][:, 0:count], func=ACT.Sqrt)
             else:
-                nc.vector.tensor_scalar(out=inv[f][:], in0=inv[f][:], scalar1=EPS, scalar2=None, op0=ADD)
+                nc.scalar.activation(
+                    out=factors[group][:], in_=sums[group][:, 0:1], func=ACT.Sqrt, bias=sums[group][:, 2:3]
+                )
 
-        def reciprocal(f):
-            nc.vector.reciprocal(out=inv[f][:], in_=inv[f][:])
+        def add_eps(group):
+            nc.scalar.activation(out=factors[group][:], in_=factors[group][:], func=ACT.Copy, bias=EPS)
 
-        def scale_out(i, n, engine):
-            cols = slice(0, D) if n is None else slice(n * 512, (n + 1) * 512)
-            r = res[i][:, cols]
-            factor = inv[GROUP[i][0]][:, GROUP[i][1] : GROUP[i][1] + 1]
-            if engine == "v":
-                nc.vector.tensor_scalar(out=r, in0=r, scalar1=factor, scalar2=None, op0=MULT)
-            elif engine == "g":
-                nc.gpsimd.tensor_scalar(out=r, in0=r, scalar1=factor, scalar2=0.0, op0=MULT, op1=ADD)
+        def reciprocal(group):
+            nc.vector.reciprocal(out=factors[group][:], in_=factors[group][:])
+
+        def scale_and_store(i, engine, cols=slice(0, D)):
+            group, n = PLACE[i]
+            values, factor = h2[i][:, cols], factors[group][:, n : n + 1]
+            if engine == "vector":
+                nc.vector.tensor_scalar(out=values, in0=values, scalar1=factor, scalar2=None, op0=MULT)
             else:
-                nc.scalar.activation(out=r, in_=r, func=ACT.Copy, scale=factor)
-            s0 = (i // 2) * P
-            nc.sync.dma_start(out=out[i % 2, s0 : s0 + P, cols], in_=r)
+                nc.gpsimd.tensor_scalar(out=values, in0=values, scalar1=factor, scalar2=0.0, op0=MULT, op1=ADD)
+            p, b = divmod(i, B)
+            nc.sync.dma_start(out=out[b, p * P : (p + 1) * P, cols], in_=values)
 
-        GROUPS = [(0, 1), (2, 3), (4, 5), (6, 7), (8, 9), (10, 11), (12, 13), (14,), (15,)]
-        GROUP = {i: (f, e) for f, tiles in enumerate(GROUPS) for e, i in enumerate(tiles)}
-        load_scale()
-        load_x(0, 0)
+        first, second = slice(0, 1), slice(1, 2)
+        nc.sync.dma_start(out=scale_cols[:], in_=enc_w1_scale.rearrange("o (p j) -> p (o j)", p=P))
+        load_x(0, first)
         load_pos(0)
         load_w0(0)
-        load_x(0, 1)
+        load_x(0, second)
         load_w1(0)
         load_w0(1)
-        load_w1(1)
-        load_w0(2)
-        load_w0(3)
-        load_w1(2)
-        load_w0(4)
-        load_w0(5)
-        load_w1(3)
-        load_w0(6)
-        load_w0(7)
-        load_x(1)
-        load_pos(1)
-        load_w1(4)
-        load_x(2)
-        load_pos(2)
-        load_w1(5)
-        load_w1(6)
-        load_x(3)
-        load_pos(3)
-        load_w1(7)
-        load_x(4)
-        load_pos(4)
-        load_x(5)
-        load_pos(5)
-        load_x(6)
-        load_pos(6)
-        load_x(7)
-        load_pos(7)
-        spread_scale(0)
-        spread_scale(1)
-        copy_scale(0, "s")
-        copy_scale(1, "s")
-        add_pos(0, 0)
-        add_pos(0, 1)
-        transpose_y(0)
-        copy_y(0, "s")
-        transpose_w0(0)
-        copy_w0(0, "s")
-        transpose_y(1)
-        copy_y(1, "s")
+        for q in range(1, CHUNKS // 2):
+            load_w1(q)
+            load_w0(2 * q)
+            load_w0(2 * q + 1)
+        for p in range(1, PAIRS):
+            load_x(p)
+            load_pos(p)
+            for a in W1_STEPS.get(p, ()):
+                load_w1(a)
+
+        scale_banks = [spread_scale(half) for half in range(2)]
+        for half in range(2):
+            copy_scale(half, scale_banks[half])
+        add_pos(0, first)
+        add_pos(0, second)
+        turn_y(0, "scalar")
+        turn_w0(0)
+        turn_y(1, "scalar")
         scale_w1(0)
-        transpose_w0(1)
-        copy_w0(1, "s")
+        turn_w0(1)
         scale_w1(1)
-        transpose_w1(0)
-        copy_w1(0, "s")
-        transpose_w0(2)
-        copy_w0(2, "s")
-        transpose_w0(3)
-        copy_w0(3, "s")
+        turn_w1(0)
+        turn_w0(2)
+        turn_w0(3)
         scale_w1(2)
-        quant_w0(0)
-        transpose_w0(4)
-        copy_w0(4, "s")
-        quant_y(0)
-        transpose_w1(1)
-        copy_w1(1, "s")
-        quant_w0(1)
-        transpose_w0(5)
-        copy_w0(5, "s")
+        quantise_w0(0)
+        turn_w0(4)
+        quantise_y(0)
+        turn_w1(1)
+        quantise_w0(1)
+        turn_w0(5)
         scale_w1(3)
-        transpose_w0(6)
-        copy_w0(6, "s")
-        transpose_w0(7)
-        copy_w0(7, "s")
-        transpose_w1(2)
-        copy_w1(2, "s")
-        stage1(0, 0)
-        relu_h(0, 0, "s")
-        quant_w0(2)
+        turn_w0(6)
+        turn_w0(7)
+        turn_w1(2)
+        stage1(0, 0, "scalar")
+        quantise_w0(2)
         add_pos(1)
-        stage1(1, 0)
-        relu_h(1, 0, "s")
-        quant_w0(3)
-        transpose_y(2)
-        copy_y(2, "s")
-        transpose_y(3)
-        copy_y(3, "s")
+        stage1(1, 0, "scalar")
+        quantise_w0(3)
+        turn_y(2, "scalar")
+        turn_y(3, "scalar")
         add_pos(2)
-        transpose_w1(3)
-        copy_w1(3, "s")
-        stage1(0, 1)
-        relu_h(0, 1, "s")
+        turn_w1(3)
+        stage1(0, 1, "scalar")
         scale_w1(4)
-        stage1(1, 1)
-        relu_h(1, 1, "s")
-        quant_y(1)
-        transpose_y(4)
-        copy_y(4, "s")
-        transpose_y(5)
-        copy_y(5, "s")
+        stage1(1, 1, "scalar")
+        quantise_y(1)
+
+        turn_y(4, "scalar")
+        turn_y(5, "scalar")
         scale_w1(5)
-        transpose_w1(4)
-        copy_w1(4, "s")
+        turn_w1(4)
         add_pos(3)
-        stage1(2, 0)
-        relu_h(2, 0, "s")
-        stage1(2, 1)
-        relu_h(2, 1, "s")
+        stage1(2, 0, "scalar")
+        stage1(2, 1, "scalar")
         scale_w1(6)
-        stage1(3, 0)
-        relu_h(3, 0, "s")
-        quant_y(2)
-        stage1(3, 1)
-        relu_h(3, 1, "s")
-        transpose_w1(5)
-        copy_w1(5, "s")
-        transpose_y(6)
-        copy_y(6, "s")
-        transpose_y(7)
-        copy_y(7, "s")
+        stage1(3, 0, "scalar")
+        quantise_y(2)
+        stage1(3, 1, "scalar")
+
+        turn_w1(5)
+        turn_y(6, "scalar")
+        turn_y(7, "scalar")
         scale_w1(7)
-        stage1(4, 0)
-        relu_h(4, 0, "s")
-        stage1(4, 1)
-        relu_h(4, 1, "s")
+        stage1(4, 0, "scalar")
+        stage1(4, 1, "scalar")
         add_pos(4)
-        quant_w1(0, 0)
-        quant_w1(0, 1)
-        transpose_w1(6)
-        copy_w1(6, "s")
-        stage1(5, 0)
-        relu_h(5, 0, "s")
-        quant_y(3)
-        stage1(5, 1)
-        relu_h(5, 1, "s")
-        quant_w1(1, 0)
-        quant_w1(1, 1)
-        transpose_w1(7)
-        copy_w1(7, "s")
-        transpose_y(8)
-        copy_y(8, "s")
-        transpose_y(9)
-        copy_y(9, "s")
+        quantise_w1(0)
+        turn_w1(6)
+        stage1(5, 0, "scalar")
+        quantise_y(3)
+        stage1(5, 1, "scalar")
+        quantise_w1(1)
+
+        turn_w1(7)
+        turn_y(8, "scalar")
+        turn_y(9, "scalar")
         add_pos(5)
-        quant_w1(2, 0)
-        quant_w1(2, 1)
-        stage1(6, 0)
-        relu_h(6, 0, "s")
-        stage1(6, 1)
-        relu_h(6, 1, "s")
-        quant_h(0)
-        stage1(7, 0)
-        relu_h(7, 0, "s")
-        quant_y(4)
-        stage1(7, 1)
-        relu_h(7, 1, "s")
-        quant_w1(3, 0)
-        quant_w1(3, 1)
-        transpose_y(10)
-        copy_y(10, "s")
-        transpose_y(11)
-        copy_y(11, "s")
+        quantise_w1(2)
+        stage1(6, 0, "scalar")
+        stage1(6, 1, "scalar")
+        quantise_h(0)
+        stage1(7, 0, "scalar")
+        quantise_y(4)
+        stage1(7, 1, "scalar")
+        quantise_w1(3)
+
+        turn_y(10, "scalar")
+        turn_y(11, "scalar")
         add_pos(6)
-        stage2(0, 0)
-        relu_out(0, 0, "s")
-        stage2(0, 1)
-        relu_out(0, 1, "s")
-        quant_h(1)
-        stage2(1, 0)
-        relu_out(1, 0, "s")
+        stage2(0, 0, "scalar")
+        stage2(0, 1, "scalar")
+        quantise_h(1)
+        stage2(1, 0, "scalar")
         add_pos(7)
-        stage2(1, 1)
-        relu_out(1, 1, "s")
-        stage1(8, 0)
-        relu_h(8, 0, "v")
-        squares(0, "s")
-        stage1(8, 1)
-        relu_h(8, 1, "v")
-        quant_y(5)
-        quant_h(2)
-        squares(1, "s")
-        stage1(9, 0)
-        relu_h(9, 0, "v")
-        stage1(9, 1)
-        relu_h(9, 1, "v")
-        stage2(2, 0)
-        relu_out(2, 0, "s")
-        stage2(2, 1)
-        relu_out(2, 1, "v")
-        root(0)
-        stage2(3, 0)
-        relu_out(3, 0, "s")
-        stage2(3, 1)
-        relu_out(3, 1, "v")
-        add_eps(0, "s")
-        reciprocal(0)
-        quant_h(3)
-        quant_h(4)
-        squares(2, "s")
-        scale_out(0, None, "g")
-        scale_out(1, None, "g")
-        stage1(10, 0)
-        relu_h(10, 0, "v")
-        stage1(10, 1)
-        relu_h(10, 1, "v")
-        transpose_y(12)
-        copy_y(12, "v")
-        transpose_y(13)
-        copy_y(13, "s")
-        squares(3, "s")
-        stage2(4, 0)
-        relu_out(4, 0, "s")
-        stage2(4, 1)
-        relu_out(4, 1, "v")
-        root(1)
-        stage2(5, 0)
-        relu_out(5, 0, "s")
-        stage2(5, 1)
-        relu_out(5, 1, "v")
-        add_eps(1, "s")
-        reciprocal(1)
-        quant_y(6)
-        squares(4, "s")
-        scale_out(2, None, "g")
-        scale_out(3, None, "g")
-        stage1(11, 0)
-        relu_h(11, 0, "v")
-        stage1(11, 1)
-        relu_h(11, 1, "v")
-        transpose_y(14)
-        copy_y(14, "v")
-        transpose_y(15)
-        copy_y(15, "s")
-        squares(5, "s")
-        stage2(6, 0)
-        relu_out(6, 0, "s")
-        stage2(6, 1)
-        relu_out(6, 1, "v")
-        root(2)
-        stage2(7, 0)
-        relu_out(7, 0, "s")
-        stage2(7, 1)
-        relu_out(7, 1, "v")
-        add_eps(2, "s")
-        reciprocal(2)
-        quant_h(5)
-        quant_y(7)
-        squares(6, "s")
-        scale_out(4, None, "g")
-        scale_out(5, None, "g")
-        stage1(12, 0)
-        relu_h(12, 0, "v")
-        stage1(12, 1)
-        relu_h(12, 1, "v")
-        squares(7, "s")
-        stage2(8, 0)
-        relu_out(8, 0, "s")
-        stage2(8, 1)
-        relu_out(8, 1, "v")
-        root(3)
-        stage2(9, 0)
-        relu_out(9, 0, "s")
-        stage2(9, 1)
-        relu_out(9, 1, "v")
-        add_eps(3, "s")
-        reciprocal(3)
-        squares(8, "s")
-        scale_out(6, None, "g")
-        scale_out(7, None, "g")
-        stage1(13, 0)
-        relu_h(13, 0, "v")
-        stage1(13, 1)
-        relu_h(13, 1, "v")
-        squares(9, "s")
-        stage2(10, 0)
-        relu_out(10, 0, "s")
-        stage2(10, 1)
-        relu_out(10, 1, "v")
-        root(4)
-        stage2(11, 0)
-        relu_out(11, 0, "s")
-        stage2(11, 1)
-        relu_out(11, 1, "v")
-        add_eps(4, "s")
-        reciprocal(4)
-        quant_h(6)
-        squares(10, "s")
-        scale_out(8, None, "g")
-        scale_out(9, None, "g")
-        stage1(14, 0)
-        relu_h(14, 0, "v")
-        stage1(14, 1)
-        relu_h(14, 1, "v")
-        squares(11, "s")
-        stage1(15, 0)
-        relu_h(15, 0, "v")
-        stage1(15, 1)
-        relu_h(15, 1, "v")
-        stage2(12, 0)
-        relu_out(12, 0, "s")
+        stage2(1, 1, "scalar")
+        stage1(8, 0, "vector")
+        squares(0, "scalar")
+        stage1(8, 1, "vector")
+        quantise_y(5)
+        quantise_h(2)
+        squares(1, "scalar")
+        stage1(9, 0, "vector")
+        stage1(9, 1, "vector")
+
+        for f in range(1, PAIRS - 2):
+            a, b, i = B * f, B * f + 1, 9 + f
+            stage2(a, 0, "scalar")
+            stage2(a, 1, "vector")
+            root(f - 1)
+            stage2(b, 0, "scalar")
+            stage2(b, 1, "vector")
+            add_eps(f - 1)
+            reciprocal(f - 1)
+            for p in [p for p in h_turned if B * p + 1 < i]:
+                quantise_h(p)
+            for p in list(y_turned):
+                quantise_y(p)
+            squares(a, "scalar")
+            scale_and_store(a - 2, "gpsimd")
+            scale_and_store(a - 1, "gpsimd")
+            stage1(i, 0, "vector")
+            stage1(i, 1, "vector")
+            if f <= 2:
+                turn_y(B * (f + 5), "vector")
+                turn_y(B * (f + 5) + 1, "scalar")
+            squares(b, "scalar")
+
+        low, high = slice(0, BANK), slice(BANK, D)
+        stage1(15, 0, "vector")
+        stage1(15, 1, "vector")
+        stage2(12, 0, "scalar")
         root(5)
-        stage2(12, 1)
-        relu_out(12, 1, "s")
-        add_eps(5, "s")
-        stage2(13, 1)
-        relu_out(13, 1, "v")
-        quant_h(7)
+        stage2(12, 1, "scalar")
+        add_eps(5)
+        stage2(13, 1, "vector")
+        quantise_h(7)
         reciprocal(5)
-        stage2(13, 0)
-        relu_out(13, 0, "s")
-        squares(12, "s")
-        scale_out(10, None, "v")
-        scale_out(11, None, "g")
-        stage2(14, 0)
-        relu_out(14, 0, "v")
-        squares(13, "s")
-        stage2(14, 1)
-        relu_out(14, 1, "v")
-        stage2(15, 0)
-        relu_out(15, 0, "v")
+        stage2(13, 0, "scalar")
+        squares(12, "scalar")
+        scale_and_store(10, "vector")
+        scale_and_store(11, "gpsimd")
+        stage2(14, 0, "vector")
+        squares(13, "scalar")
+        stage2(14, 1, "vector")
+        stage2(15, 0, "vector")
         root(6)
-        squares(14, "s", 0)
-        add_eps(6, "s")
-        stage2(15, 1)
-        relu_out(15, 1, "v")
-        squares(14, "s", 1)
+        squares(14, "scalar", 0)
+        add_eps(6)
+        stage2(15, 1, "vector")
+        squares(14, "scalar", 1)
         reciprocal(6)
-        scale_out(12, None, "v")
-        squares(15, "s", 0)
-        root_of_halves(14)
-        squares(15, "v", 1)
-        add_eps(7, "s")
-        scale_out(13, None, "v")
-        root_of_halves(15)
+        scale_and_store(12, "vector")
+        squares(15, "scalar", 0)
+        root(7)
+        squares(15, "vector", 1)
+        add_eps(7)
+        scale_and_store(13, "vector")
+        root(8)
         reciprocal(7)
-        add_eps(8, "s")
-        scale_out(14, None, "v")
+        add_eps(8)
+        scale_and_store(14, "vector")
         reciprocal(8)
-        scale_out(15, 1, "v")
-        scale_out(15, 0, "v")
+        scale_and_store(15, "vector", high)
+        scale_and_store(15, "vector", low)

@@ -260,8 +260,8 @@ def tile_mybadtransfomerblock_pa_kernel(tc, x, pos_emb, enc_w0, enc_w1_bytes, en
         def add_eps(group):
             nc.scalar.activation(out=factors[group][:], in_=factors[group][:], func=ACT.Copy, bias=EPS)
 
-        def reciprocal(group):
-            nc.vector.reciprocal(out=factors[group][:], in_=factors[group][:])
+        def reciprocal(group, cols=slice(0, B)):
+            nc.vector.reciprocal(out=factors[group][:, cols], in_=factors[group][:, cols])
 
         def scale_and_store(i, engine, cols=slice(0, D)):
             group, n = PLACE[i]
@@ -395,11 +395,11 @@ def tile_mybadtransfomerblock_pa_kernel(tc, x, pos_emb, enc_w0, enc_w1_bytes, en
             stage2(b, 0, "scalar")
             stage2(b, 1, "vector")
             add_eps(f - 1)
-            reciprocal(f - 1)
             for p in [p for p in h_turned if B * p + 1 < i]:
                 quantise_h(p)
             for p in list(y_turned):
                 quantise_y(p)
+            reciprocal(f - 1)
             squares(a, "scalar")
             scale_and_store(a - 2, "gpsimd")
             scale_and_store(a - 1, "gpsimd")
@@ -419,10 +419,11 @@ def tile_mybadtransfomerblock_pa_kernel(tc, x, pos_emb, enc_w0, enc_w1_bytes, en
         add_eps(5)
         stage2(13, 1, "vector")
         quantise_h(7)
-        reciprocal(5)
+        reciprocal(5, first)
         stage2(13, 0, "scalar")
         squares(12, "scalar")
         scale_and_store(10, "vector")
+        reciprocal(5, second)
         scale_and_store(11, "gpsimd")
         stage2(14, 0, "vector")
         squares(13, "scalar")
@@ -441,9 +442,9 @@ def tile_mybadtransfomerblock_pa_kernel(tc, x, pos_emb, enc_w0, enc_w1_bytes, en
         add_eps(7)
         scale_and_store(13, "vector")
         root(8)
-        reciprocal(7)
+        reciprocal(7, first)
         add_eps(8)
         scale_and_store(14, "vector")
-        reciprocal(8)
+        reciprocal(8, first)
         scale_and_store(15, "vector", high)
         scale_and_store(15, "vector", low)

@@ -29,7 +29,8 @@ WIDE = 22
 WORDS = D // 4
 
 W1_STEPS = {1: (4,), 2: (5, 6), 3: (7,)}
-GROUPS = [(B * f, B * f + 1) for f in range(PAIRS - 1)] + [(TILES - 2,), (TILES - 1,)]
+PAIRED = 6
+GROUPS = [(B * f, B * f + 1) for f in range(PAIRED)] + [(i,) for i in range(B * PAIRED, TILES)]
 PLACE = {i: (group, n) for group, tiles in enumerate(GROUPS) for n, i in enumerate(tiles)}
 
 
@@ -57,14 +58,19 @@ def tile_mybadtransfomerblock_pa_kernel(tc, x, pos_emb, enc_w0, enc_w1_bytes, en
 
         x_in, pos_in, w0_in, w1_in = {}, {}, {}, {}
         y_rows, y_turned, y_codes, y_scales = {}, {}, {}, {}
-        w0_turned, w1_rows, w1_turned = {}, {}, {}
+        w0_turned, w1_rows, w1_sorted, w1_turned = {}, {}, {}, {}
         h_turned, h_codes, h_scales = {}, {}, {}
-        h2, sums, factors = {}, {}, {}
-        banks_used = []
+        h2, z_bank, sums, factors = {}, {}, {}, {}
+        banks_used, held, halved = [], [], set()
 
         def next_bank():
             banks_used.append(psum.tile([P, BANK], F32, tag="bank%d" % (len(banks_used) % BANKS), name="bank"))
             return banks_used[-1]
+
+        def empty(step, hold):
+            held.append(step)
+            while held and not hold:
+                held.pop()()
 
         def relu(engine, dst, src):
             if engine == "scalar":
@@ -123,29 +129,36 @@ def tile_mybadtransfomerblock_pa_kernel(tc, x, pos_emb, enc_w0, enc_w1_bytes, en
             words = rows[:].bitcast(F32)
             return lambda g, u: words[:, 2 * P * g + u : 2 * P * (g + 1) : 2]
 
-        def turn_y(i, engine):
+        def turn_y(i, engine, hold=False):
             p, b = divmod(i, B)
             words = y_rows[p][:, :, b].bitcast(F32)
             bank = transpose_words(lambda g, u: words[:, u, g * P : (g + 1) * P])
             if b == 0:
                 y_turned[p] = work.tile([P, B, D], BF16, tag="wide", bufs=WIDE, name="y_turned", align_bytes=64)
-            copy_words(engine, bank, y_turned[p][:, b].bitcast(F32).rearrange("p (g n) -> p g n", g=PASSES))
+            dst = y_turned[p][:, b].bitcast(F32).rearrange("p (g n) -> p g n", g=PASSES)
+            empty(lambda: copy_words(engine, bank, dst), hold)
 
-        def turn_w0(c):
+        def turn_w0(c, hold=False):
             q, e = divmod(c, 2)
             bank = transpose_words(every_second_word(w0_in.pop(c)))
             if e == 0:
                 w0_turned[q] = work.tile([P, 2, D], BF16, tag="wide", bufs=WIDE, name="w0_turned", align_bytes=64)
-            copy_words("scalar", bank, w0_turned[q][:, e].bitcast(F32).rearrange("p (g n) -> p g n", g=PASSES))
+            dst = w0_turned[q][:, e].bitcast(F32).rearrange("p (g n) -> p g n", g=PASSES)
+            empty(lambda: copy_words("scalar", bank, dst), hold)
 
-        def turn_w1(a):
+        def turn_w1(a, hold=False):
             q, e = divmod(a, 2)
-            bank = transpose_words(every_second_word(w1_rows.pop(a)))
+            if a in w1_sorted:
+                words = w1_sorted.pop(a)
+                bank = transpose_words(lambda g, u: words[:, u, g * P : (g + 1) * P])
+            else:
+                bank = transpose_words(every_second_word(w1_rows.pop(a)))
             if e == 0:
                 w1_turned[q] = work.tile([P, PASSES, 2, P * 4], BF16, tag="wide", bufs=WIDE, name="w1_turned", align_bytes=64)
-            copy_words("scalar", bank, w1_turned[q][:, :, e].bitcast(F32))
+            dst = w1_turned[q][:, :, e].bitcast(F32)
+            empty(lambda: copy_words("scalar", bank, dst), hold)
 
-        def stage1(i, h, engine):
+        def stage1(i, h, engine, hold=False):
             p, b = divmod(i, B)
             bank = next_bank()
             for t in range(4):
@@ -162,9 +175,9 @@ def tile_mybadtransfomerblock_pa_kernel(tc, x, pos_emb, enc_w0, enc_w1_bytes, en
             if p not in h_turned:
                 h_turned[p] = work.tile([P, B, PASSES, P, 4], BF16, tag="wide", bufs=WIDE, name="h_turned", align_bytes=64)
             dst = h_turned[p][:, b, h].rearrange("p (c i) t -> p c t i", i=2)
-            relu(engine, dst, bank[:].rearrange("p (t c i) -> p c t i", t=4, i=2))
+            empty(lambda: relu(engine, dst, bank[:].rearrange("p (t c i) -> p c t i", t=4, i=2)), hold)
 
-        def stage2(i, n, engine):
+        def stage2(i, n, engine, hold=False):
             p, b = divmod(i, B)
             cols = slice(n * BANK, (n + 1) * BANK)
             bank = next_bank()
@@ -180,7 +193,8 @@ def tile_mybadtransfomerblock_pa_kernel(tc, x, pos_emb, enc_w0, enc_w1_bytes, en
                 )
             if i not in h2:
                 h2[i] = work.tile([P, D], F32, tag="wide", bufs=WIDE, name="h2", align_bytes=64)
-            relu(engine, h2[i][:, cols], bank[:])
+            z_bank[i, n] = bank
+            empty(lambda: relu(engine, h2[i][:, cols], bank[:]), hold)
 
         def add_pos(p, batches=slice(0, B)):
             if p not in y_rows:
@@ -195,8 +209,13 @@ def tile_mybadtransfomerblock_pa_kernel(tc, x, pos_emb, enc_w0, enc_w1_bytes, en
             )
 
         def scale_w1(a):
-            w1_rows[a] = work.tile([P, D], BF16, tag="w1_rows", name="w1_rows", bufs=CHUNKS)
+            w1_rows[a] = work.tile([P, D], BF16, tag="w1_rows", name="w1_rows", bufs=6)
             nc.vector.tensor_tensor(out=w1_rows[a][:], in0=w1_in.pop(a)[:].bitcast(FP8), in1=w1_scale[:], op=MULT)
+
+        def sort_w1(a):
+            w1_sorted[a] = work.tile([P, 2, D // 4], F32, tag="w1_sorted", name="w1_sorted", bufs=2)
+            words = w1_rows.pop(a)[:].bitcast(F32)
+            nc.vector.tensor_copy(out=w1_sorted[a][:], in_=words.rearrange("p (w u) -> p u w", u=2))
 
         def quantise_pair(p, values, codes, scales, tag, bufs):
             codes[p] = work.tile([P, B, WORDS], U32, tag=tag + "_codes", name="codes", align_bytes=256, bufs=bufs)
@@ -210,8 +229,18 @@ def tile_mybadtransfomerblock_pa_kernel(tc, x, pos_emb, enc_w0, enc_w1_bytes, en
         def quantise_y(p):
             quantise_pair(p, y_turned.pop(p)[:].rearrange("p b n -> p (b n)"), y_codes, y_scales, "y", 4)
 
-        def quantise_h(p):
-            quantise_pair(p, h_turned.pop(p)[:].rearrange("p b h n t -> p (b h n t)"), h_codes, h_scales, "h", PAIRS)
+        def quantise_h(p, b=None):
+            if b is None:
+                quantise_pair(p, h_turned.pop(p)[:].rearrange("p b h n t -> p (b h n t)"), h_codes, h_scales, "h", PAIRS)
+                return
+            if p not in h_codes:
+                h_codes[p] = work.tile([P, B, WORDS], U32, tag="h_codes", name="codes", align_bytes=256, bufs=PAIRS)
+                h_scales[p] = work.tile([P, B, WORDS], U8, tag="h_scales", name="scales", align_bytes=256, bufs=PAIRS)
+            nc.vector.quantize_mx(
+                out=h_codes[p][:, b].bitcast(FP8X4),
+                scales=h_scales[p][:, b],
+                in_=h_turned[p][:, b].rearrange("p h n t -> p (h n t)"),
+            )
 
         def quantise_w0(q):
             nc.vector.quantize_mx(
@@ -236,6 +265,8 @@ def tile_mybadtransfomerblock_pa_kernel(tc, x, pos_emb, enc_w0, enc_w1_bytes, en
                 sums[group] = work.tile([P, 4], F32, tag="sums", name="sums", bufs=len(GROUPS))
             cols = slice(0, D) if half is None else slice(half * BANK, (half + 1) * BANK)
             slot = n if half is None else n + 2 * half
+            if half is not None:
+                halved.add(group)
             total = sums[group][:, slot : slot + 1]
             values = h2[i][:, cols]
             if engine == "scalar":
@@ -244,21 +275,26 @@ def tile_mybadtransfomerblock_pa_kernel(tc, x, pos_emb, enc_w0, enc_w1_bytes, en
             else:
                 squared = work.tile([P, D], BF16, tag="squared_v", name="squared", bufs=1)
                 nc.vector.scalar_tensor_tensor(
-                    out=squared[:, cols], in0=values, scalar=1.0, in1=values, op0=MULT, op1=MULT, accum_out=total
+                    out=squared[:, cols], in0=z_bank[i, half][:], scalar=0.0, in1=values, op0=MAX, op1=MULT, accum_out=total
                 )
 
         def root(group):
             count = len(GROUPS[group])
             factors[group] = work.tile([P, count], F32, tag="factors", name="factors", bufs=len(GROUPS))
-            if count == B:
+            if group not in halved:
                 nc.scalar.activation(out=factors[group][:], in_=sums[group][:, 0:count], func=ACT.Sqrt)
             else:
                 nc.scalar.activation(
                     out=factors[group][:], in_=sums[group][:, 0:1], func=ACT.Sqrt, bias=sums[group][:, 2:3]
                 )
 
-        def add_eps(group):
-            nc.scalar.activation(out=factors[group][:], in_=factors[group][:], func=ACT.Copy, bias=EPS)
+        def add_eps(group, engine="scalar"):
+            if engine == "scalar":
+                nc.scalar.activation(out=factors[group][:], in_=factors[group][:], func=ACT.Copy, bias=EPS)
+            elif engine == "vector":
+                nc.vector.tensor_scalar(out=factors[group][:], in0=factors[group][:], scalar1=EPS, scalar2=None, op0=ADD)
+            else:
+                nc.gpsimd.tensor_scalar(out=factors[group][:], in0=factors[group][:], scalar1=1.0, scalar2=EPS, op0=MULT, op1=ADD)
 
         def reciprocal(group, cols=slice(0, B)):
             nc.vector.reciprocal(out=factors[group][:, cols], in_=factors[group][:, cols])
@@ -268,6 +304,8 @@ def tile_mybadtransfomerblock_pa_kernel(tc, x, pos_emb, enc_w0, enc_w1_bytes, en
             values, factor = h2[i][:, cols], factors[group][:, n : n + 1]
             if engine == "vector":
                 nc.vector.tensor_scalar(out=values, in0=values, scalar1=factor, scalar2=None, op0=MULT)
+            elif engine == "scalar":
+                nc.scalar.activation(out=values, in_=values, func=ACT.Copy, scale=factor)
             else:
                 nc.gpsimd.tensor_scalar(out=values, in0=values, scalar1=factor, scalar2=0.0, op0=MULT, op1=ADD)
             p, b = divmod(i, B)
@@ -323,32 +361,35 @@ def tile_mybadtransfomerblock_pa_kernel(tc, x, pos_emb, enc_w0, enc_w1_bytes, en
         quantise_w0(3)
         turn_y(2, "scalar")
         turn_y(3, "scalar")
+        scale_w1(4)
         add_pos(2)
+        sort_w1(4)
         turn_w1(3)
         stage1(0, 1, "scalar")
-        scale_w1(4)
-        stage1(1, 1, "scalar")
         quantise_y(1)
-
+        stage1(1, 1, "scalar")
         turn_y(4, "scalar")
         turn_y(5, "scalar")
         scale_w1(5)
         turn_w1(4)
         add_pos(3)
+        sort_w1(5)
         stage1(2, 0, "scalar")
         stage1(2, 1, "scalar")
-        scale_w1(6)
-        stage1(3, 0, "scalar")
         quantise_y(2)
+        stage1(3, 0, "scalar")
+        scale_w1(6)
         stage1(3, 1, "scalar")
 
         turn_w1(5)
         turn_y(6, "scalar")
         turn_y(7, "scalar")
         scale_w1(7)
+        sort_w1(6)
         stage1(4, 0, "scalar")
         stage1(4, 1, "scalar")
         add_pos(4)
+        sort_w1(7)
         quantise_w1(0)
         turn_w1(6)
         stage1(5, 0, "scalar")
@@ -378,73 +419,89 @@ def tile_mybadtransfomerblock_pa_kernel(tc, x, pos_emb, enc_w0, enc_w1_bytes, en
         stage2(1, 0, "scalar")
         add_pos(7)
         stage2(1, 1, "scalar")
-        stage1(8, 0, "vector")
         squares(0, "scalar")
-        stage1(8, 1, "vector")
-        quantise_y(5)
         quantise_h(2)
+        quantise_y(5)
+        stage1(8, 0, "vector")
+        stage1(8, 1, "vector")
+        quantise_h(3)
         squares(1, "scalar")
         stage1(9, 0, "vector")
         stage1(9, 1, "vector")
 
+        V, S, G = "vector", "scalar", "gpsimd"
+        low, high = slice(0, BANK), slice(BANK, D)
         for f in range(1, PAIRS - 2):
             a, b, i = B * f, B * f + 1, 9 + f
-            stage2(a, 0, "scalar")
-            stage2(a, 1, "vector")
+            stage2(a, 0, S)
             root(f - 1)
-            stage2(b, 0, "scalar")
-            stage2(b, 1, "vector")
+            stage2(a, 1, V)
+            stage2(b, 0, V if f in (2,) else S)
             add_eps(f - 1)
+            stage2(b, 1, V)
             for p in [p for p in h_turned if B * p + 1 < i]:
                 quantise_h(p)
             for p in list(y_turned):
                 quantise_y(p)
-            reciprocal(f - 1)
-            squares(a, "scalar")
-            scale_and_store(a - 2, "gpsimd")
-            scale_and_store(a - 1, "gpsimd")
-            stage1(i, 0, "vector")
-            stage1(i, 1, "vector")
+            reciprocal(f - 1, slice(0, B) if f < 4 else first)
+            squares(a, S)
+            if f == 4:
+                stage1(i, 0, V)
+                scale_and_store(a - 2, V)
+                reciprocal(f - 1, second)
+                scale_and_store(a - 1, G)
+                stage1(i, 1, V)
+            else:
+                scale_and_store(a - 2, G)
+                if f < 5:
+                    scale_and_store(a - 1, G)
+                stage1(i, 0, V)
+                stage1(i, 1, V)
+            squares(b, S)
             if f <= 2:
-                turn_y(B * (f + 5), "vector")
-                turn_y(B * (f + 5) + 1, "scalar")
-            squares(b, "scalar")
-
-        low, high = slice(0, BANK), slice(BANK, D)
-        stage1(15, 0, "vector")
-        stage1(15, 1, "vector")
-        stage2(12, 0, "scalar")
+                turn_y(B * (f + 5), V)
+                turn_y(B * (f + 5) + 1, S)
+        stage1(15, 0, V)
+        stage1(15, 1, S)
         root(5)
-        stage2(12, 1, "scalar")
+        reciprocal(4, second)
+        quantise_h(7, 0)
+        scale_and_store(9, V)
+        stage2(12, 0, S)
         add_eps(5)
-        stage2(13, 1, "vector")
-        quantise_h(7)
+        quantise_h(7, 1)
+        stage2(12, 1, S)
         reciprocal(5, first)
-        stage2(13, 0, "scalar")
-        squares(12, "scalar")
-        scale_and_store(10, "vector")
+        stage2(13, 0, V)
+        scale_and_store(10, V)
         reciprocal(5, second)
-        scale_and_store(11, "gpsimd")
-        stage2(14, 0, "vector")
-        squares(13, "scalar")
-        stage2(14, 1, "vector")
-        stage2(15, 0, "vector")
+        scale_and_store(11, G)
+        squares(12, S)
+        stage2(13, 1, V)
+        stage2(14, 0, V)
         root(6)
-        squares(14, "scalar", 0)
+        squares(13, S, 0)
         add_eps(6)
-        stage2(15, 1, "vector")
-        squares(14, "scalar", 1)
-        reciprocal(6)
-        scale_and_store(12, "vector")
-        squares(15, "scalar", 0)
+        squares(13, S, 1)
+        stage2(14, 1, V)
+        reciprocal(6, first)
+        stage2(15, 0, V)
+        squares(14, S, 0)
         root(7)
-        squares(15, "vector", 1)
+        scale_and_store(12, V)
+        stage2(15, 1, S)
         add_eps(7)
-        scale_and_store(13, "vector")
-        root(8)
+        squares(14, S, 1)
         reciprocal(7, first)
+        squares(15, V, 1)
+        root(8)
+        squares(15, S, 0)
         add_eps(8)
-        scale_and_store(14, "vector")
+        scale_and_store(13, V)
+        root(9)
         reciprocal(8, first)
-        scale_and_store(15, "vector", high)
-        scale_and_store(15, "vector", low)
+        add_eps(9)
+        scale_and_store(14, V)
+        reciprocal(9, first)
+        scale_and_store(15, V, high)
+        scale_and_store(15, V, low)

@@ -316,8 +316,8 @@ def tile_mybadtransfomerblock_pa_kernel(tc, x, pos_emb, enc_w0, enc_w1_bytes, en
         load_x(0, first)
         load_pos(0)
         load_w0(0)
-        load_x(0, second)
         load_w1(0)
+        load_x(0, second)
         load_w0(1)
         for q in range(1, CHUNKS // 2):
             load_w1(q)
@@ -333,14 +333,14 @@ def tile_mybadtransfomerblock_pa_kernel(tc, x, pos_emb, enc_w0, enc_w1_bytes, en
         for half in range(2):
             copy_scale(half, scale_banks[half])
         add_pos(0, first)
+        scale_w1(0)
         add_pos(0, second)
         turn_y(0, "scalar")
         turn_w0(0)
-        turn_y(1, "scalar")
-        scale_w1(0)
         turn_w0(1)
-        scale_w1(1)
         turn_w1(0)
+        turn_y(1, "scalar")
+        scale_w1(1)
         turn_w0(2)
         turn_w0(3)
         scale_w1(2)
@@ -356,6 +356,7 @@ def tile_mybadtransfomerblock_pa_kernel(tc, x, pos_emb, enc_w0, enc_w1_bytes, en
         turn_w1(2)
         stage1(0, 0, "scalar")
         quantise_w0(2)
+        sort_w1(3)
         add_pos(1)
         stage1(1, 0, "scalar")
         quantise_w0(3)
@@ -368,66 +369,66 @@ def tile_mybadtransfomerblock_pa_kernel(tc, x, pos_emb, enc_w0, enc_w1_bytes, en
         stage1(0, 1, "scalar")
         quantise_y(1)
         stage1(1, 1, "scalar")
-        turn_y(4, "scalar")
+        turn_y(4, "scalar", hold=True)
         turn_y(5, "scalar")
         scale_w1(5)
         turn_w1(4)
         add_pos(3)
         sort_w1(5)
-        stage1(2, 0, "scalar")
+        stage1(2, 0, "scalar", hold=True)
         stage1(2, 1, "scalar")
         quantise_y(2)
-        stage1(3, 0, "scalar")
+        stage1(3, 0, "scalar", hold=True)
         scale_w1(6)
         stage1(3, 1, "scalar")
 
         turn_w1(5)
-        turn_y(6, "scalar")
+        turn_y(6, "scalar", hold=True)
         turn_y(7, "scalar")
-        scale_w1(7)
-        sort_w1(6)
-        stage1(4, 0, "scalar")
-        stage1(4, 1, "scalar")
         add_pos(4)
-        sort_w1(7)
-        quantise_w1(0)
-        turn_w1(6)
-        stage1(5, 0, "scalar")
-        quantise_y(3)
+        sort_w1(6)
+        stage1(4, 0, "scalar", hold=True)
+        stage1(4, 1, "scalar")
+        scale_w1(7)
+        stage1(5, 0, "scalar", hold=True)
         stage1(5, 1, "scalar")
+        quantise_y(3)
+        add_pos(5)
+        sort_w1(7)
+
+        turn_w1(6)
+        turn_y(8, "scalar", hold=True)
+        turn_y(9, "scalar")
+        quantise_w1(0)
+        quantise_h(0)
         quantise_w1(1)
+        stage1(6, 0, "scalar", hold=True)
+        stage1(6, 1, "scalar")
+        quantise_y(4)
+        stage1(7, 0, "scalar", hold=True)
+        stage1(7, 1, "scalar")
+        quantise_w1(2)
+        add_pos(6)
 
         turn_w1(7)
-        turn_y(8, "scalar")
-        turn_y(9, "scalar")
-        add_pos(5)
-        quantise_w1(2)
-        stage1(6, 0, "scalar")
-        stage1(6, 1, "scalar")
-        quantise_h(0)
-        stage1(7, 0, "scalar")
-        quantise_y(4)
-        stage1(7, 1, "scalar")
-        quantise_w1(3)
-
-        turn_y(10, "scalar")
+        turn_y(10, "scalar", hold=True)
         turn_y(11, "scalar")
-        add_pos(6)
-        stage2(0, 0, "scalar")
-        stage2(0, 1, "scalar")
-        quantise_h(1)
+        stage2(0, 0, "scalar", hold=True)
         stage2(1, 0, "scalar")
+        quantise_w1(3)
+        quantise_h(1)
         add_pos(7)
+        stage1(8, 0, "vector", hold=True)
+        stage1(8, 1, "vector")
+        stage2(0, 1, "scalar")
         stage2(1, 1, "scalar")
         squares(0, "scalar")
         quantise_h(2)
         quantise_y(5)
-        stage1(8, 0, "vector")
-        stage1(8, 1, "vector")
-        quantise_h(3)
         squares(1, "scalar")
-        stage1(9, 0, "vector")
+        stage1(9, 0, "vector", hold=True)
         stage1(9, 1, "vector")
+        quantise_h(3)
 
         V, S, G = "vector", "scalar", "gpsimd"
         low, high = slice(0, BANK), slice(BANK, D)
@@ -443,7 +444,7 @@ def tile_mybadtransfomerblock_pa_kernel(tc, x, pos_emb, enc_w0, enc_w1_bytes, en
                 quantise_h(p)
             for p in list(y_turned):
                 quantise_y(p)
-            reciprocal(f - 1, slice(0, B) if f < 4 else first)
+            reciprocal(f - 1, first if f == 4 else slice(0, B))
             squares(a, S)
             if f == 4:
                 stage1(i, 0, V)
@@ -453,29 +454,26 @@ def tile_mybadtransfomerblock_pa_kernel(tc, x, pos_emb, enc_w0, enc_w1_bytes, en
                 stage1(i, 1, V)
             else:
                 scale_and_store(a - 2, G)
-                if f < 5:
-                    scale_and_store(a - 1, G)
-                stage1(i, 0, V)
+                scale_and_store(a - 1, G)
+                stage1(i, 0, V, hold=True)
                 stage1(i, 1, V)
             squares(b, S)
             if f <= 2:
                 turn_y(B * (f + 5), V)
                 turn_y(B * (f + 5) + 1, S)
-        stage1(15, 0, V)
-        stage1(15, 1, S)
+        stage1(15, 0, V, hold=True)
+        stage1(15, 1, V)
         root(5)
-        reciprocal(4, second)
-        quantise_h(7, 0)
-        scale_and_store(9, V)
         stage2(12, 0, S)
         add_eps(5)
-        quantise_h(7, 1)
-        stage2(12, 1, S)
+        stage2(12, 1, V)
+        quantise_h(7, 0)
         reciprocal(5, first)
-        stage2(13, 0, V)
+        quantise_h(7, 1)
         scale_and_store(10, V)
         reciprocal(5, second)
         scale_and_store(11, G)
+        stage2(13, 0, S)
         squares(12, S)
         stage2(13, 1, V)
         stage2(14, 0, V)
@@ -485,23 +483,23 @@ def tile_mybadtransfomerblock_pa_kernel(tc, x, pos_emb, enc_w0, enc_w1_bytes, en
         squares(13, S, 1)
         stage2(14, 1, V)
         reciprocal(6, first)
+        root(7)
         stage2(15, 0, V)
         squares(14, S, 0)
-        root(7)
-        scale_and_store(12, V)
-        stage2(15, 1, S)
         add_eps(7)
+        scale_and_store(12, V)
         squares(14, S, 1)
         reciprocal(7, first)
-        squares(15, V, 1)
+        stage2(15, 1, V)
         root(8)
+        scale_and_store(13, V)
         squares(15, S, 0)
         add_eps(8)
-        scale_and_store(13, V)
-        root(9)
+        squares(15, S, 1)
         reciprocal(8, first)
-        add_eps(9)
+        root(9)
         scale_and_store(14, V)
+        add_eps(9)
         reciprocal(9, first)
         scale_and_store(15, V, high)
         scale_and_store(15, V, low)

@@ -356,7 +356,6 @@ def tile_mybadtransfomerblock_pa_kernel(tc, x, pos_emb, enc_w0, enc_w1_bytes, en
         turn_w1(2)
         stage1(0, 0, "scalar")
         quantise_w0(2)
-        sort_w1(3)
         add_pos(1)
         stage1(1, 0, "scalar")
         quantise_w0(3)
@@ -418,7 +417,7 @@ def tile_mybadtransfomerblock_pa_kernel(tc, x, pos_emb, enc_w0, enc_w1_bytes, en
         quantise_w1(3)
         quantise_h(1)
         add_pos(7)
-        stage1(8, 0, "vector", hold=True)
+        stage1(8, 0, "scalar")
         stage1(8, 1, "vector")
         stage2(0, 1, "scalar")
         stage2(1, 1, "scalar")

@@ -23,13 +23,14 @@ PASSES = 2
 TILES = B * S // P
 PAIRS = TILES // B
 CHUNKS = D // P
+QUARTERS = CHUNKS // 2
 BANKS = 8
 BANK = 512
-WIDE = 22
+WIDE = 20
 WORDS = D // 4
+V, SC, G = "vector", "scalar", "gpsimd"
 
-W1_STEPS = {1: (4,), 2: (5, 6), 3: (7,)}
-PAIRED = 6
+PAIRED = 4
 GROUPS = [(B * f, B * f + 1) for f in range(PAIRED)] + [(i,) for i in range(B * PAIRED, TILES)]
 PLACE = {i: (group, n) for group, tiles in enumerate(GROUPS) for n, i in enumerate(tiles)}
 
@@ -49,8 +50,7 @@ def tile_mybadtransfomerblock_pa_kernel(tc, x, pos_emb, enc_w0, enc_w1_bytes, en
         unread = keep.tile([P, 1], F32, tag="unread")
         nc.scalar.activation(out=unread[:], in_=one[:], func=ACT.Sqrt)
 
-        scale_cols = keep.tile([P, CHUNKS], F32, tag="scale_cols")
-        w1_scale = keep.tile([P, D], F32, tag="w1_scale")
+        w1_scale = keep.tile([P, PASSES, 4], F32, tag="w1_scale")
         w0_codes = keep.tile([P, CHUNKS, PASSES, P], U32, tag="w0_codes", align_bytes=256)
         w0_scales = keep.tile([P, CHUNKS, PASSES, P], U8, tag="w0_scales", align_bytes=256)
         w1_codes = keep.tile([P, PASSES, D], U32, tag="w1_codes", align_bytes=256)
@@ -58,22 +58,28 @@ def tile_mybadtransfomerblock_pa_kernel(tc, x, pos_emb, enc_w0, enc_w1_bytes, en
 
         x_in, pos_in, w0_in, w1_in = {}, {}, {}, {}
         y_rows, y_turned, y_codes, y_scales = {}, {}, {}, {}
-        w0_turned, w1_rows, w1_sorted, w1_turned = {}, {}, {}, {}
+        w0_turned, w1_rows, w1_unsorted, w1_bank, w1_turned, w1_sorted = {}, {}, {}, {}, {}, set()
         h_turned, h_codes, h_scales = {}, {}, {}
         h2, z_bank, sums, factors = {}, {}, {}, {}
-        banks_used, held, halved = [], [], set()
+        free_banks, held, halved = list(range(BANKS)), [], set()
+
+        def wide(shape, dtype, name, tag="wide", bufs=WIDE):
+            return work.tile(shape, dtype, tag=tag, bufs=bufs, name=name, align_bytes=64)
 
         def next_bank():
-            banks_used.append(psum.tile([P, BANK], F32, tag="bank%d" % (len(banks_used) % BANKS), name="bank"))
-            return banks_used[-1]
+            number = free_banks.pop(0)
+            bank = psum.tile([P, BANK], F32, tag="bank%d" % number, name="bank")
+            return bank, number
 
-        def empty(step, hold):
-            held.append(step)
+        def empty(step, number, hold):
+            held.append((step, number))
             while held and not hold:
-                held.pop()()
+                step, number = held.pop()
+                step()
+                free_banks.append(number)
 
         def relu(engine, dst, src):
-            if engine == "scalar":
+            if engine == SC:
                 nc.scalar.activation(out=dst, in_=src, func=ACT.Relu)
             else:
                 nc.vector.tensor_scalar(out=dst, in0=src, scalar1=0.0, scalar2=None, op0=MAX)
@@ -94,73 +100,77 @@ def tile_mybadtransfomerblock_pa_kernel(tc, x, pos_emb, enc_w0, enc_w1_bytes, en
             w0_in[c] = work.tile([P, D], BF16, tag="w0_in", bufs=CHUNKS, name="w0_in")
             nc.sync.dma_start(out=w0_in[c][:], in_=w0_rows[c // 4, c % 4])
 
-        def load_w1(a):
-            w1_in[a] = work.tile([P, D], U8, tag="w1_in", bufs=CHUNKS, name="w1_in")
-            nc.sync.dma_start(out=w1_in[a][:], in_=enc_w1_bytes[a * P : (a + 1) * P, :])
+        def load_w1(q, chunks=slice(0, 2)):
+            if q not in w1_in:
+                w1_in[q] = work.tile([P, 2, D], U8, tag="w1_in", bufs=QUARTERS, name="w1_in")
+            rows = enc_w1_bytes[2 * P * q : 2 * P * (q + 1), :].rearrange("(e m) k -> m e k", e=2)
+            nc.sync.dma_start(out=w1_in[q][:, chunks], in_=rows[:, chunks])
 
-        def spread_scale(half):
-            bank = next_bank()
-            for j in range(4):
-                column = scale_cols[:, 4 * half + j : 4 * half + j + 1]
-                nc.tensor.transpose(bank[:, j * P : (j + 1) * P], column.to_broadcast([P, P]), ident[:])
-            return bank
-
-        def copy_scale(half, bank):
-            dst = w1_scale[:].rearrange("q (p j) -> q p j", j=CHUNKS)[:, :, 4 * half : 4 * half + 4]
-            nc.scalar.copy(out=dst, in_=bank[:].rearrange("q (j p) -> q p j", j=4))
-
-        def transpose_words(source):
-            bank = next_bank()
-            blocks = bank[:].rearrange("p (u g n) -> p g u n", g=PASSES, u=2)
-            for g in range(PASSES):
-                for u in range(2):
-                    nc.tensor.transpose(blocks[:, g, u, :], source(g, u), ident[:])
-            return bank
+        def load_scale():
+            nc.sync.dma_start(out=w1_scale[:], in_=enc_w1_scale.rearrange("o (g p t) -> p (o g) t", p=P, t=4))
 
         def copy_words(engine, bank, dst):
             src = bank[:].rearrange("p (u g c i) -> p g c u i", g=PASSES, u=2, i=2)
             dst = dst.rearrange("p g (c i u) -> p g c u i", u=2, i=2)
-            if engine == "scalar":
+            if engine == SC:
                 nc.scalar.copy(out=dst, in_=src)
             else:
                 nc.vector.tensor_copy(out=dst, in_=src)
 
-        def every_second_word(rows):
-            words = rows[:].bitcast(F32)
-            return lambda g, u: words[:, 2 * P * g + u : 2 * P * (g + 1) : 2]
+        def transpose_words(source):
+            bank, number = next_bank()
+            blocks = bank[:].rearrange("p (u j n) -> p j u n", j=2, u=2)
+            for j in range(2):
+                for u in range(2):
+                    nc.tensor.transpose(blocks[:, j, u, :], source(j, u), ident[:])
+            return bank, number
 
         def turn_y(i, engine, hold=False):
             p, b = divmod(i, B)
             words = y_rows[p][:, :, b].bitcast(F32)
-            bank = transpose_words(lambda g, u: words[:, u, g * P : (g + 1) * P])
+            bank, number = transpose_words(lambda g, u: words[:, u, g * P : (g + 1) * P])
             if b == 0:
-                y_turned[p] = work.tile([P, B, D], BF16, tag="wide", bufs=WIDE, name="y_turned", align_bytes=64)
+                y_turned[p] = wide([P, B, D], BF16, "y_turned", *tags.get(("y", p), ()))
             dst = y_turned[p][:, b].bitcast(F32).rearrange("p (g n) -> p g n", g=PASSES)
-            empty(lambda: copy_words(engine, bank, dst), hold)
+            empty(lambda: copy_words(engine, bank, dst), number, hold)
 
-        def turn_w0(c, hold=False):
+        def turn_w0(c, engine=SC, hold=False):
             q, e = divmod(c, 2)
-            bank = transpose_words(every_second_word(w0_in.pop(c)))
+            words = w0_in.pop(c)[:].bitcast(F32)
+            bank, number = transpose_words(lambda g, u: words[:, 2 * P * g + u : 2 * P * (g + 1) : 2])
             if e == 0:
-                w0_turned[q] = work.tile([P, 2, D], BF16, tag="wide", bufs=WIDE, name="w0_turned", align_bytes=64)
+                w0_turned[q] = wide([P, 2, D], BF16, "w0_turned", *tags.get(("w0", q), ()))
             dst = w0_turned[q][:, e].bitcast(F32).rearrange("p (g n) -> p g n", g=PASSES)
-            empty(lambda: copy_words("scalar", bank, dst), hold)
+            empty(lambda: copy_words(engine, bank, dst), number, hold)
 
-        def turn_w1(a, hold=False):
-            q, e = divmod(a, 2)
-            if a in w1_sorted:
-                words = w1_sorted.pop(a)
-                bank = transpose_words(lambda g, u: words[:, u, g * P : (g + 1) * P])
-            else:
-                bank = transpose_words(every_second_word(w1_rows.pop(a)))
-            if e == 0:
-                w1_turned[q] = work.tile([P, PASSES, 2, P * 4], BF16, tag="wide", bufs=WIDE, name="w1_turned", align_bytes=64)
-            dst = w1_turned[q][:, :, e].bitcast(F32)
-            empty(lambda: copy_words("scalar", bank, dst), hold)
+        def turn_w1(q):
+            for g in range(PASSES):
+                w1_bank[q, g] = next_bank()
+            for e in range(2):
+                words = w1_rows[q][:, e].bitcast(F32)
+                for g in range(PASSES):
+                    blocks = w1_bank[q, g][0][:].rearrange("p (u e n) -> p e u n", e=2, u=2)
+                    for u in range(2):
+                        if (q, e) in w1_sorted:
+                            block = words[:, (2 * u + g) * P : (2 * u + g + 1) * P]
+                        else:
+                            block = words[:, 2 * P * g + u : 2 * P * (g + 1) : 2]
+                        nc.tensor.transpose(blocks[:, e, u, :], block, ident[:])
+
+        def scale_w1(q, g):
+            n, j = divmod(q, 2)
+            if j == 0:
+                w1_turned[n, g] = wide([P, 2, 2 * P, 4], BF16, "w1_turned")
+            dst = w1_turned[n, g][:, j].rearrange("p r (u e) -> p r u e", u=2)
+            scales = w1_scale[:, g].unsqueeze(1).to_broadcast([P, 2 * P, 4]).rearrange("p r (u e) -> p r u e", u=2)
+            bank, number = w1_bank.pop((q, g))
+            values = bank[:].bitcast(BF16).rearrange("p (u r e) -> p r u e", u=2, e=2)
+            nc.vector.tensor_tensor(out=dst, in0=values, in1=scales, op=MULT)
+            free_banks.append(number)
 
         def stage1(i, h, engine, hold=False):
             p, b = divmod(i, B)
-            bank = next_bank()
+            bank, number = next_bank()
             for t in range(4):
                 for g in range(PASSES):
                     nc.tensor.matmul_mx(
@@ -173,14 +183,14 @@ def tile_mybadtransfomerblock_pa_kernel(tc, x, pos_emb, enc_w0, enc_w1_bytes, en
                         stop=(g == PASSES - 1),
                     )
             if p not in h_turned:
-                h_turned[p] = work.tile([P, B, PASSES, P, 4], BF16, tag="wide", bufs=WIDE, name="h_turned", align_bytes=64)
+                h_turned[p] = wide([P, B, PASSES, P, 4], BF16, "h_turned", *tags.get(("h", p), ()))
             dst = h_turned[p][:, b, h].rearrange("p (c i) t -> p c t i", i=2)
-            empty(lambda: relu(engine, dst, bank[:].rearrange("p (t c i) -> p c t i", t=4, i=2)), hold)
+            empty(lambda: relu(engine, dst, bank[:].rearrange("p (t c i) -> p c t i", t=4, i=2)), number, hold)
 
         def stage2(i, n, engine, hold=False):
             p, b = divmod(i, B)
             cols = slice(n * BANK, (n + 1) * BANK)
-            bank = next_bank()
+            bank, number = next_bank()
             for g in range(PASSES):
                 nc.tensor.matmul_mx(
                     out=bank[:],
@@ -192,72 +202,75 @@ def tile_mybadtransfomerblock_pa_kernel(tc, x, pos_emb, enc_w0, enc_w1_bytes, en
                     stop=(g == PASSES - 1),
                 )
             if i not in h2:
-                h2[i] = work.tile([P, D], F32, tag="wide", bufs=WIDE, name="h2", align_bytes=64)
+                h2[i] = wide([P, D], F32, "h2")
             z_bank[i, n] = bank
-            empty(lambda: relu(engine, h2[i][:, cols], bank[:]), hold)
+            empty(lambda: relu(engine, h2[i][:, cols], bank[:]), number, hold)
 
-        def add_pos(p, batches=slice(0, B)):
+        def widen_w1(q, engine, chunks=slice(0, 2)):
+            if q not in w1_rows:
+                w1_rows[q] = wide([P, 2, D], BF16, "w1_rows", *tags.get(("w1", q), ()))
+            dst = w1_rows[q][:, chunks].rearrange("p e k -> p (e k)")
+            src = w1_in[q][:, chunks].rearrange("p e k -> p (e k)").bitcast(FP8)
+            if engine == SC:
+                nc.scalar.copy(out=dst, in_=src)
+            elif engine == V:
+                w1_sorted.add((q, chunks.start))
+                nc.vector.tensor_scalar(
+                    out=dst.rearrange("p (u w i) -> p w u i", u=2, i=2),
+                    in0=src.rearrange("p (w u i) -> p w u i", u=2, i=2),
+                    scalar1=one[:],
+                    scalar2=None,
+                    op0=MULT,
+                )
+            else:
+                nc.gpsimd.tensor_copy(out=dst, in_=src)
+
+        def sort_w1(q, e):
+            if e == 0:
+                w1_unsorted[q] = w1_rows[q]
+                w1_rows[q] = wide([P, 2, D], BF16, "w1_sorted")
+            w1_sorted.add((q, e))
+            words = w1_unsorted[q][:, e].bitcast(F32).rearrange("p (w u) -> p u w", u=2)
+            nc.scalar.copy(out=w1_rows[q][:, e].bitcast(F32).rearrange("p (u w) -> p u w", u=2), in_=words)
+
+        def add_pos(p, batches=slice(0, B), engine=V):
             if p not in y_rows:
-                y_rows[p] = work.tile([P, 2, B, D // 2], BF16, tag="wide", bufs=WIDE, name="y_rows", align_bytes=64)
+                y_rows[p] = wide([P, 2, B, D // 2], BF16, "y_rows", *tags.get(("yr", p), ()))
             words = "p b (w u e) -> p b w u e"
             count = batches.stop - batches.start
-            nc.vector.tensor_tensor(
+            (nc.vector if engine == V else nc.gpsimd).tensor_tensor(
                 out=y_rows[p][:, :, batches].rearrange("p u b (w e) -> p b w u e", e=2),
                 in0=x_in[p][:, batches].rearrange(words, u=2, e=2),
                 in1=pos_in[p][:].unsqueeze(1).to_broadcast([P, count, D]).rearrange(words, u=2, e=2),
                 op=ADD,
             )
 
-        def scale_w1(a):
-            w1_rows[a] = work.tile([P, D], BF16, tag="w1_rows", name="w1_rows", bufs=6)
-            nc.vector.tensor_tensor(out=w1_rows[a][:], in0=w1_in.pop(a)[:].bitcast(FP8), in1=w1_scale[:], op=MULT)
+        def quantise(values, codes, scales):
+            nc.vector.quantize_mx(out=codes.bitcast(FP8X4), scales=scales, in_=values)
 
-        def sort_w1(a):
-            w1_sorted[a] = work.tile([P, 2, D // 4], F32, tag="w1_sorted", name="w1_sorted", bufs=2)
-            words = w1_rows.pop(a)[:].bitcast(F32)
-            nc.vector.tensor_copy(out=w1_sorted[a][:], in_=words.rearrange("p (w u) -> p u w", u=2))
+        def quantise_pair(p, batches, values, codes, scales, tag):
+            if p not in codes:
+                codes[p] = work.tile([P, B, WORDS], U32, tag=tag + "_codes", name="codes", align_bytes=256, bufs=PAIRS)
+                scales[p] = work.tile([P, B, WORDS], U8, tag=tag + "_scales", name="scales", align_bytes=256, bufs=PAIRS)
+            flat = "p b n -> p (b n)"
+            quantise(values[:, batches].rearrange(flat), codes[p][:, batches].rearrange(flat), scales[p][:, batches].rearrange(flat))
 
-        def quantise_pair(p, values, codes, scales, tag, bufs):
-            codes[p] = work.tile([P, B, WORDS], U32, tag=tag + "_codes", name="codes", align_bytes=256, bufs=bufs)
-            scales[p] = work.tile([P, B, WORDS], U8, tag=tag + "_scales", name="scales", align_bytes=256, bufs=bufs)
-            nc.vector.quantize_mx(
-                out=codes[p][:].rearrange("p b n -> p (b n)").bitcast(FP8X4),
-                scales=scales[p][:].rearrange("p b n -> p (b n)"),
-                in_=values,
-            )
+        def quantise_y(p, batches=slice(0, B)):
+            quantise_pair(p, batches, y_turned[p][:], y_codes, y_scales, "y")
 
-        def quantise_y(p):
-            quantise_pair(p, y_turned.pop(p)[:].rearrange("p b n -> p (b n)"), y_codes, y_scales, "y", 4)
-
-        def quantise_h(p, b=None):
-            if b is None:
-                quantise_pair(p, h_turned.pop(p)[:].rearrange("p b h n t -> p (b h n t)"), h_codes, h_scales, "h", PAIRS)
-                return
-            if p not in h_codes:
-                h_codes[p] = work.tile([P, B, WORDS], U32, tag="h_codes", name="codes", align_bytes=256, bufs=PAIRS)
-                h_scales[p] = work.tile([P, B, WORDS], U8, tag="h_scales", name="scales", align_bytes=256, bufs=PAIRS)
-            nc.vector.quantize_mx(
-                out=h_codes[p][:, b].bitcast(FP8X4),
-                scales=h_scales[p][:, b],
-                in_=h_turned[p][:, b].rearrange("p h n t -> p (h n t)"),
-            )
+        def quantise_h(p, batches=slice(0, B)):
+            quantise_pair(p, batches, h_turned[p][:].rearrange("p b h n t -> p b (h n t)"), h_codes, h_scales, "h")
 
         def quantise_w0(q):
-            nc.vector.quantize_mx(
-                out=w0_codes[:, 2 * q : 2 * q + 2].rearrange("p c g m -> p (c g m)").bitcast(FP8X4),
-                scales=w0_scales[:, 2 * q : 2 * q + 2].rearrange("p c g m -> p (c g m)"),
-                in_=w0_turned.pop(q)[:].rearrange("p c n -> p (c n)"),
-            )
+            flat = "p c g m -> p (c g m)"
+            chunks = slice(2 * q, 2 * q + 2)
+            values = w0_turned.pop(q)[:].rearrange("p c n -> p (c n)")
+            quantise(values, w0_codes[:, chunks].rearrange(flat), w0_scales[:, chunks].rearrange(flat))
 
-        def quantise_w1(q):
-            values = w1_turned.pop(q)
-            cols = slice(2 * P * q, 2 * P * (q + 1))
-            for g in range(PASSES):
-                nc.vector.quantize_mx(
-                    out=w1_codes[:, g, cols].bitcast(FP8X4),
-                    scales=w1_scales[:, g, cols],
-                    in_=values[:, g].rearrange("p e n -> p (e n)"),
-                )
+        def quantise_w1(n, g):
+            cols = slice(n * BANK, (n + 1) * BANK)
+            values = w1_turned.pop((n, g))[:].rearrange("p j r t -> p (j r t)")
+            quantise(values, w1_codes[:, g, cols], w1_scales[:, g, cols])
 
         def squares(i, engine, half=None):
             group, n = PLACE[i]
@@ -269,7 +282,7 @@ def tile_mybadtransfomerblock_pa_kernel(tc, x, pos_emb, enc_w0, enc_w1_bytes, en
                 halved.add(group)
             total = sums[group][:, slot : slot + 1]
             values = h2[i][:, cols]
-            if engine == "scalar":
+            if engine == SC:
                 squared = work.tile([P, D], BF16, tag="squared_s", name="squared", bufs=2)
                 nc.scalar.activation(out=squared[:, cols], in_=values, func=ACT.Square, accum_out=total)
             else:
@@ -283,18 +296,18 @@ def tile_mybadtransfomerblock_pa_kernel(tc, x, pos_emb, enc_w0, enc_w1_bytes, en
             factors[group] = work.tile([P, count], F32, tag="factors", name="factors", bufs=len(GROUPS))
             if group not in halved:
                 nc.scalar.activation(out=factors[group][:], in_=sums[group][:, 0:count], func=ACT.Sqrt)
-            else:
+                return
+            for n in range(count):
+                total = sums[group]
                 nc.scalar.activation(
-                    out=factors[group][:], in_=sums[group][:, 0:1], func=ACT.Sqrt, bias=sums[group][:, 2:3]
+                    out=factors[group][:, n : n + 1], in_=total[:, n : n + 1], func=ACT.Sqrt, bias=total[:, n + 2 : n + 3]
                 )
 
-        def add_eps(group, engine="scalar"):
-            if engine == "scalar":
+        def add_eps(group, engine=SC):
+            if engine == SC:
                 nc.scalar.activation(out=factors[group][:], in_=factors[group][:], func=ACT.Copy, bias=EPS)
-            elif engine == "vector":
-                nc.vector.tensor_scalar(out=factors[group][:], in0=factors[group][:], scalar1=EPS, scalar2=None, op0=ADD)
             else:
-                nc.gpsimd.tensor_scalar(out=factors[group][:], in0=factors[group][:], scalar1=1.0, scalar2=EPS, op0=MULT, op1=ADD)
+                nc.vector.tensor_scalar(out=factors[group][:], in0=factors[group][:], scalar1=EPS, scalar2=None, op0=ADD)
 
         def reciprocal(group, cols=slice(0, B)):
             nc.vector.reciprocal(out=factors[group][:, cols], in_=factors[group][:, cols])
@@ -302,9 +315,9 @@ def tile_mybadtransfomerblock_pa_kernel(tc, x, pos_emb, enc_w0, enc_w1_bytes, en
         def scale_and_store(i, engine, cols=slice(0, D)):
             group, n = PLACE[i]
             values, factor = h2[i][:, cols], factors[group][:, n : n + 1]
-            if engine == "vector":
+            if engine == V:
                 nc.vector.tensor_scalar(out=values, in0=values, scalar1=factor, scalar2=None, op0=MULT)
-            elif engine == "scalar":
+            elif engine == SC:
                 nc.scalar.activation(out=values, in_=values, func=ACT.Copy, scale=factor)
             else:
                 nc.gpsimd.tensor_scalar(out=values, in0=values, scalar1=factor, scalar2=0.0, op0=MULT, op1=ADD)
@@ -312,193 +325,249 @@ def tile_mybadtransfomerblock_pa_kernel(tc, x, pos_emb, enc_w0, enc_w1_bytes, en
             nc.sync.dma_start(out=out[b, p * P : (p + 1) * P, cols], in_=values)
 
         first, second = slice(0, 1), slice(1, 2)
-        nc.sync.dma_start(out=scale_cols[:], in_=enc_w1_scale.rearrange("o (p j) -> p (o j)", p=P))
+        low, high = slice(0, BANK), slice(BANK, D)
+
+        def release(group):
+            reciprocal(group, slice(0, len(GROUPS[group])))
+            for i in GROUPS[group]:
+                scale_and_store(i, G)
+
+        def quantise_tile(i):
+            p, b = divmod(i, B)
+            quantise_h(p, slice(b, b + 1))
+
+
+        tags = {("h", 0): ("held_b", 1), ("w1", 3): ("held_b", 1)}
+        load_w1(0, first)
+        load_w1(0, second)
+        load_scale()
+        load_w1(1)
+        load_w0(0)
         load_x(0, first)
         load_pos(0)
-        load_w0(0)
-        load_w1(0)
+        load_w1(2)
+        for c in range(1, 4):
+            load_w0(c)
         load_x(0, second)
-        load_w0(1)
-        for q in range(1, CHUNKS // 2):
-            load_w1(q)
-            load_w0(2 * q)
-            load_w0(2 * q + 1)
-        for p in range(1, PAIRS):
+        for c in range(4, CHUNKS):
+            load_w0(c)
+        load_x(1)
+        load_pos(1)
+        load_x(2)
+        load_pos(2)
+        load_w1(3)
+        for p in range(3, PAIRS):
             load_x(p)
             load_pos(p)
-            for a in W1_STEPS.get(p, ()):
-                load_w1(a)
 
-        scale_banks = [spread_scale(half) for half in range(2)]
-        for half in range(2):
-            copy_scale(half, scale_banks[half])
-        add_pos(0, first)
-        scale_w1(0)
-        add_pos(0, second)
-        turn_y(0, "scalar")
-        turn_w0(0)
-        turn_w0(1)
+        widen_w1(0, V, first)
+        widen_w1(0, V, second)
+        widen_w1(1, V, first)
+        widen_w1(1, SC, second)
         turn_w1(0)
-        turn_y(1, "scalar")
-        scale_w1(1)
+        turn_w0(0)
+        turn_w1(1)
+        scale_w1(0, 0)
+        add_pos(0, first)
+        widen_w1(2, G)
+        scale_w1(0, 1)
+        scale_w1(1, 0)
+        turn_y(0, SC)
+        turn_w0(1)
         turn_w0(2)
         turn_w0(3)
-        scale_w1(2)
         quantise_w0(0)
-        turn_w0(4)
-        quantise_y(0)
-        turn_w1(1)
+        add_pos(0, second)
+        quantise_y(0, first)
         quantise_w0(1)
+        turn_w1(2)
+        turn_w0(4)
+        turn_y(1, SC)
+        scale_w1(1, 1)
         turn_w0(5)
-        scale_w1(3)
         turn_w0(6)
         turn_w0(7)
-        turn_w1(2)
-        stage1(0, 0, "scalar")
+        stage1(0, 0, SC)
+        quantise_y(0, second)
         quantise_w0(2)
         add_pos(1)
-        stage1(1, 0, "scalar")
         quantise_w0(3)
-        turn_y(2, "scalar")
-        turn_y(3, "scalar")
-        scale_w1(4)
+        stage1(1, 0, SC)
+        turn_y(2, SC)
+        turn_y(3, SC)
         add_pos(2)
-        sort_w1(4)
-        turn_w1(3)
-        stage1(0, 1, "scalar")
+        quantise_w1(0, 0)
+        stage1(0, 1, SC)
+        stage1(1, 1, SC)
         quantise_y(1)
-        stage1(1, 1, "scalar")
-        turn_y(4, "scalar", hold=True)
-        turn_y(5, "scalar")
-        scale_w1(5)
-        turn_w1(4)
-        add_pos(3)
-        sort_w1(5)
-        stage1(2, 0, "scalar", hold=True)
-        stage1(2, 1, "scalar")
-        quantise_y(2)
-        stage1(3, 0, "scalar", hold=True)
-        scale_w1(6)
-        stage1(3, 1, "scalar")
-
-        turn_w1(5)
-        turn_y(6, "scalar", hold=True)
-        turn_y(7, "scalar")
-        add_pos(4)
-        sort_w1(6)
-        stage1(4, 0, "scalar", hold=True)
-        stage1(4, 1, "scalar")
-        scale_w1(7)
-        stage1(5, 0, "scalar", hold=True)
-        stage1(5, 1, "scalar")
-        quantise_y(3)
-        add_pos(5)
-        sort_w1(7)
-
-        turn_w1(6)
-        turn_y(8, "scalar", hold=True)
-        turn_y(9, "scalar")
-        quantise_w1(0)
+        quantise_w1(0, 1)
         quantise_h(0)
-        quantise_w1(1)
-        stage1(6, 0, "scalar", hold=True)
-        stage1(6, 1, "scalar")
-        quantise_y(4)
-        stage1(7, 0, "scalar", hold=True)
-        stage1(7, 1, "scalar")
-        quantise_w1(2)
-        add_pos(6)
-
-        turn_w1(7)
-        turn_y(10, "scalar", hold=True)
-        turn_y(11, "scalar")
-        stage2(0, 0, "scalar", hold=True)
-        stage2(1, 0, "scalar")
-        quantise_w1(3)
+        widen_w1(3, G)
+        turn_y(4, SC)
+        turn_y(5, SC)
+        scale_w1(2, 0)
+        stage1(2, 0, SC)
+        stage1(2, 1, SC)
+        scale_w1(2, 1)
+        stage1(3, 0, SC)
+        stage1(3, 1, SC)
+        add_pos(3)
+        quantise_y(2)
+        stage2(0, 0, SC)
+        stage2(1, 0, SC)
         quantise_h(1)
-        add_pos(7)
-        stage1(8, 0, "scalar")
-        stage1(8, 1, "vector")
-        stage2(0, 1, "scalar")
-        stage2(1, 1, "scalar")
-        squares(0, "scalar")
-        quantise_h(2)
-        quantise_y(5)
-        squares(1, "scalar")
-        stage1(9, 0, "vector", hold=True)
-        stage1(9, 1, "vector")
-        quantise_h(3)
+        squares(0, SC, 0)
+        squares(1, SC, 0)
+        turn_w1(3)
+        turn_y(6, SC)
+        turn_y(7, SC)
+        scale_w1(3, 0)
+        stage1(4, 0, SC)
+        stage1(4, 1, SC)
+        scale_w1(3, 1)
+        stage1(5, 0, SC)
+        stage1(5, 1, SC)
+        quantise_w1(1, 0)
+        quantise_w1(1, 1)
 
-        V, S, G = "vector", "scalar", "gpsimd"
-        low, high = slice(0, BANK), slice(BANK, D)
-        for f in range(1, PAIRS - 2):
-            a, b, i = B * f, B * f + 1, 9 + f
-            stage2(a, 0, S)
-            root(f - 1)
-            stage2(a, 1, V)
-            stage2(b, 0, V if f in (2,) else S)
-            add_eps(f - 1)
-            stage2(b, 1, V)
-            for p in [p for p in h_turned if B * p + 1 < i]:
-                quantise_h(p)
-            for p in list(y_turned):
-                quantise_y(p)
-            reciprocal(f - 1, first if f == 4 else slice(0, B))
-            squares(a, S)
-            if f == 4:
-                stage1(i, 0, V)
-                scale_and_store(a - 2, V)
-                reciprocal(f - 1, second)
-                scale_and_store(a - 1, G)
-                stage1(i, 1, V)
-            else:
-                scale_and_store(a - 2, G)
-                scale_and_store(a - 1, G)
-                stage1(i, 0, V, hold=True)
-                stage1(i, 1, V)
-            squares(b, S)
-            if f <= 2:
-                turn_y(B * (f + 5), V)
-                turn_y(B * (f + 5) + 1, S)
-        stage1(15, 0, V, hold=True)
-        stage1(15, 1, V)
+        add_pos(4)
+        quantise_y(3)
+        quantise_h(2)
+        add_pos(5)
+        add_pos(6)
+        stage2(2, 0, SC)
+        stage2(3, 0, SC)
+
+        stage2(0, 1, SC)
+        stage2(1, 1, SC)
+        turn_y(8, SC)
+        turn_y(9, SC)
+        quantise_y(4)
+        add_pos(7)
+        squares(0, SC, 1)
+        squares(1, SC, 1)
+        stage1(6, 0, SC)
+        root(0)
+        stage1(6, 1, SC)
+        add_eps(0)
+        stage1(7, 0, V)
+        release(0)
+        stage1(7, 1, V)
+        stage2(2, 1, SC)
+        stage2(3, 1, SC)
+        squares(2, SC)
+        squares(3, SC)
+        turn_y(10, V)
+        turn_y(11, V)
+        stage2(4, 0, V)
+        stage2(4, 1, V)
+        quantise_h(3)
+        quantise_y(5)
+        stage2(5, 0, SC)
+        root(1)
+        stage2(5, 1, SC)
+        add_eps(1)
+        stage1(8, 0, V)
+        release(1)
+        squares(4, SC)
+        squares(5, SC)
+        stage1(8, 1, V)
+        stage1(9, 0, V)
+        stage1(9, 1, V)
+        turn_y(12, V)
+        turn_y(13, V)
+        turn_y(14, SC)
+        root(2)
+        turn_y(15, SC)
+        add_eps(2)
+        quantise_h(4)
+        release(2)
+        stage2(6, 0, SC)
+        stage2(6, 1, SC)
+        stage2(7, 0, V)
+        stage2(7, 1, V)
+        squares(6, SC)
+        squares(7, SC)
+        stage1(10, 0, V)
+        stage1(10, 1, V)
+        stage1(11, 0, V)
+        stage1(11, 1, SC)
+        root(3)
+        quantise_y(6)
+        quantise_y(7)
+        quantise_h(5)
+        stage2(8, 0, SC)
+        add_eps(3)
+        release(3)
+
+        stage2(8, 1, SC)
+        stage2(9, 0, SC)
+        stage2(9, 1, V)
+        squares(8, SC)
+        stage1(12, 0, V)
+        stage1(12, 1, V)
+        root(4)
+        squares(9, SC, 0)
+        add_eps(4)
+        squares(9, SC, 1)
+        stage2(10, 0, V)
+        stage2(10, 1, V)
+        quantise_tile(12)
+        release(4)
+        stage1(13, 0, SC)
         root(5)
-        stage2(12, 0, S)
+        squares(10, SC, 0)
         add_eps(5)
-        stage2(12, 1, V)
-        quantise_h(7, 0)
-        reciprocal(5, first)
-        quantise_h(7, 1)
-        scale_and_store(10, V)
-        reciprocal(5, second)
-        scale_and_store(11, G)
-        stage2(13, 0, S)
-        squares(12, S)
-        stage2(13, 1, V)
-        stage2(14, 0, V)
+        stage1(13, 1, V)
+        squares(10, SC, 1)
+        stage2(11, 0, V)
+        release(5)
+        stage2(11, 1, V)
         root(6)
-        squares(13, S, 0)
+        squares(11, SC, 0)
         add_eps(6)
-        squares(13, S, 1)
-        stage2(14, 1, V)
-        reciprocal(6, first)
+        squares(11, SC, 1)
+        stage1(14, 0, V)
+        stage1(14, 1, V)
+
+        quantise_tile(13)
+        quantise_tile(14)
+        release(6)
+        stage2(12, 0, SC)
         root(7)
-        stage2(15, 0, V)
-        squares(14, S, 0)
+        stage2(12, 1, V)
+        squares(12, SC, 0)
         add_eps(7)
-        scale_and_store(12, V)
-        squares(14, S, 1)
-        reciprocal(7, first)
-        stage2(15, 1, V)
+        squares(12, SC, 1)
+        stage1(15, 0, V)
+        stage1(15, 1, V)
+        stage2(13, 0, SC)
         root(8)
-        scale_and_store(13, V)
-        squares(15, S, 0)
+        quantise_tile(15)
+        release(7)
+        stage2(13, 1, V)
+        squares(13, SC, 0)
         add_eps(8)
-        squares(15, S, 1)
-        reciprocal(8, first)
+        squares(13, SC, 1)
+        stage2(14, 0, V)
+        release(8)
+        stage2(14, 1, V)
         root(9)
-        scale_and_store(14, V)
+        squares(14, SC, 0)
         add_eps(9)
+        stage2(15, 0, V)
+        squares(14, SC, 1)
+        stage2(15, 1, V)
         reciprocal(9, first)
+        root(10)
+        squares(15, SC, 0)
+        scale_and_store(13, V)
+        add_eps(10)
+        squares(15, SC, 1)
+        reciprocal(10, first)
+        root(11)
+        scale_and_store(14, V)
+        add_eps(11)
+        reciprocal(11, first)
         scale_and_store(15, V, high)
         scale_and_store(15, V, low)

@@ -61,7 +61,7 @@ def tile_mybadtransfomerblock_pa_kernel(tc, x, pos_emb, enc_w0, enc_w1_bytes, en
         w0_turned, w1_rows, w1_unsorted, w1_bank, w1_turned, w1_sorted = {}, {}, {}, {}, {}, set()
         h_turned, h_codes, h_scales = {}, {}, {}
         h2, z_bank, sums, factors = {}, {}, {}, {}
-        free_banks, held, halved = list(range(BANKS)), [], set()
+        free_banks, pending, halved = list(range(BANKS)), {}, set()
 
         def wide(shape, dtype, name, tag="wide", bufs=WIDE):
             return work.tile(shape, dtype, tag=tag, bufs=bufs, name=name, align_bytes=64)
@@ -71,12 +71,15 @@ def tile_mybadtransfomerblock_pa_kernel(tc, x, pos_emb, enc_w0, enc_w1_bytes, en
             bank = psum.tile([P, BANK], F32, tag="bank%d" % number, name="bank")
             return bank, number
 
-        def empty(step, number, hold):
-            held.append((step, number))
-            while held and not hold:
-                step, number = held.pop()
-                step()
-                free_banks.append(number)
+        def filled(key, number, step, engine):
+            pending[key] = (number, step)
+            if engine:
+                empty(key, engine)
+
+        def empty(key, engine):
+            number, step = pending.pop(key)
+            step(engine)
+            free_banks.append(number)
 
         def relu(engine, dst, src):
             if engine == SC:
@@ -125,23 +128,23 @@ def tile_mybadtransfomerblock_pa_kernel(tc, x, pos_emb, enc_w0, enc_w1_bytes, en
                     nc.tensor.transpose(blocks[:, j, u, :], source(j, u), ident[:])
             return bank, number
 
-        def turn_y(i, engine, hold=False):
+        def turn_y(i, engine=None):
             p, b = divmod(i, B)
             words = y_rows[p][:, :, b].bitcast(F32)
             bank, number = transpose_words(lambda g, u: words[:, u, g * P : (g + 1) * P])
             if b == 0:
                 y_turned[p] = wide([P, B, D], BF16, "y_turned", *tags.get(("y", p), ()))
             dst = y_turned[p][:, b].bitcast(F32).rearrange("p (g n) -> p g n", g=PASSES)
-            empty(lambda: copy_words(engine, bank, dst), number, hold)
+            filled(("y", i), number, lambda engine: copy_words(engine, bank, dst), engine)
 
-        def turn_w0(c, engine=SC, hold=False):
+        def turn_w0(c, engine=SC):
             q, e = divmod(c, 2)
             words = w0_in.pop(c)[:].bitcast(F32)
             bank, number = transpose_words(lambda g, u: words[:, 2 * P * g + u : 2 * P * (g + 1) : 2])
             if e == 0:
                 w0_turned[q] = wide([P, 2, D], BF16, "w0_turned", *tags.get(("w0", q), ()))
             dst = w0_turned[q][:, e].bitcast(F32).rearrange("p (g n) -> p g n", g=PASSES)
-            empty(lambda: copy_words(engine, bank, dst), number, hold)
+            filled(("w0", c), number, lambda engine: copy_words(engine, bank, dst), engine)
 
         def turn_w1(q):
             for g in range(PASSES):
@@ -168,7 +171,7 @@ def tile_mybadtransfomerblock_pa_kernel(tc, x, pos_emb, enc_w0, enc_w1_bytes, en
             nc.vector.tensor_tensor(out=dst, in0=values, in1=scales, op=MULT)
             free_banks.append(number)
 
-        def stage1(i, h, engine, hold=False):
+        def stage1(i, h, engine=None):
             p, b = divmod(i, B)
             bank, number = next_bank()
             for t in range(4):
@@ -185,26 +188,32 @@ def tile_mybadtransfomerblock_pa_kernel(tc, x, pos_emb, enc_w0, enc_w1_bytes, en
             if p not in h_turned:
                 h_turned[p] = wide([P, B, PASSES, P, 4], BF16, "h_turned", *tags.get(("h", p), ()))
             dst = h_turned[p][:, b, h].rearrange("p (c i) t -> p c t i", i=2)
-            empty(lambda: relu(engine, dst, bank[:].rearrange("p (t c i) -> p c t i", t=4, i=2)), number, hold)
+            src = bank[:].rearrange("p (t c i) -> p c t i", t=4, i=2)
+            filled(("h", i, h), number, lambda engine: relu(engine, dst, src), engine)
 
-        def stage2(i, n, engine, hold=False):
+        def stage2_pass(i, n, g):
             p, b = divmod(i, B)
             cols = slice(n * BANK, (n + 1) * BANK)
-            bank, number = next_bank()
+            if g == 0:
+                z_bank[i, n] = next_bank()
+            nc.tensor.matmul_mx(
+                out=z_bank[i, n][0][:],
+                lhsT=h_codes[p][:, b, g * P : (g + 1) * P].bitcast(FP8X4),
+                lhsT_scale=h_scales[p][:, b, g * P : (g + 1) * P],
+                rhs=w1_codes[:, g, cols].bitcast(FP8X4),
+                rhs_scale=w1_scales[:, g, cols],
+                start=(g == 0),
+                stop=(g == PASSES - 1),
+            )
+
+        def stage2(i, n, engine=None):
             for g in range(PASSES):
-                nc.tensor.matmul_mx(
-                    out=bank[:],
-                    lhsT=h_codes[p][:, b, g * P : (g + 1) * P].bitcast(FP8X4),
-                    lhsT_scale=h_scales[p][:, b, g * P : (g + 1) * P],
-                    rhs=w1_codes[:, g, cols].bitcast(FP8X4),
-                    rhs_scale=w1_scales[:, g, cols],
-                    start=(g == 0),
-                    stop=(g == PASSES - 1),
-                )
+                if g or (i, n) not in z_bank:
+                    stage2_pass(i, n, g)
             if i not in h2:
                 h2[i] = wide([P, D], F32, "h2")
-            z_bank[i, n] = bank
-            empty(lambda: relu(engine, h2[i][:, cols], bank[:]), number, hold)
+            bank, number = z_bank[i, n]
+            filled(("z", i, n), number, lambda engine: relu(engine, h2[i][:, n * BANK : (n + 1) * BANK], bank[:]), engine)
 
         def widen_w1(q, engine, chunks=slice(0, 2)):
             if q not in w1_rows:
@@ -261,6 +270,12 @@ def tile_mybadtransfomerblock_pa_kernel(tc, x, pos_emb, enc_w0, enc_w1_bytes, en
         def quantise_h(p, batches=slice(0, B)):
             quantise_pair(p, batches, h_turned[p][:].rearrange("p b h n t -> p b (h n t)"), h_codes, h_scales, "h")
 
+        def quantise_half(i, h):
+            p, b = divmod(i, B)
+            words = slice(h * P, (h + 1) * P)
+            values = h_turned[p][:, b, h].rearrange("p n t -> p (n t)")
+            quantise(values, h_codes[p][:, b, words], h_scales[p][:, b, words])
+
         def quantise_w0(q):
             flat = "p c g m -> p (c g m)"
             chunks = slice(2 * q, 2 * q + 2)
@@ -288,7 +303,7 @@ def tile_mybadtransfomerblock_pa_kernel(tc, x, pos_emb, enc_w0, enc_w1_bytes, en
             else:
                 squared = work.tile([P, D], BF16, tag="squared_v", name="squared", bufs=1)
                 nc.vector.scalar_tensor_tensor(
-                    out=squared[:, cols], in0=z_bank[i, half][:], scalar=0.0, in1=values, op0=MAX, op1=MULT, accum_out=total
+                    out=squared[:, cols], in0=z_bank[i, half][0][:], scalar=0.0, in1=values, op0=MAX, op1=MULT, accum_out=total
                 )
 
         def root(group):
@@ -329,6 +344,12 @@ def tile_mybadtransfomerblock_pa_kernel(tc, x, pos_emb, enc_w0, enc_w1_bytes, en
 
         def release(group):
             reciprocal(group, slice(0, len(GROUPS[group])))
+            for i in GROUPS[group]:
+                scale_and_store(i, G)
+
+        def release_behind(group, last):
+            reciprocal(group, slice(0, len(GROUPS[group])))
+            last()
             for i in GROUPS[group]:
                 scale_and_store(i, G)
 
@@ -427,38 +448,39 @@ def tile_mybadtransfomerblock_pa_kernel(tc, x, pos_emb, enc_w0, enc_w1_bytes, en
         scale_w1(3, 1)
         stage1(5, 0, SC)
         stage1(5, 1, SC)
+
         quantise_w1(1, 0)
         quantise_w1(1, 1)
-
-        add_pos(4)
         quantise_y(3)
-        quantise_h(2)
+        add_pos(4)
         add_pos(5)
+        quantise_h(2)
+
         add_pos(6)
+        add_pos(7)
         stage2(2, 0, SC)
         stage2(3, 0, SC)
-
         stage2(0, 1, SC)
         stage2(1, 1, SC)
-        turn_y(8, SC)
-        turn_y(9, SC)
-        quantise_y(4)
-        add_pos(7)
+        stage1(6, 0, SC)
+        stage1(6, 1, SC)
         squares(0, SC, 1)
         squares(1, SC, 1)
-        stage1(6, 0, SC)
+
+        turn_y(8, SC)
         root(0)
-        stage1(6, 1, SC)
+        turn_y(9, SC)
         add_eps(0)
+        turn_y(10, V)
+        release_behind(0, lambda: quantise_y(4))
+        turn_y(11, V)
         stage1(7, 0, V)
-        release(0)
-        stage1(7, 1, V)
+        stage1(7, 1)
         stage2(2, 1, SC)
         stage2(3, 1, SC)
+        empty(("h", 7, 1), V)
         squares(2, SC)
         squares(3, SC)
-        turn_y(10, V)
-        turn_y(11, V)
         stage2(4, 0, V)
         stage2(4, 1, V)
         quantise_h(3)
@@ -478,12 +500,12 @@ def tile_mybadtransfomerblock_pa_kernel(tc, x, pos_emb, enc_w0, enc_w1_bytes, en
         turn_y(13, V)
         turn_y(14, SC)
         root(2)
-        turn_y(15, SC)
-        add_eps(2)
-        quantise_h(4)
-        release(2)
+        turn_y(15)
         stage2(6, 0, SC)
+        add_eps(2)
+        release_behind(2, lambda: quantise_h(4))
         stage2(6, 1, SC)
+        empty(("y", 15), SC)
         stage2(7, 0, V)
         stage2(7, 1, V)
         squares(6, SC)
@@ -499,21 +521,19 @@ def tile_mybadtransfomerblock_pa_kernel(tc, x, pos_emb, enc_w0, enc_w1_bytes, en
         stage2(8, 0, SC)
         add_eps(3)
         release(3)
-
         stage2(8, 1, SC)
         stage2(9, 0, SC)
         stage2(9, 1, V)
         squares(8, SC)
         stage1(12, 0, V)
         stage1(12, 1, V)
-        root(4)
         squares(9, SC, 0)
-        add_eps(4)
+        root(4)
         squares(9, SC, 1)
+        add_eps(4)
         stage2(10, 0, V)
         stage2(10, 1, V)
-        quantise_tile(12)
-        release(4)
+        release_behind(4, lambda: quantise_tile(12))
         stage1(13, 0, SC)
         root(5)
         squares(10, SC, 0)
@@ -523,28 +543,26 @@ def tile_mybadtransfomerblock_pa_kernel(tc, x, pos_emb, enc_w0, enc_w1_bytes, en
         stage2(11, 0, V)
         release(5)
         stage2(11, 1, V)
-        root(6)
         squares(11, SC, 0)
-        add_eps(6)
+        root(6)
         squares(11, SC, 1)
+        add_eps(6)
         stage1(14, 0, V)
         stage1(14, 1, V)
-
         quantise_tile(13)
-        quantise_tile(14)
-        release(6)
+        release_behind(6, lambda: quantise_tile(14))
+
         stage2(12, 0, SC)
         root(7)
-        stage2(12, 1, V)
-        squares(12, SC, 0)
+        stage2(12, 1, SC)
         add_eps(7)
+        squares(12, SC, 0)
         squares(12, SC, 1)
         stage1(15, 0, V)
         stage1(15, 1, V)
         stage2(13, 0, SC)
         root(8)
-        quantise_tile(15)
-        release(7)
+        release_behind(7, lambda: quantise_tile(15))
         stage2(13, 1, V)
         squares(13, SC, 0)
         add_eps(8)

@@ -27,6 +27,7 @@ QUARTERS = CHUNKS // 2
 BANKS = 8
 BANK = 512
 WIDE = 20
+SINGLE_PAIRS = 8
 WORDS = D // 4
 V, SC, G = "vector", "scalar", "gpsimd"
 
@@ -89,12 +90,22 @@ def tile_mybadtransfomerblock_pa_kernel(tc, x, pos_emb, enc_w0, enc_w1_bytes, en
 
         def load_x(p, batches=slice(0, B)):
             if p not in x_in:
-                x_in[p] = work.tile([P, B, D], BF16, tag="x_in", bufs=PAIRS, name="x_in")
+                x_in[p] = work.tile([P, B, D], BF16, tag="x_in", bufs=SINGLE_PAIRS, name="x_in")
             rows = x[:, p * P : (p + 1) * P, :].rearrange("b s k -> s b k")
             nc.sync.dma_start(out=x_in[p][:, batches], in_=rows[:, batches])
 
+        def load_last_pairs(start):
+            count = PAIRS - start
+            rows = work.tile([P, B, count, D], BF16, tag="x_last", bufs=1, name="x_last")
+            for b in range(B):
+                nc.sync.dma_start(out=rows[:, b], in_=x[b, start * P :, :].rearrange("(j m) k -> m j k", m=P))
+            table = work.tile([P, count, D], BF16, tag="pos_last", bufs=1, name="pos_last")
+            nc.sync.dma_start(out=table[:], in_=pos_emb[0, start * P :, :].rearrange("(j m) k -> m j k", m=P))
+            for p in range(start, PAIRS):
+                x_in[p], pos_in[p] = rows[:, :, p - start], table[:, p - start]
+
         def load_pos(p):
-            pos_in[p] = work.tile([P, D], BF16, tag="pos_in", bufs=PAIRS, name="pos_in")
+            pos_in[p] = work.tile([P, D], BF16, tag="pos_in", bufs=SINGLE_PAIRS, name="pos_in")
             nc.sync.dma_start(out=pos_in[p][:], in_=pos_emb[0, p * P : (p + 1) * P, :])
 
         w0_rows = enc_w0.rearrange("(h m t) k -> h t m k", h=PASSES, m=P, t=4)
@@ -312,7 +323,7 @@ def tile_mybadtransfomerblock_pa_kernel(tc, x, pos_emb, enc_w0, enc_w1_bytes, en
             if group not in halved:
                 nc.scalar.activation(out=factors[group][:], in_=sums[group][:, 0:count], func=ACT.Sqrt)
                 return
-            for n in range(count):
+            for n in reversed(range(count)):
                 total = sums[group]
                 nc.scalar.activation(
                     out=factors[group][:, n : n + 1], in_=total[:, n : n + 1], func=ACT.Sqrt, bias=total[:, n + 2 : n + 3]
@@ -358,7 +369,7 @@ def tile_mybadtransfomerblock_pa_kernel(tc, x, pos_emb, enc_w0, enc_w1_bytes, en
             quantise_h(p, slice(b, b + 1))
 
 
-        tags = {("h", 0): ("held_b", 1), ("w1", 3): ("held_b", 1)}
+        tags = {("y", 2): ("held_a", 1), ("yr", 4): ("held_a", 1), ("h", 0): ("held_b", 1), ("w1", 3): ("held_b", 1)}
         load_w1(0, first)
         load_w1(0, second)
         load_scale()
@@ -372,8 +383,9 @@ def tile_mybadtransfomerblock_pa_kernel(tc, x, pos_emb, enc_w0, enc_w1_bytes, en
         load_x(0, second)
         for c in range(4, CHUNKS):
             load_w0(c)
-        load_x(1)
+        load_x(1, first)
         load_pos(1)
+        load_x(1, second)
         load_x(2)
         load_pos(2)
         load_w1(3)
@@ -410,8 +422,9 @@ def tile_mybadtransfomerblock_pa_kernel(tc, x, pos_emb, enc_w0, enc_w1_bytes, en
         turn_w0(7)
         stage1(0, 0, SC)
         quantise_y(0, second)
+        add_pos(1, first)
         quantise_w0(2)
-        add_pos(1)
+        add_pos(1, second)
         quantise_w0(3)
         stage1(1, 0, SC)
         turn_y(2, SC)
@@ -443,16 +456,17 @@ def tile_mybadtransfomerblock_pa_kernel(tc, x, pos_emb, enc_w0, enc_w1_bytes, en
         turn_y(6, SC)
         turn_y(7, SC)
         scale_w1(3, 0)
+        add_pos(4, first, G)
         stage1(4, 0, SC)
         stage1(4, 1, SC)
         scale_w1(3, 1)
         stage1(5, 0, SC)
         stage1(5, 1, SC)
 
+        quantise_y(3)
         quantise_w1(1, 0)
         quantise_w1(1, 1)
-        quantise_y(3)
-        add_pos(4)
+        add_pos(4, second)
         add_pos(5)
         quantise_h(2)
 
@@ -460,10 +474,10 @@ def tile_mybadtransfomerblock_pa_kernel(tc, x, pos_emb, enc_w0, enc_w1_bytes, en
         add_pos(7)
         stage2(2, 0, SC)
         stage2(3, 0, SC)
-        stage2(0, 1, SC)
-        stage2(1, 1, SC)
         stage1(6, 0, SC)
         stage1(6, 1, SC)
+        stage2(0, 1, SC)
+        stage2(1, 1, SC)
         squares(0, SC, 1)
         squares(1, SC, 1)
 
@@ -484,13 +498,12 @@ def tile_mybadtransfomerblock_pa_kernel(tc, x, pos_emb, enc_w0, enc_w1_bytes, en
         stage2(4, 0, V)
         stage2(4, 1, V)
         quantise_h(3)
-        quantise_y(5)
         stage2(5, 0, SC)
         root(1)
         stage2(5, 1, SC)
         add_eps(1)
         stage1(8, 0, V)
-        release(1)
+        release_behind(1, lambda: quantise_y(5))
         squares(4, SC)
         squares(5, SC)
         stage1(8, 1, V)
@@ -541,46 +554,49 @@ def tile_mybadtransfomerblock_pa_kernel(tc, x, pos_emb, enc_w0, enc_w1_bytes, en
         stage1(13, 1, V)
         squares(10, SC, 1)
         stage2(11, 0, V)
-        release(5)
+        release_behind(5, lambda: quantise_tile(13))
         stage2(11, 1, V)
         squares(11, SC, 0)
         root(6)
-        squares(11, SC, 1)
         add_eps(6)
+        squares(11, SC, 1)
+
+        stage2(12, 0, V)
+        release(6)
+        stage2(12, 1, SC)
+        root(7)
+        squares(12, SC, 0)
+        add_eps(7)
+        squares(12, SC, 1)
         stage1(14, 0, V)
         stage1(14, 1, V)
-        quantise_tile(13)
-        release_behind(6, lambda: quantise_tile(14))
-
-        stage2(12, 0, SC)
-        root(7)
-        stage2(12, 1, SC)
-        add_eps(7)
-        squares(12, SC, 0)
-        squares(12, SC, 1)
-        stage1(15, 0, V)
-        stage1(15, 1, V)
-        stage2(13, 0, SC)
+        stage2(13, 0, V)
+        release_behind(7, lambda: quantise_tile(14))
+        stage2(13, 1, SC)
         root(8)
-        release_behind(7, lambda: quantise_tile(15))
-        stage2(13, 1, V)
         squares(13, SC, 0)
         add_eps(8)
         squares(13, SC, 1)
-        stage2(14, 0, V)
-        release(8)
-        stage2(14, 1, V)
+        stage1(15, 0, V)
+        stage1(15, 1, V)
+        reciprocal(8, first)
+        quantise_half(15, 0)
+        quantise_half(15, 1)
+        scale_and_store(12, V)
         root(9)
-        squares(14, SC, 0)
+        stage2(14, 0, SC)
         add_eps(9)
-        stage2(15, 0, V)
+        stage2(14, 1, V)
+        release(9)
+        squares(14, SC, 0)
+        stage2_pass(15, 0, 0)
+        stage2_pass(15, 1, 0)
         squares(14, SC, 1)
+        stage2(15, 0, V)
         stage2(15, 1, V)
-        reciprocal(9, first)
         root(10)
         squares(15, SC, 0)
-        scale_and_store(13, V)
-        add_eps(10)
+        add_eps(10, V)
         squares(15, SC, 1)
         reciprocal(10, first)
         root(11)

@@ -226,13 +226,15 @@ def tile_mybadtransfomerblock_pa_kernel(tc, x, pos_emb, enc_w0, enc_w1_bytes, en
             bank, number = z_bank[i, n]
             filled(("z", i, n), number, lambda engine: relu(engine, h2[i][:, n * BANK : (n + 1) * BANK], bank[:]), engine)
 
-        def widen_w1(q, engine, chunks=slice(0, 2)):
+        def widen_w1(q, engine, chunks=slice(0, 2), cols=slice(None)):
             if q not in w1_rows:
                 w1_rows[q] = wide([P, 2, D], BF16, "w1_rows", *tags.get(("w1", q), ()))
-            dst = w1_rows[q][:, chunks].rearrange("p e k -> p (e k)")
-            src = w1_in[q][:, chunks].rearrange("p e k -> p (e k)").bitcast(FP8)
+            dst = w1_rows[q][:, chunks].rearrange("p e k -> p (e k)")[:, cols]
+            src = w1_in[q][:, chunks].rearrange("p e k -> p (e k)")[:, cols].bitcast(FP8)
             if engine == SC:
                 nc.scalar.copy(out=dst, in_=src)
+            elif engine == V and chunks.stop - chunks.start == 2:
+                nc.vector.tensor_copy(out=dst, in_=src)
             elif engine == V:
                 w1_sorted.add((q, chunks.start))
                 nc.vector.tensor_scalar(
@@ -253,15 +255,15 @@ def tile_mybadtransfomerblock_pa_kernel(tc, x, pos_emb, enc_w0, enc_w1_bytes, en
             words = w1_unsorted[q][:, e].bitcast(F32).rearrange("p (w u) -> p u w", u=2)
             nc.scalar.copy(out=w1_rows[q][:, e].bitcast(F32).rearrange("p (u w) -> p u w", u=2), in_=words)
 
-        def add_pos(p, batches=slice(0, B), engine=V):
+        def add_pos(p, batches=slice(0, B), engine=V, part=slice(0, WORDS)):
             if p not in y_rows:
                 y_rows[p] = wide([P, 2, B, D // 2], BF16, "y_rows", *tags.get(("yr", p), ()))
             words = "p b (w u e) -> p b w u e"
             count = batches.stop - batches.start
             (nc.vector if engine == V else nc.gpsimd).tensor_tensor(
-                out=y_rows[p][:, :, batches].rearrange("p u b (w e) -> p b w u e", e=2),
-                in0=x_in[p][:, batches].rearrange(words, u=2, e=2),
-                in1=pos_in[p][:].unsqueeze(1).to_broadcast([P, count, D]).rearrange(words, u=2, e=2),
+                out=y_rows[p][:, :, batches].rearrange("p u b (w e) -> p b w u e", e=2)[:, :, part],
+                in0=x_in[p][:, batches].rearrange(words, u=2, e=2)[:, :, part],
+                in1=pos_in[p][:].unsqueeze(1).to_broadcast([P, count, D]).rearrange(words, u=2, e=2)[:, :, part],
                 op=ADD,
             )
 
@@ -402,7 +404,8 @@ def tile_mybadtransfomerblock_pa_kernel(tc, x, pos_emb, enc_w0, enc_w1_bytes, en
         turn_w1(1)
         scale_w1(0, 0)
         add_pos(0, first)
-        widen_w1(2, G)
+        widen_w1(2, G, cols=slice(0, 3 * BANK))
+        widen_w1(2, SC, cols=slice(3 * BANK, 4 * BANK))
         scale_w1(0, 1)
         scale_w1(1, 0)
         turn_y(0, SC)
@@ -436,7 +439,7 @@ def tile_mybadtransfomerblock_pa_kernel(tc, x, pos_emb, enc_w0, enc_w1_bytes, en
         quantise_y(1)
         quantise_w1(0, 1)
         quantise_h(0)
-        widen_w1(3, G)
+        widen_w1(3, G, cols=slice(0, 7 * WORDS))
         turn_y(4, SC)
         turn_y(5, SC)
         scale_w1(2, 0)
@@ -445,6 +448,7 @@ def tile_mybadtransfomerblock_pa_kernel(tc, x, pos_emb, enc_w0, enc_w1_bytes, en
         scale_w1(2, 1)
         stage1(3, 0, SC)
         stage1(3, 1, SC)
+        widen_w1(3, V, cols=slice(7 * WORDS, 8 * WORDS))
         add_pos(3)
         quantise_y(2)
         stage2(0, 0, SC)
@@ -456,7 +460,7 @@ def tile_mybadtransfomerblock_pa_kernel(tc, x, pos_emb, enc_w0, enc_w1_bytes, en
         turn_y(6, SC)
         turn_y(7, SC)
         scale_w1(3, 0)
-        add_pos(4, first, G)
+        add_pos(4, first, G, slice(0, 224))
         stage1(4, 0, SC)
         stage1(4, 1, SC)
         scale_w1(3, 1)
@@ -466,6 +470,7 @@ def tile_mybadtransfomerblock_pa_kernel(tc, x, pos_emb, enc_w0, enc_w1_bytes, en
         quantise_y(3)
         quantise_w1(1, 0)
         quantise_w1(1, 1)
+        add_pos(4, first, V, slice(224, 256))
         add_pos(4, second)
         add_pos(5)
         quantise_h(2)

from contextlib import ExitStack

import concourse.mybir as mybir
from concourse.masks import make_identity

B, S, D = 2, 1024, 1024
EPS = 1e-6
FLOPS = 2 * (2 * B * S * D * D)

F32 = mybir.dt.float32
BF16 = mybir.dt.bfloat16
U32 = mybir.dt.uint32
U8 = mybir.dt.uint8
FP8 = mybir.dt.float8_e4m3fn
FP8X4 = mybir.dt.float8_e4m3fn_x4
ADD = mybir.AluOpType.add
MULT = mybir.AluOpType.mult
MAX = mybir.AluOpType.max
ACT = mybir.ActivationFunctionType

P = 128
PASSES = 2
TILES = B * S // P
PAIRS = TILES // B
CHUNKS = D // P
QUARTERS = CHUNKS // 2
BANKS = 8
BANK = 512
WIDE = 20
SINGLE_PAIRS = 8
WORDS = D // 4
V, SC, G = "vector", "scalar", "gpsimd"

PAIRED = 4
GROUPS = [(B * f, B * f + 1) for f in range(PAIRED)] + [(i,) for i in range(B * PAIRED, TILES)]
PLACE = {i: (group, n) for group, tiles in enumerate(GROUPS) for n, i in enumerate(tiles)}


def tile_mybadtransfomerblock_pa_kernel(tc, x, pos_emb, enc_w0, enc_w1_bytes, enc_w1_scale, out):
    nc = tc.nc
    with ExitStack() as ctx:
        keep = ctx.enter_context(tc.tile_pool(name="keep", bufs=1))
        work = ctx.enter_context(tc.tile_pool(name="work", bufs=3))
        psum = ctx.enter_context(tc.psum_pool(name="psum", bufs=1))
        ctx.enter_context(tc.manual_schedule())

        ident = keep.tile([P, P], F32, tag="ident")
        make_identity(nc, ident[:])
        one = keep.tile([P, 1], F32, tag="one")
        nc.vector.memset(one[:], 1.0)
        unread = keep.tile([P, 1], F32, tag="unread")
        nc.scalar.activation(out=unread[:], in_=one[:], func=ACT.Sqrt)

        w1_scale = keep.tile([P, PASSES, 4], F32, tag="w1_scale")
        w0_codes = keep.tile([P, CHUNKS, PASSES, P], U32, tag="w0_codes", align_bytes=256)
        w0_scales = keep.tile([P, CHUNKS, PASSES, P], U8, tag="w0_scales", align_bytes=256)
        w1_codes = keep.tile([P, PASSES, D], U32, tag="w1_codes", align_bytes=256)
        w1_scales = keep.tile([P, PASSES, D], U8, tag="w1_scales", align_bytes=256)

        x_in, pos_in, w0_in, w1_in = {}, {}, {}, {}
        y_rows, y_turned, y_codes, y_scales = {}, {}, {}, {}
        w0_turned, w1_rows, w1_unsorted, w1_bank, w1_turned, w1_sorted = {}, {}, {}, {}, {}, set()
        h_turned, h_codes, h_scales = {}, {}, {}
        h2, z_bank, sums, factors = {}, {}, {}, {}
        free_banks, pending, halved = list(range(BANKS)), {}, set()

        def wide(shape, dtype, name, tag="wide", bufs=WIDE):
            return work.tile(shape, dtype, tag=tag, bufs=bufs, name=name, align_bytes=64)

        def next_bank():
            number = free_banks.pop(0)
            bank = psum.tile([P, BANK], F32, tag="bank%d" % number, name="bank")
            return bank, number

        def filled(key, number, step, engine):
            pending[key] = (number, step)
            if engine:
                empty(key, engine)

        def empty(key, engine):
            number, step = pending.pop(key)
            step(engine)
            free_banks.append(number)

        def relu(engine, dst, src):
            if engine == SC:
                nc.scalar.activation(out=dst, in_=src, func=ACT.Relu)
            else:
                nc.vector.tensor_scalar(out=dst, in0=src, scalar1=0.0, scalar2=None, op0=MAX)

        def load_x(p, batches=slice(0, B)):
            if p not in x_in:
                x_in[p] = work.tile([P, B, D], BF16, tag="x_in", bufs=SINGLE_PAIRS, name="x_in")
            rows = x[:, p * P : (p + 1) * P, :].rearrange("b s k -> s b k")
            nc.sync.dma_start(out=x_in[p][:, batches], in_=rows[:, batches])

        def load_last_pairs(start):
            count = PAIRS - start
            rows = work.tile([P, B, count, D], BF16, tag="x_last", bufs=1, name="x_last")
            for b in range(B):
                nc.sync.dma_start(out=rows[:, b], in_=x[b, start * P :, :].rearrange("(j m) k -> m j k", m=P))
            table = work.tile([P, count, D], BF16, tag="pos_last", bufs=1, name="pos_last")
            nc.sync.dma_start(out=table[:], in_=pos_emb[0, start * P :, :].rearrange("(j m) k -> m j k", m=P))
            for p in range(start, PAIRS):
                x_in[p], pos_in[p] = rows[:, :, p - start], table[:, p - start]

        def load_pos(p):
            pos_in[p] = work.tile([P, D], BF16, tag="pos_in", bufs=SINGLE_PAIRS, name="pos_in")
            nc.sync.dma_start(out=pos_in[p][:], in_=pos_emb[0, p * P : (p + 1) * P, :])

        w0_rows = enc_w0.rearrange("(h m t) k -> h t m k", h=PASSES, m=P, t=4)

        def load_w0(c):
            w0_in[c] = work.tile([P, D], BF16, tag="w0_in", bufs=CHUNKS, name="w0_in")
            nc.sync.dma_start(out=w0_in[c][:], in_=w0_rows[c // 4, c % 4])

        def load_w1(q, chunks=slice(0, 2)):
            if q not in w1_in:
                w1_in[q] = work.tile([P, 2, D], U8, tag="w1_in", bufs=QUARTERS, name="w1_in")
            rows = enc_w1_bytes[2 * P * q : 2 * P * (q + 1), :].rearrange("(e m) k -> m e k", e=2)
            nc.sync.dma_start(out=w1_in[q][:, chunks], in_=rows[:, chunks])

        def load_scale():
            nc.sync.dma_start(out=w1_scale[:], in_=enc_w1_scale.rearrange("o (g p t) -> p (o g) t", p=P, t=4))

        def copy_words(engine, bank, dst):
            src = bank[:].rearrange("p (u g c i) -> p g c u i", g=PASSES, u=2, i=2)
            dst = dst.rearrange("p g (c i u) -> p g c u i", u=2, i=2)
            if engine == SC:
                nc.scalar.copy(out=dst, in_=src)
            else:
                nc.vector.tensor_copy(out=dst, in_=src)

        def transpose_words(source):
            bank, number = next_bank()
            blocks = bank[:].rearrange("p (u j n) -> p j u n", j=2, u=2)
            for j in range(2):
                for u in range(2):
                    nc.tensor.transpose(blocks[:, j, u, :], source(j, u), ident[:])
            return bank, number

        def turn_y(i, engine=None):
            p, b = divmod(i, B)
            words = y_rows[p][:, :, b].bitcast(F32)
            bank, number = transpose_words(lambda g, u: words[:, u, g * P : (g + 1) * P])
            if b == 0:
                y_turned[p] = wide([P, B, D], BF16, "y_turned", *tags.get(("y", p), ()))
            dst = y_turned[p][:, b].bitcast(F32).rearrange("p (g n) -> p g n", g=PASSES)
            filled(("y", i), number, lambda engine: copy_words(engine, bank, dst), engine)

        def turn_w0(c, engine=SC):
            q, e = divmod(c, 2)
            words = w0_in.pop(c)[:].bitcast(F32)
            bank, number = transpose_words(lambda g, u: words[:, 2 * P * g + u : 2 * P * (g + 1) : 2])
            if e == 0:
                w0_turned[q] = wide([P, 2, D], BF16, "w0_turned", *tags.get(("w0", q), ()))
            dst = w0_turned[q][:, e].bitcast(F32).rearrange("p (g n) -> p g n", g=PASSES)
            filled(("w0", c), number, lambda engine: copy_words(engine, bank, dst), engine)

        def turn_w1(q):
            for g in range(PASSES):
                w1_bank[q, g] = next_bank()
            for e in range(2):
                words = w1_rows[q][:, e].bitcast(F32)
                for g in range(PASSES):
                    blocks = w1_bank[q, g][0][:].rearrange("p (u e n) -> p e u n", e=2, u=2)
                    for u in range(2):
                        if (q, e) in w1_sorted:
                            block = words[:, (2 * u + g) * P : (2 * u + g + 1) * P]
                        else:
                            block = words[:, 2 * P * g + u : 2 * P * (g + 1) : 2]
                        nc.tensor.transpose(blocks[:, e, u, :], block, ident[:])

        def scale_w1(q, g):
            n, j = divmod(q, 2)
            if j == 0:
                w1_turned[n, g] = wide([P, 2, 2 * P, 4], BF16, "w1_turned")
            dst = w1_turned[n, g][:, j].rearrange("p r (u e) -> p r u e", u=2)
            scales = w1_scale[:, g].unsqueeze(1).to_broadcast([P, 2 * P, 4]).rearrange("p r (u e) -> p r u e", u=2)
            bank, number = w1_bank.pop((q, g))
            values = bank[:].bitcast(BF16).rearrange("p (u r e) -> p r u e", u=2, e=2)
            nc.vector.tensor_tensor(out=dst, in0=values, in1=scales, op=MULT)
            free_banks.append(number)

        def stage1(i, h, engine=None):
            p, b = divmod(i, B)
            bank, number = next_bank()
            for t in range(4):
                for g in range(PASSES):
                    nc.tensor.matmul_mx(
                        out=bank[:, t * P : (t + 1) * P],
                        lhsT=w0_codes[:, 4 * h + t, g, :].bitcast(FP8X4),
                        lhsT_scale=w0_scales[:, 4 * h + t, g, :],
                        rhs=y_codes[p][:, b, g * P : (g + 1) * P].bitcast(FP8X4),
                        rhs_scale=y_scales[p][:, b, g * P : (g + 1) * P],
                        start=(g == 0),
                        stop=(g == PASSES - 1),
                    )
            if p not in h_turned:
                h_turned[p] = wide([P, B, PASSES, P, 4], BF16, "h_turned", *tags.get(("h", p), ()))
            dst = h_turned[p][:, b, h].rearrange("p (c i) t -> p c t i", i=2)
            src = bank[:].rearrange("p (t c i) -> p c t i", t=4, i=2)
            filled(("h", i, h), number, lambda engine: relu(engine, dst, src), engine)

        def stage2_pass(i, n, g):
            p, b = divmod(i, B)
            cols = slice(n * BANK, (n + 1) * BANK)
            if g == 0:
                z_bank[i, n] = next_bank()
            nc.tensor.matmul_mx(
                out=z_bank[i, n][0][:],
                lhsT=h_codes[p][:, b, g * P : (g + 1) * P].bitcast(FP8X4),
                lhsT_scale=h_scales[p][:, b, g * P : (g + 1) * P],
                rhs=w1_codes[:, g, cols].bitcast(FP8X4),
                rhs_scale=w1_scales[:, g, cols],
                start=(g == 0),
                stop=(g == PASSES - 1),
            )

        def stage2(i, n, engine=None):
            for g in range(PASSES):
                if g or (i, n) not in z_bank:
                    stage2_pass(i, n, g)
            if i not in h2:
                h2[i] = wide([P, D], F32, "h2")
            bank, number = z_bank[i, n]
            filled(("z", i, n), number, lambda engine: relu(engine, h2[i][:, n * BANK : (n + 1) * BANK], bank[:]), engine)

        def widen_w1(q, engine, chunks=slice(0, 2), cols=slice(None)):
            if q not in w1_rows:
                w1_rows[q] = wide([P, 2, D], BF16, "w1_rows", *tags.get(("w1", q), ()))
            dst = w1_rows[q][:, chunks].rearrange("p e k -> p (e k)")[:, cols]
            src = w1_in[q][:, chunks].rearrange("p e k -> p (e k)")[:, cols].bitcast(FP8)
            if engine == SC:
                nc.scalar.copy(out=dst, in_=src)
            elif engine == V and chunks.stop - chunks.start == 2:
                nc.vector.tensor_copy(out=dst, in_=src)
            elif engine == V:
                w1_sorted.add((q, chunks.start))
                nc.vector.tensor_scalar(
                    out=dst.rearrange("p (u w i) -> p w u i", u=2, i=2),
                    in0=src.rearrange("p (w u i) -> p w u i", u=2, i=2),
                    scalar1=one[:],
                    scalar2=None,
                    op0=MULT,
                )
            else:
                nc.gpsimd.tensor_copy(out=dst, in_=src)

        def sort_w1(q, e):
            if e == 0:
                w1_unsorted[q] = w1_rows[q]
                w1_rows[q] = wide([P, 2, D], BF16, "w1_sorted")
            w1_sorted.add((q, e))
            words = w1_unsorted[q][:, e].bitcast(F32).rearrange("p (w u) -> p u w", u=2)
            nc.scalar.copy(out=w1_rows[q][:, e].bitcast(F32).rearrange("p (u w) -> p u w", u=2), in_=words)

        def add_pos(p, batches=slice(0, B), engine=V, part=slice(0, WORDS)):
            if p not in y_rows:
                y_rows[p] = wide([P, 2, B, D // 2], BF16, "y_rows", *tags.get(("yr", p), ()))
            words = "p b (w u e) -> p b w u e"
            count = batches.stop - batches.start
            (nc.vector if engine == V else nc.gpsimd).tensor_tensor(
                out=y_rows[p][:, :, batches].rearrange("p u b (w e) -> p b w u e", e=2)[:, :, part],
                in0=x_in[p][:, batches].rearrange(words, u=2, e=2)[:, :, part],
                in1=pos_in[p][:].unsqueeze(1).to_broadcast([P, count, D]).rearrange(words, u=2, e=2)[:, :, part],
                op=ADD,
            )

        def quantise(values, codes, scales):
            nc.vector.quantize_mx(out=codes.bitcast(FP8X4), scales=scales, in_=values)

        def quantise_pair(p, batches, values, codes, scales, tag):
            if p not in codes:
                codes[p] = work.tile([P, B, WORDS], U32, tag=tag + "_codes", name="codes", align_bytes=256, bufs=PAIRS)
                scales[p] = work.tile([P, B, WORDS], U8, tag=tag + "_scales", name="scales", align_bytes=256, bufs=PAIRS)
            flat = "p b n -> p (b n)"
            quantise(values[:, batches].rearrange(flat), codes[p][:, batches].rearrange(flat), scales[p][:, batches].rearrange(flat))

        def quantise_y(p, batches=slice(0, B)):
            quantise_pair(p, batches, y_turned[p][:], y_codes, y_scales, "y")

        def quantise_h(p, batches=slice(0, B)):
            quantise_pair(p, batches, h_turned[p][:].rearrange("p b h n t -> p b (h n t)"), h_codes, h_scales, "h")

        def quantise_half(i, h):
            p, b = divmod(i, B)
            words = slice(h * P, (h + 1) * P)
            values = h_turned[p][:, b, h].rearrange("p n t -> p (n t)")
            quantise(values, h_codes[p][:, b, words], h_scales[p][:, b, words])

        def quantise_w0(q):
            flat = "p c g m -> p (c g m)"
            chunks = slice(2 * q, 2 * q + 2)
            values = w0_turned.pop(q)[:].rearrange("p c n -> p (c n)")
            quantise(values, w0_codes[:, chunks].rearrange(flat), w0_scales[:, chunks].rearrange(flat))

        def quantise_w1(n, g):
            cols = slice(n * BANK, (n + 1) * BANK)
            values = w1_turned.pop((n, g))[:].rearrange("p j r t -> p (j r t)")
            quantise(values, w1_codes[:, g, cols], w1_scales[:, g, cols])

        def squares(i, engine, half=None):
            group, n = PLACE[i]
            if group not in sums:
                sums[group] = work.tile([P, 4], F32, tag="sums", name="sums", bufs=len(GROUPS))
            cols = slice(0, D) if half is None else slice(half * BANK, (half + 1) * BANK)
            slot = n if half is None else n + 2 * half
            if half is not None:
                halved.add(group)
            total = sums[group][:, slot : slot + 1]
            values = h2[i][:, cols]
            if engine == SC:
                squared = work.tile([P, D], BF16, tag="squared_s", name="squared", bufs=2)
                nc.scalar.activation(out=squared[:, cols], in_=values, func=ACT.Square, accum_out=total)
            else:
                squared = work.tile([P, D], BF16, tag="squared_v", name="squared", bufs=1)
                nc.vector.scalar_tensor_tensor(
                    out=squared[:, cols], in0=z_bank[i, half][0][:], scalar=0.0, in1=values, op0=MAX, op1=MULT, accum_out=total
                )

        def root(group):
            count = len(GROUPS[group])
            factors[group] = work.tile([P, count], F32, tag="factors", name="factors", bufs=len(GROUPS))
            if group not in halved:
                nc.scalar.activation(out=factors[group][:], in_=sums[group][:, 0:count], func=ACT.Sqrt)
                return
            for n in reversed(range(count)):
                total = sums[group]
                nc.scalar.activation(
                    out=factors[group][:, n : n + 1], in_=total[:, n : n + 1], func=ACT.Sqrt, bias=total[:, n + 2 : n + 3]
                )

        def add_eps(group, engine=SC):
            if engine == SC:
                nc.scalar.activation(out=factors[group][:], in_=factors[group][:], func=ACT.Copy, bias=EPS)
            else:
                nc.vector.tensor_scalar(out=factors[group][:], in0=factors[group][:], scalar1=EPS, scalar2=None, op0=ADD)

        def reciprocal(group, cols=slice(0, B)):
            nc.vector.reciprocal(out=factors[group][:, cols], in_=factors[group][:, cols])

        def scale_and_store(i, engine, cols=slice(0, D)):
            group, n = PLACE[i]
            values, factor = h2[i][:, cols], factors[group][:, n : n + 1]
            if engine == V:
                nc.vector.tensor_scalar(out=values, in0=values, scalar1=factor, scalar2=None, op0=MULT)
            elif engine == SC:
                nc.scalar.activation(out=values, in_=values, func=ACT.Copy, scale=factor)
            else:
                nc.gpsimd.tensor_scalar(out=values, in0=values, scalar1=factor, scalar2=0.0, op0=MULT, op1=ADD)
            p, b = divmod(i, B)
            nc.sync.dma_start(out=out[b, p * P : (p + 1) * P, cols], in_=values)

        first, second = slice(0, 1), slice(1, 2)
        low, high = slice(0, BANK), slice(BANK, D)

        def release(group):
            reciprocal(group, slice(0, len(GROUPS[group])))
            for i in GROUPS[group]:
                scale_and_store(i, G)

        def release_behind(group, last):
            reciprocal(group, slice(0, len(GROUPS[group])))
            last()
            for i in GROUPS[group]:
                scale_and_store(i, G)

        def quantise_tile(i):
            p, b = divmod(i, B)
            quantise_h(p, slice(b, b + 1))


        tags = {("y", 2): ("held_a", 1), ("yr", 4): ("held_a", 1), ("h", 0): ("held_b", 1), ("w1", 3): ("held_b", 1)}
        load_w1(0, first)
        load_w1(0, second)
        load_scale()
        load_w1(1)
        load_w0(0)
        load_x(0, first)
        load_pos(0)
        load_w1(2)
        for c in range(1, 4):
            load_w0(c)
        load_x(0, second)
        for c in range(4, CHUNKS):
            load_w0(c)
        load_x(1, first)
        load_pos(1)
        load_x(1, second)
        load_x(2)
        load_pos(2)
        load_w1(3)
        for p in range(3, PAIRS):
            load_x(p)
            load_pos(p)

        widen_w1(0, V, first)
        widen_w1(0, V, second)
        widen_w1(1, V, first)
        widen_w1(1, SC, second)
        turn_w1(0)
        turn_w0(0)
        turn_w1(1)
        scale_w1(0, 0)
        add_pos(0, first)
        widen_w1(2, G, cols=slice(0, 3 * BANK))
        widen_w1(2, SC, cols=slice(3 * BANK, 4 * BANK))
        scale_w1(0, 1)
        scale_w1(1, 0)
        turn_y(0, SC)
        turn_w0(1)
        turn_w0(2)
        turn_w0(3)
        quantise_w0(0)
        add_pos(0, second)
        quantise_y(0, first)
        quantise_w0(1)
        turn_w1(2)
        turn_w0(4)
        turn_y(1, SC)
        scale_w1(1, 1)
        turn_w0(5)
        turn_w0(6)
        turn_w0(7)
        stage1(0, 0, SC)
        quantise_y(0, second)
        add_pos(1, first)
        quantise_w0(2)
        add_pos(1, second)
        quantise_w0(3)
        stage1(1, 0, SC)
        turn_y(2, SC)
        turn_y(3, SC)
        add_pos(2)
        quantise_w1(0, 0)
        stage1(0, 1, SC)
        stage1(1, 1, SC)
        quantise_y(1)
        quantise_w1(0, 1)
        quantise_h(0)
        widen_w1(3, G, cols=slice(0, 7 * WORDS))
        turn_y(4, SC)
        turn_y(5, SC)
        scale_w1(2, 0)
        stage1(2, 0, SC)
        stage1(2, 1, SC)
        scale_w1(2, 1)
        stage1(3, 0, SC)
        stage1(3, 1, SC)
        widen_w1(3, V, cols=slice(7 * WORDS, 8 * WORDS))
        add_pos(3)
        quantise_y(2)
        stage2(0, 0, SC)
        stage2(1, 0, SC)
        quantise_h(1)
        squares(0, SC, 0)
        squares(1, SC, 0)
        turn_w1(3)
        turn_y(6, SC)
        turn_y(7, SC)
        scale_w1(3, 0)
        add_pos(4, first, G, slice(0, 224))
        stage1(4, 0, SC)
        stage1(4, 1, SC)
        scale_w1(3, 1)
        stage1(5, 0, SC)
        stage1(5, 1, SC)

        quantise_y(3)
        quantise_w1(1, 0)
        quantise_w1(1, 1)
        add_pos(4, first, V, slice(224, 256))
        add_pos(4, second)
        add_pos(5)
        quantise_h(2)

        add_pos(6)
        add_pos(7)
        stage2(2, 0, SC)
        stage2(3, 0, SC)
        stage1(6, 0, SC)
        stage1(6, 1, SC)
        stage2(0, 1, SC)
        stage2(1, 1, SC)
        squares(0, SC, 1)
        squares(1, SC, 1)

        turn_y(8, SC)
        root(0)
        turn_y(9, SC)
        add_eps(0)
        turn_y(10, V)
        release_behind(0, lambda: quantise_y(4))
        turn_y(11, V)
        stage1(7, 0, V)
        stage1(7, 1)
        stage2(2, 1, SC)
        stage2(3, 1, SC)
        empty(("h", 7, 1), V)
        squares(2, SC)
        squares(3, SC)
        stage2(4, 0, V)
        stage2(4, 1, V)
        quantise_h(3)
        stage2(5, 0, SC)
        root(1)
        stage2(5, 1, SC)
        add_eps(1)
        stage1(8, 0, V)
        release_behind(1, lambda: quantise_y(5))
        squares(4, SC)
        squares(5, SC)
        stage1(8, 1, V)
        stage1(9, 0, V)
        stage1(9, 1, V)
        turn_y(12, V)
        turn_y(13, V)
        turn_y(14, SC)
        root(2)
        turn_y(15)
        stage2(6, 0, SC)
        add_eps(2)
        release_behind(2, lambda: quantise_h(4))
        stage2(6, 1, SC)
        empty(("y", 15), SC)
        stage2(7, 0, V)
        stage2(7, 1, V)
        squares(6, SC)
        squares(7, SC)
        stage1(10, 0, V)
        stage1(10, 1, V)
        stage1(11, 0, V)
        stage1(11, 1, SC)
        root(3)
        quantise_y(6)
        quantise_y(7)
        quantise_h(5)
        stage2(8, 0, SC)
        add_eps(3)
        release(3)
        stage2(8, 1, SC)
        stage2(9, 0, SC)
        stage2(9, 1, V)
        squares(8, SC)
        stage1(12, 0, V)
        stage1(12, 1, V)
        squares(9, SC, 0)
        root(4)
        squares(9, SC, 1)
        add_eps(4)
        stage2(10, 0, V)
        stage2(10, 1, V)
        release_behind(4, lambda: quantise_tile(12))
        stage1(13, 0, SC)
        root(5)
        squares(10, SC, 0)
        add_eps(5)
        stage1(13, 1, V)
        squares(10, SC, 1)
        stage2(11, 0, V)
        release_behind(5, lambda: quantise_tile(13))
        stage2(11, 1, V)
        squares(11, SC, 0)
        root(6)
        add_eps(6)
        squares(11, SC, 1)

        stage2(12, 0, V)
        release(6)
        stage2(12, 1, SC)
        root(7)
        squares(12, SC, 0)
        add_eps(7)
        squares(12, SC, 1)
        stage1(14, 0, V)
        stage1(14, 1, V)
        stage2(13, 0, V)
        release_behind(7, lambda: quantise_tile(14))
        stage2(13, 1, SC)
        root(8)
        squares(13, SC, 0)
        add_eps(8)
        squares(13, SC, 1)
        stage1(15, 0, V)
        stage1(15, 1, V)
        reciprocal(8, first)
        quantise_half(15, 0)
        quantise_half(15, 1)
        scale_and_store(12, V)
        root(9)
        stage2(14, 0, SC)
        add_eps(9)
        stage2(14, 1, V)
        release(9)
        squares(14, SC, 0)
        stage2_pass(15, 0, 0)
        stage2_pass(15, 1, 0)
        squares(14, SC, 1)
        stage2(15, 0, V)
        stage2(15, 1, V)
        root(10)
        squares(15, SC, 0)
        add_eps(10, V)
        squares(15, SC, 1)
        reciprocal(10, first)
        root(11)
        scale_and_store(14, V)
        add_eps(11)
        reciprocal(11, first)
        scale_and_store(15, V, high)
        scale_and_store(15, V, low)
